import numpy as np
import ml_dtypes


def mxq(x, axis, fmt="e4m3"):
    dtype, down = {"e4m3": (ml_dtypes.float8_e4m3fn, 7), "e5m2": (ml_dtypes.float8_e5m2, 14)}[fmt]
    v = np.moveaxis(np.asarray(x, np.float32).astype(ml_dtypes.bfloat16).astype(np.float64), axis, -1)
    blocks = v.reshape(v.shape[:-1] + (-1, 32))
    amax = np.abs(blocks).max(-1, keepdims=True)
    byte = np.maximum(np.where(amax > 0, np.frexp(amax)[1] - 1 + 127, 0) - down, 1)
    scale = np.exp2(byte - 127.0)
    codes = (blocks / scale).astype(np.float32).astype(dtype).astype(np.float64)
    return np.moveaxis((codes * scale).reshape(v.shape), -1, axis)


WIDE = False


def mx_kscale(k):
    if not WIDE:
        return np.ones(k)
    levels = np.array([10, -10, 5, -5, 0])
    a = np.random.permutation(np.resize(levels, k // 512 * 4)).reshape(k // 512, 4)
    idx = np.arange(k)
    return np.exp2(a[idx // 512, idx % 128 // 32])


BF16 = ml_dtypes.bfloat16


def bf(x):
    return np.asarray(x, np.float32).astype(BF16)


def f64(x):
    return np.asarray(x).astype(np.float64)


E2M1 = np.array([0.0, 0.5, 1.0, 1.5, 2.0, 3.0, 4.0, 6.0, -0.0, -0.5, -1.0, -1.5, -2.0, -3.0, -4.0, -6.0])


def pack_weight(w, fmt):
    k, n = w.shape
    w = f64(bf(w)).reshape(k // 32, 32, n)
    amax = np.abs(w).max(1)
    if fmt == "e4m3":
        byte = np.frexp(amax)[1] - 1 + 127 - 7
    else:
        mant, ex = np.frexp(amax / 6.0)
        byte = np.where(mant > 0.5, ex, ex - 1) + 127
    byte = np.clip(np.where(amax > 0, byte, 1), 1, 254)
    scaled = (w * np.exp2(127.0 - byte)[:, None, :]).reshape(k, n).astype(np.float32)
    by_word = np.ascontiguousarray(scaled.reshape(k // 512, 128, 4, n).transpose(0, 1, 3, 2))
    if fmt == "e4m3":
        words = by_word.astype(ml_dtypes.float8_e4m3fn).view(np.uint8)
    else:
        c = by_word.astype(ml_dtypes.float4_e2m1fn).view(np.uint8) & 0xF
        words = c[..., 0::2] | (c[..., 1::2] << 4)
    return np.ascontiguousarray(words), np.ascontiguousarray(byte.astype(np.uint8).reshape(k // 512, 16, n))


def unpack_weight(words, scales, fmt):
    g, p, n, _ = words.shape
    if fmt == "e4m3":
        vals = np.ascontiguousarray(words).view(ml_dtypes.float8_e4m3fn).astype(np.float64)
    else:
        nib = np.empty((g, p, n, 4), np.uint8)
        nib[..., 0::2] = words & 0xF
        nib[..., 1::2] = words >> 4
        vals = E2M1[nib]
    vals = vals * np.repeat(np.exp2(scales.astype(np.float64) - 127.0), 8, axis=1)[..., None]
    return vals.transpose(0, 1, 3, 2).reshape(g * 512, n)

def pack4(w):
    words, scales = pack_weight(w, "e2m1")
    return words.reshape(words.shape[0], 128, -1), scales


def unpack4(words, scales):
    return unpack_weight(words.reshape(words.shape[0], 128, -1, 2), scales, "e2m1")


B, S, HID, NH, HD, RD, RATIO = 4, 4096, 512, 8, 64, 32, 4
THETA = 10000.0
NW = S // RATIO
HALF = RD // 2


def rope_tables(positions):
    inv_freq = 1.0 / THETA ** (np.arange(HALF) / HALF)
    ang = positions[:, None] * inv_freq[None, :]
    return np.cos(ang), np.sin(ang)


def rope_interleaved(x, cos, sin):
    nope, rope = x[..., :-RD], x[..., -RD:]
    pr = rope.reshape(rope.shape[:-1] + (HALF, 2))
    a, b = pr[..., 0], pr[..., 1]
    new = np.stack([a * cos - b * sin, a * sin + b * cos], axis=-1).reshape(rope.shape)
    return np.concatenate([nope, new], axis=-1)


def remap(t, fill):
    cur = t[..., HD:]
    prev = np.concatenate([np.full((B, 1, RATIO, HD), fill), t[:, :-1, :, :HD]], axis=1)
    return np.concatenate([prev, cur], axis=2)


def pool_overlap(kv, gate, ape):
    kv_o = remap(kv.reshape(B, NW, RATIO, 2 * HD), 0.0)
    gate_o = remap(gate.reshape(B, NW, RATIO, 2 * HD) + ape, -np.inf)
    e = np.exp(gate_o - gate_o.max(axis=2, keepdims=True))
    w = e / e.sum(axis=2, keepdims=True)
    return (kv_o * w).sum(axis=2)


def setup_inputs():
    s = mx_kscale(HID)
    hidden = bf(np.random.standard_normal((B, S, HID)) * s)
    wkv_words, wkv_scales = pack4(np.random.standard_normal((HID, 2 * HD)) * 2.0 / np.sqrt(HID) / s[:, None])
    wgate_words, wgate_scales = pack4(np.random.standard_normal((HID, 2 * HD)) / np.sqrt(HID) / s[:, None])
    ape = bf(np.random.standard_normal((RATIO, 2 * HD)) * 0.5)
    return {"hidden": hidden,
            "wkv_words": wkv_words, "wkv_scales": wkv_scales,
            "wgate_words": wgate_words, "wgate_scales": wgate_scales,
            "ape": ape}


def reference(hidden, wkv_words, wkv_scales, wgate_words, wgate_scales, ape):
    hq = mxq(f64(hidden), 2, "e4m3")
    kv = hq @ unpack4(wkv_words, wkv_scales)
    gate = hq @ unpack4(wgate_words, wgate_scales)
    pooled = pool_overlap(kv, gate, f64(ape))
    ck, sk = rope_tables(np.arange(NW) * RATIO)
    k_rot = rope_interleaved(pooled, ck, sk)
    return k_rot, pooled

@@ -1,0 +1,273 @@
+import math
+from contextlib import ExitStack
+
+import concourse.masks as masks
+import concourse.mybir as mybir
+
+F32 = mybir.dt.float32
+BF16 = mybir.dt.bfloat16
+I32 = mybir.dt.int32
+U32 = mybir.dt.uint32
+U8 = mybir.dt.uint8
+FP8X4 = mybir.dt.float8_e4m3fn_x4
+FP4X4 = mybir.dt.float4_e2m1fn_x4
+ALU = mybir.AluOpType
+ACT = mybir.ActivationFunctionType
+AXIS = mybir.AxisListType
+
+P = 128
+BATCH, SEQ, HID = 4, 4096, 512
+RATIO = 4
+FEAT = 64
+COLS = 2 * FEAT
+ROPE = 32
+PAIRS = ROPE // 2
+THETA = 10000.0
+
+RUN_TOKENS = BATCH * SEQ // P
+RUN_WINDOWS = RUN_TOKENS // RATIO
+RUNS_PER_SEQ = SEQ // RUN_TOKENS
+WORDS = HID // 2
+CHUNK_WINDOWS = 2
+CHUNK_TOKENS = CHUNK_WINDOWS * RATIO
+N_CHUNKS = 1 + RUN_WINDOWS // CHUNK_WINDOWS
+BATCH_TARGETS = 8
+NO_SLOT = -1.0e30
+ROUND = 1.5 * 2.0**23
+
+FLOPS = 2 * BATCH * SEQ * HID * 2 * COLS
+
+
+def tile_deepseekv4attention_pa_t_kernel(
+    tc, hidden, wkv_words, wkv_scales, wgate_words, wgate_scales, ape, out_0, out_1
+):
+    nc = tc.nc
+    x_runs = hidden.rearrange("b (q j) k -> (b q) j k", j=RUN_TOKENS)
+    krot_runs = out_0.rearrange("b (q u) f -> (b q) u f", u=RUN_WINDOWS)
+    pooled_runs = out_1.rearrange("b (q u) f -> (b q) u f", u=RUN_WINDOWS)
+
+    with ExitStack() as ctx:
+        const = ctx.enter_context(tc.tile_pool(name="const", bufs=1))
+        x_pool = ctx.enter_context(tc.tile_pool(name="x", bufs=4))
+        q_pool = ctx.enter_context(tc.tile_pool(name="quant", bufs=2))
+        g_pool = ctx.enter_context(tc.tile_pool(name="gates", bufs=4))
+        e_pool = ctx.enter_context(tc.tile_pool(name="weighted", bufs=3))
+        m_pool = ctx.enter_context(tc.tile_pool(name="maxima", bufs=3))
+        o_pool = ctx.enter_context(tc.tile_pool(name="outs", bufs=2))
+        psum_t = ctx.enter_context(tc.psum_pool(name="psum_t", bufs=2))
+        psum_g = ctx.enter_context(tc.psum_pool(name="psum_g", bufs=2))
+        psum_k = ctx.enter_context(tc.psum_pool(name="psum_k", bufs=4))
+
+        raw_words = const.tile([P, 2, 2 * COLS], U8, align_bytes=64)
+        raw_plane = const.tile([P, 2, COLS], U8, align_bytes=64)
+        w_words = const.tile([P, 2, 2 * COLS], U8, align_bytes=64)
+        w_plane = const.tile([P, 2, COLS], U8, align_bytes=64)
+        nc.vector.memset(raw_plane[:].rearrange("p w c -> p (w c)").bitcast(I32), 0)
+        for i, (words, scales) in enumerate(((wgate_words, wgate_scales), (wkv_words, wkv_scales))):
+            nc.sync.dma_start(out=raw_words[:, i, :].bitcast(I32), in_=words[0].bitcast(I32))
+            for quad in range(4):
+                nc.sync.dma_start(
+                    out=raw_plane[32 * quad : 32 * quad + 4, i, :].bitcast(I32),
+                    in_=scales[0, 4 * quad : 4 * quad + 4, :].bitcast(I32),
+                )
+        nc.vector.tensor_copy(out=w_words[:, :, 0:COLS].bitcast(I32), in_=raw_words[:, :, COLS : 2 * COLS].bitcast(I32))
+        nc.vector.tensor_copy(out=w_words[:, :, COLS : 2 * COLS].bitcast(I32), in_=raw_words[:, :, 0:COLS].bitcast(I32))
+        nc.vector.tensor_copy(out=w_plane[:, :, 0:FEAT].bitcast(I32), in_=raw_plane[:, :, FEAT:COLS].bitcast(I32))
+        nc.vector.tensor_copy(out=w_plane[:, :, FEAT:COLS].bitcast(I32), in_=raw_plane[:, :, 0:FEAT].bitcast(I32))
+
+        ape_rows = const.tile([P, RATIO, COLS], BF16)
+        nc.sync.dma_start(
+            out=ape_rows[:].rearrange("p r c -> p (r c)"),
+            in_=ape.rearrange("r c -> (r c)").partition_broadcast(P),
+        )
+        ape_f = const.tile([P, RATIO, COLS], F32)
+        nc.vector.tensor_copy(out=ape_f[:, :, 0:FEAT], in_=ape_rows[:, :, FEAT:COLS])
+        nc.vector.tensor_copy(out=ape_f[:, :, FEAT:COLS], in_=ape_rows[:, :, 0:FEAT])
+        start_bias = const.tile([P, 1], F32)
+        nc.vector.memset(start_bias[:], 0.0)
+        for b in range(BATCH):
+            nc.vector.memset(start_bias[RUNS_PER_SEQ * b : RUNS_PER_SEQ * b + 1, :], NO_SLOT)
+        ape_before = const.tile([P, RATIO, COLS], F32)
+        nc.vector.tensor_scalar(out=ape_before[:], in0=ape_f[:], scalar1=start_bias[:, 0:1], scalar2=None, op0=ALU.add)
+
+        ident = const.tile([P, P], F32)
+        masks.make_identity(nc, ident[:])
+        from_left = const.tile([P, P], F32)
+        nc.vector.tensor_copy(out=from_left[:, 1:P], in_=ident[:, 0 : P - 1])
+        nc.vector.tensor_copy(out=from_left[:, 0:1], in_=ident[:, P - 1 : P])
+
+        win_i = const.tile([P, RUN_WINDOWS], I32)
+        nc.gpsimd.iota(win_i[:], pattern=[[1, RUN_WINDOWS]], base=0, channel_multiplier=0)
+        part_i = const.tile([P, 1], I32)
+        nc.gpsimd.iota(part_i[:], pattern=[[0, 1]], base=0, channel_multiplier=1)
+        run_i = const.tile([P, 1], I32)
+        nc.vector.tensor_single_scalar(out=run_i[:], in_=part_i[:], scalar=RUNS_PER_SEQ - 1, op=ALU.bitwise_and)
+        win_f = const.tile([P, RUN_WINDOWS], F32)
+        nc.vector.tensor_copy(out=win_f[:], in_=win_i[:])
+        run_f = const.tile([P, 1], F32)
+        nc.vector.tensor_copy(out=run_f[:], in_=run_i[:])
+        run_turns = const.tile([P, PAIRS], F32)
+        turns = const.tile([P, 2, RUN_WINDOWS, PAIRS], F32)
+        for j in range(PAIRS):
+            per_window = RATIO * THETA ** (-j / PAIRS) / (2.0 * math.pi)
+            per_run = RUN_WINDOWS * per_window
+            per_run = per_run - round(per_run)
+            nc.vector.tensor_scalar(
+                out=run_turns[:, j : j + 1], in0=run_f[:], scalar1=per_run, scalar2=None, op0=ALU.mult
+            )
+            nc.vector.tensor_scalar(
+                out=turns[:, 0, :, j], in0=win_f[:], scalar1=per_window, scalar2=run_turns[:, j : j + 1],
+                op0=ALU.mult, op1=ALU.add,
+            )
+        nc.vector.tensor_scalar(out=turns[:, 1], in0=turns[:, 0], scalar1=0.25, scalar2=None, op0=ALU.add)
+        whole = const.tile([P, 2, RUN_WINDOWS, PAIRS], F32)
+        nc.vector.tensor_scalar(
+            out=whole[:], in0=turns[:], scalar1=ROUND, scalar2=ROUND, op0=ALU.add, op1=ALU.subtract
+        )
+        nc.vector.tensor_tensor(out=turns[:], in0=turns[:], in1=whole[:], op=ALU.subtract)
+        sin_cos = const.tile([P, 2, RUN_WINDOWS, PAIRS], F32)
+        nc.scalar.activation(out=sin_cos[:], in_=turns[:], func=ACT.Sin, scale=2.0 * math.pi)
+        neg_sin = const.tile([P, RUN_WINDOWS, PAIRS], F32)
+        nc.scalar.activation(out=neg_sin[:], in_=turns[:, 0], func=ACT.Sin, scale=-2.0 * math.pi)
+
+        top = const.tile([P, RUN_WINDOWS + 3, COLS], F32)
+        den_half = const.tile([P, RUN_WINDOWS + 3, COLS], F32)
+        num_half = const.tile([P, RUN_WINDOWS + 3, COLS], F32)
+        nc.vector.memset(top[:, 0, :], NO_SLOT)
+        nc.vector.memset(top[:, RUN_WINDOWS + 2, :], NO_SLOT)
+
+        def windows_of(chunk):
+            if chunk == 0:
+                return [-1]
+            return [CHUNK_WINDOWS * (chunk - 1) + i for i in range(CHUNK_WINDOWS)]
+
+        kv_banks = {}
+        gate_tiles = {}
+
+        def project(chunk):
+            windows = windows_of(chunk)
+            n_win = len(windows)
+            n_tok = RATIO * n_win
+            first_token = RUN_TOKENS - RATIO if chunk == 0 else RATIO * windows[0]
+            x_sb = x_pool.tile([P, CHUNK_TOKENS, HID], BF16)
+            nc.sync.dma_start(out=x_sb[:, 0:n_tok, :], in_=x_runs[:, first_token : first_token + n_tok, :])
+            x_words = x_sb[:].rearrange("p j k -> p (j k)").bitcast(F32)
+            order = from_left if chunk == 0 else ident
+            grouped = q_pool.tile([P, CHUNK_TOKENS * P * 4], BF16, align_bytes=64)
+            grouped_words = grouped[:].bitcast(F32)
+            for pair in range(n_tok // 2):
+                flipped = psum_t.tile([P, 2, 2, P], F32)
+                for t in range(2):
+                    base = (2 * pair + t) * WORDS
+                    for h in range(2):
+                        nc.tensor.transpose(flipped[:, t, h, :], x_words[:, base + h : base + WORDS : 2], order[:])
+                nc.scalar.copy(
+                    out=grouped_words[:, pair * 4 * P : (pair + 1) * 4 * P].rearrange(
+                        "p (t n h) -> p t n h", t=2, h=2
+                    ),
+                    in_=flipped[:].rearrange("p t h n -> p t n h"),
+                )
+            codes = q_pool.tile([P, CHUNK_TOKENS * P], U32, align_bytes=64)
+            plane = q_pool.tile([P, CHUNK_TOKENS * P], U8, align_bytes=64)
+            nc.vector.quantize_mx(
+                out=codes[:, 0 : n_tok * P].bitcast(FP8X4),
+                scales=plane[:, 0 : n_tok * P],
+                in_=grouped[:, 0 : n_tok * P * 4],
+            )
+            offset = ape_before if chunk == 0 else ape_f
+            gates = g_pool.tile([P, CHUNK_WINDOWS, RATIO, COLS], F32)
+            for i, window in enumerate(windows):
+                gate_ps = psum_g.tile([P, RATIO, COLS], F32)
+                kv_ps = psum_k.tile([P, RATIO, COLS], F32)
+                for which, bank in ((0, gate_ps), (1, kv_ps)):
+                    for r in range(RATIO):
+                        cols = slice((RATIO * i + r) * P, (RATIO * i + r + 1) * P)
+                        nc.tensor.matmul_mx(
+                            out=bank[:, r, :],
+                            lhsT=codes[:, cols].bitcast(FP8X4),
+                            lhsT_scale=plane[:, cols],
+                            rhs=w_words[:, which, :].bitcast(FP4X4),
+                            rhs_scale=w_plane[:, which, :],
+                            start=True,
+                            stop=True,
+                        )
+                kv_banks[window] = kv_ps
+                nc.vector.tensor_tensor(out=gates[:, i], in0=gate_ps[:], in1=offset[:], op=ALU.add)
+            nc.vector.tensor_reduce(
+                out=top[:, windows[0] + 2 : windows[0] + 2 + n_win, :],
+                in_=gates[:, 0:n_win].rearrange("p w r c -> p w c r"),
+                axis=AXIS.X, op=ALU.max,
+            )
+            gate_tiles[chunk] = gates
+
+        def weigh(chunk):
+            windows = windows_of(chunk)
+            n_win = len(windows)
+            w_a = windows[0]
+            gates = gate_tiles[chunk]
+            peak = m_pool.tile([P, CHUNK_WINDOWS + 1, FEAT], F32)
+            nc.vector.tensor_tensor(
+                out=peak[:, 0 : n_win + 1, :],
+                in0=top[:, w_a + 2 : w_a + n_win + 3, 0:FEAT],
+                in1=top[:, w_a + 1 : w_a + n_win + 2, FEAT:COLS],
+                op=ALU.max,
+            )
+            peak_flat = peak[:].rearrange("p t f -> p (t f)")
+            for i in range(n_win):
+                nc.gpsimd.tensor_tensor(
+                    out=gates[:, i], in0=gates[:, i],
+                    in1=peak_flat[:, i * FEAT : i * FEAT + COLS].unsqueeze(1).to_broadcast([P, RATIO, COLS]),
+                    op=ALU.subtract,
+                )
+            nc.scalar.activation(out=gates[:, 0:n_win], in_=gates[:, 0:n_win], func=ACT.Exp)
+            weighted = e_pool.tile([P, CHUNK_WINDOWS, RATIO, COLS], F32)
+            for i, window in enumerate(windows):
+                nc.vector.tensor_tensor(out=weighted[:, i], in0=kv_banks[window][:], in1=gates[:, i], op=ALU.mult)
+            two = e_pool.tile([P, CHUNK_WINDOWS, 2, COLS], F32)
+            nc.gpsimd.tensor_tensor(out=two[:, 0:n_win], in0=gates[:, 0:n_win, 0:2, :], in1=gates[:, 0:n_win, 2:4, :], op=ALU.add)
+            nc.gpsimd.tensor_tensor(
+                out=den_half[:, w_a + 2 : w_a + 2 + n_win, :], in0=two[:, 0:n_win, 0, :], in1=two[:, 0:n_win, 1, :], op=ALU.add
+            )
+            nc.vector.tensor_reduce(
+                out=num_half[:, w_a + 2 : w_a + 2 + n_win, :],
+                in_=weighted[:, 0:n_win].rearrange("p w r c -> p w c r"),
+                axis=AXIS.X, op=ALU.add,
+            )
+
+        def finish(w0):
+            w1 = w0 + BATCH_TARGETS
+            den = o_pool.tile([P, BATCH_TARGETS, FEAT], F32)
+            num = o_pool.tile([P, BATCH_TARGETS, FEAT], F32)
+            nc.gpsimd.tensor_tensor(
+                out=den[:], in0=den_half[:, w0 + 2 : w1 + 2, 0:FEAT], in1=den_half[:, w0 + 1 : w1 + 1, FEAT:COLS], op=ALU.add
+            )
+            nc.vector.tensor_tensor(
+                out=num[:], in0=num_half[:, w0 + 2 : w1 + 2, 0:FEAT], in1=num_half[:, w0 + 1 : w1 + 1, FEAT:COLS], op=ALU.add
+            )
+            nc.scalar.activation(out=den[:], in_=den[:], func=ACT.Ln)
+            nc.scalar.activation(out=den[:], in_=den[:], func=ACT.Exp, scale=-1.0)
+            pooled = o_pool.tile([P, BATCH_TARGETS, FEAT], F32)
+            nc.vector.tensor_tensor(out=pooled[:], in0=num[:], in1=den[:], op=ALU.mult)
+            nc.sync.dma_start(out=pooled_runs[:, w0:w1, :], in_=pooled[:])
+
+            k_rot = o_pool.tile([P, BATCH_TARGETS, FEAT], F32)
+            cross = o_pool.tile([P, BATCH_TARGETS, PAIRS, 2], F32)
+            plain = FEAT - ROPE
+            pairs_in = pooled[:, :, plain:FEAT].rearrange("p w (j e) -> p w j e", e=2)
+            pairs_out = k_rot[:, :, plain:FEAT].rearrange("p w (j e) -> p w j e", e=2)
+            cos = sin_cos[:, 1, w0:w1, :].unsqueeze(3).to_broadcast([P, BATCH_TARGETS, PAIRS, 2])
+            nc.scalar.copy(out=k_rot[:, :, 0:plain], in_=pooled[:, :, 0:plain])
+            nc.gpsimd.tensor_tensor(out=pairs_out, in0=pairs_in, in1=cos, op=ALU.mult)
+            nc.gpsimd.tensor_tensor(out=cross[:, :, :, 0], in0=pairs_in[:, :, :, 1], in1=neg_sin[:, w0:w1, :], op=ALU.mult)
+            nc.gpsimd.tensor_tensor(out=cross[:, :, :, 1], in0=pairs_in[:, :, :, 0], in1=sin_cos[:, 0, w0:w1, :], op=ALU.mult)
+            nc.gpsimd.tensor_tensor(out=pairs_out, in0=pairs_out, in1=cross[:], op=ALU.add)
+            nc.sync.dma_start(out=krot_runs[:, w0:w1, :], in_=k_rot[:])
+
+        for step in range(N_CHUNKS + 1):
+            if step < N_CHUNKS:
+                project(step)
+            if step >= 1:
+                weigh(step - 1)
+                last_window = windows_of(step - 1)[-1]
+                if (last_window + 1) % BATCH_TARGETS == 0 and last_window > 0:
+                    finish(last_window + 1 - BATCH_TARGETS)

@@ -32,6 +32,7 @@ CHUNK_WINDOWS = 2
 CHUNK_TOKENS = CHUNK_WINDOWS * RATIO
 N_CHUNKS = 1 + RUN_WINDOWS // CHUNK_WINDOWS
 BATCH_TARGETS = 8
+LOADS_AHEAD = 3
 NO_SLOT = -1.0e30
 ROUND = 1.5 * 2.0**23
 
@@ -49,20 +50,39 @@ def tile_deepseekv4attention_pa_t_kernel(
     with ExitStack() as ctx:
         const = ctx.enter_context(tc.tile_pool(name="const", bufs=1))
         x_pool = ctx.enter_context(tc.tile_pool(name="x", bufs=4))
-        q_pool = ctx.enter_context(tc.tile_pool(name="quant", bufs=2))
+        grouped_pool = ctx.enter_context(tc.tile_pool(name="grouped", bufs=3))
+        code_pool = ctx.enter_context(tc.tile_pool(name="codes", bufs=5))
         g_pool = ctx.enter_context(tc.tile_pool(name="gates", bufs=4))
         e_pool = ctx.enter_context(tc.tile_pool(name="weighted", bufs=3))
-        m_pool = ctx.enter_context(tc.tile_pool(name="maxima", bufs=3))
+        m_pool = ctx.enter_context(tc.tile_pool(name="maxima", bufs=2))
         o_pool = ctx.enter_context(tc.tile_pool(name="outs", bufs=2))
-        psum_t = ctx.enter_context(tc.psum_pool(name="psum_t", bufs=2))
+        psum_t = ctx.enter_context(tc.psum_pool(name="psum_t", bufs=4))
         psum_g = ctx.enter_context(tc.psum_pool(name="psum_g", bufs=2))
-        psum_k = ctx.enter_context(tc.psum_pool(name="psum_k", bufs=4))
+        psum_k = ctx.enter_context(tc.psum_pool(name="psum_k", bufs=2))
+        ctx.enter_context(tc.manual_schedule())
+
+
+        def windows_of(chunk):
+            if chunk == 0:
+                return [-1]
+            return [CHUNK_WINDOWS * (chunk - 1) + i for i in range(CHUNK_WINDOWS)]
+
+        x_tiles = {}
+
+        def load(chunk):
+            n_tok = RATIO * len(windows_of(chunk))
+            first_token = RUN_TOKENS - RATIO if chunk == 0 else RATIO * windows_of(chunk)[0]
+            x_sb = x_pool.tile([P, CHUNK_TOKENS, HID], BF16)
+            nc.sync.dma_start(out=x_sb[:, 0:n_tok, :], in_=x_runs[:, first_token : first_token + n_tok, :])
+            x_tiles[chunk] = x_sb
 
         raw_words = const.tile([P, 2, 2 * COLS], U8, align_bytes=64)
         raw_plane = const.tile([P, 2, COLS], U8, align_bytes=64)
         w_words = const.tile([P, 2, 2 * COLS], U8, align_bytes=64)
         w_plane = const.tile([P, 2, COLS], U8, align_bytes=64)
+        ape_rows = const.tile([P, RATIO, COLS], BF16)
         nc.vector.memset(raw_plane[:].rearrange("p w c -> p (w c)").bitcast(I32), 0)
+        load(0)
         for i, (words, scales) in enumerate(((wgate_words, wgate_scales), (wkv_words, wkv_scales))):
             nc.sync.dma_start(out=raw_words[:, i, :].bitcast(I32), in_=words[0].bitcast(I32))
             for quad in range(4):
@@ -70,25 +90,12 @@ def tile_deepseekv4attention_pa_t_kernel(
                     out=raw_plane[32 * quad : 32 * quad + 4, i, :].bitcast(I32),
                     in_=scales[0, 4 * quad : 4 * quad + 4, :].bitcast(I32),
                 )
-        nc.vector.tensor_copy(out=w_words[:, :, 0:COLS].bitcast(I32), in_=raw_words[:, :, COLS : 2 * COLS].bitcast(I32))
-        nc.vector.tensor_copy(out=w_words[:, :, COLS : 2 * COLS].bitcast(I32), in_=raw_words[:, :, 0:COLS].bitcast(I32))
-        nc.vector.tensor_copy(out=w_plane[:, :, 0:FEAT].bitcast(I32), in_=raw_plane[:, :, FEAT:COLS].bitcast(I32))
-        nc.vector.tensor_copy(out=w_plane[:, :, FEAT:COLS].bitcast(I32), in_=raw_plane[:, :, 0:FEAT].bitcast(I32))
-
-        ape_rows = const.tile([P, RATIO, COLS], BF16)
         nc.sync.dma_start(
             out=ape_rows[:].rearrange("p r c -> p (r c)"),
             in_=ape.rearrange("r c -> (r c)").partition_broadcast(P),
         )
-        ape_f = const.tile([P, RATIO, COLS], F32)
-        nc.vector.tensor_copy(out=ape_f[:, :, 0:FEAT], in_=ape_rows[:, :, FEAT:COLS])
-        nc.vector.tensor_copy(out=ape_f[:, :, FEAT:COLS], in_=ape_rows[:, :, 0:FEAT])
-        start_bias = const.tile([P, 1], F32)
-        nc.vector.memset(start_bias[:], 0.0)
-        for b in range(BATCH):
-            nc.vector.memset(start_bias[RUNS_PER_SEQ * b : RUNS_PER_SEQ * b + 1, :], NO_SLOT)
-        ape_before = const.tile([P, RATIO, COLS], F32)
-        nc.vector.tensor_scalar(out=ape_before[:], in0=ape_f[:], scalar1=start_bias[:, 0:1], scalar2=None, op0=ALU.add)
+        for chunk in range(1, LOADS_AHEAD):
+            load(chunk)
 
         ident = const.tile([P, P], F32)
         masks.make_identity(nc, ident[:])
@@ -136,26 +143,36 @@ def tile_deepseekv4attention_pa_t_kernel(
         nc.vector.memset(top[:, 0, :], NO_SLOT)
         nc.vector.memset(top[:, RUN_WINDOWS + 2, :], NO_SLOT)
 
-        def windows_of(chunk):
-            if chunk == 0:
-                return [-1]
-            return [CHUNK_WINDOWS * (chunk - 1) + i for i in range(CHUNK_WINDOWS)]
+        nc.vector.tensor_copy(out=w_words[:, :, 0:COLS].bitcast(I32), in_=raw_words[:, :, COLS : 2 * COLS].bitcast(I32))
+        nc.vector.tensor_copy(out=w_words[:, :, COLS : 2 * COLS].bitcast(I32), in_=raw_words[:, :, 0:COLS].bitcast(I32))
+        nc.vector.tensor_copy(out=w_plane[:, :, 0:FEAT].bitcast(I32), in_=raw_plane[:, :, FEAT:COLS].bitcast(I32))
+        nc.vector.tensor_copy(out=w_plane[:, :, FEAT:COLS].bitcast(I32), in_=raw_plane[:, :, 0:FEAT].bitcast(I32))
+        ape_f = const.tile([P, RATIO, COLS], F32)
+        nc.vector.tensor_copy(out=ape_f[:, :, 0:FEAT], in_=ape_rows[:, :, FEAT:COLS])
+        nc.vector.tensor_copy(out=ape_f[:, :, FEAT:COLS], in_=ape_rows[:, :, 0:FEAT])
+        start_bias = const.tile([P, 1], F32)
+        nc.vector.memset(start_bias[:], 0.0)
+        for b in range(BATCH):
+            nc.vector.memset(start_bias[RUNS_PER_SEQ * b : RUNS_PER_SEQ * b + 1, :], NO_SLOT)
+        ape_before = const.tile([P, RATIO, COLS], F32)
+        nc.vector.tensor_scalar(out=ape_before[:], in0=ape_f[:], scalar1=start_bias[:, 0:1], scalar2=None, op0=ALU.add)
 
+        grouped_tiles = {}
+        code_tiles = {}
+        gate_banks = {}
         kv_banks = {}
         gate_tiles = {}
+        weighted_tiles = {}
+        batch_tiles = {}
 
-        def project(chunk):
-            windows = windows_of(chunk)
-            n_win = len(windows)
-            n_tok = RATIO * n_win
-            first_token = RUN_TOKENS - RATIO if chunk == 0 else RATIO * windows[0]
-            x_sb = x_pool.tile([P, CHUNK_TOKENS, HID], BF16)
-            nc.sync.dma_start(out=x_sb[:, 0:n_tok, :], in_=x_runs[:, first_token : first_token + n_tok, :])
-            x_words = x_sb[:].rearrange("p j k -> p (j k)").bitcast(F32)
+        def flip(chunk, part):
+            n_pairs = RATIO * len(windows_of(chunk)) // 2
+            if part == 0:
+                grouped_tiles[chunk] = grouped_pool.tile([P, CHUNK_TOKENS * P * 4], BF16, align_bytes=64, name="grouped")
+            grouped_words = grouped_tiles[chunk][:].bitcast(F32)
+            x_words = x_tiles[chunk][:].rearrange("p j k -> p (j k)").bitcast(F32)
             order = from_left if chunk == 0 else ident
-            grouped = q_pool.tile([P, CHUNK_TOKENS * P * 4], BF16, align_bytes=64)
-            grouped_words = grouped[:].bitcast(F32)
-            for pair in range(n_tok // 2):
+            for pair in range(part * n_pairs // 2, (part + 1) * n_pairs // 2):
                 flipped = psum_t.tile([P, 2, 2, P], F32)
                 for t in range(2):
                     base = (2 * pair + t) * WORDS
@@ -167,32 +184,42 @@ def tile_deepseekv4attention_pa_t_kernel(
                     ),
                     in_=flipped[:].rearrange("p t h n -> p t n h"),
                 )
-            codes = q_pool.tile([P, CHUNK_TOKENS * P], U32, align_bytes=64)
-            plane = q_pool.tile([P, CHUNK_TOKENS * P], U8, align_bytes=64)
+
+        def quantise(chunk):
+            n_tok = RATIO * len(windows_of(chunk))
+            codes = code_pool.tile([P, CHUNK_TOKENS * P], U32, align_bytes=64)
+            plane = code_pool.tile([P, CHUNK_TOKENS * P], U8, align_bytes=64)
             nc.vector.quantize_mx(
                 out=codes[:, 0 : n_tok * P].bitcast(FP8X4),
                 scales=plane[:, 0 : n_tok * P],
-                in_=grouped[:, 0 : n_tok * P * 4],
+                in_=grouped_tiles[chunk][:, 0 : n_tok * P * 4],
             )
+            code_tiles[chunk] = (codes, plane)
+
+        def multiply(chunk, which, pool, banks):
+            codes, plane = code_tiles[chunk]
+            for i, window in enumerate(windows_of(chunk)):
+                bank = pool.tile([P, RATIO, COLS], F32, name="bank")
+                for r in range(RATIO):
+                    cols = slice((RATIO * i + r) * P, (RATIO * i + r + 1) * P)
+                    nc.tensor.matmul_mx(
+                        out=bank[:, r, :],
+                        lhsT=codes[:, cols].bitcast(FP8X4),
+                        lhsT_scale=plane[:, cols],
+                        rhs=w_words[:, which, :].bitcast(FP4X4),
+                        rhs_scale=w_plane[:, which, :],
+                        start=True,
+                        stop=True,
+                    )
+                banks[window] = bank
+
+        def offset_and_top(chunk):
+            windows = windows_of(chunk)
+            n_win = len(windows)
             offset = ape_before if chunk == 0 else ape_f
             gates = g_pool.tile([P, CHUNK_WINDOWS, RATIO, COLS], F32)
             for i, window in enumerate(windows):
-                gate_ps = psum_g.tile([P, RATIO, COLS], F32)
-                kv_ps = psum_k.tile([P, RATIO, COLS], F32)
-                for which, bank in ((0, gate_ps), (1, kv_ps)):
-                    for r in range(RATIO):
-                        cols = slice((RATIO * i + r) * P, (RATIO * i + r + 1) * P)
-                        nc.tensor.matmul_mx(
-                            out=bank[:, r, :],
-                            lhsT=codes[:, cols].bitcast(FP8X4),
-                            lhsT_scale=plane[:, cols],
-                            rhs=w_words[:, which, :].bitcast(FP4X4),
-                            rhs_scale=w_plane[:, which, :],
-                            start=True,
-                            stop=True,
-                        )
-                kv_banks[window] = kv_ps
-                nc.vector.tensor_tensor(out=gates[:, i], in0=gate_ps[:], in1=offset[:], op=ALU.add)
+                nc.vector.tensor_tensor(out=gates[:, i], in0=gate_banks[window][:], in1=offset[:], op=ALU.add)
             nc.vector.tensor_reduce(
                 out=top[:, windows[0] + 2 : windows[0] + 2 + n_win, :],
                 in_=gates[:, 0:n_win].rearrange("p w r c -> p w c r"),
@@ -200,10 +227,9 @@ def tile_deepseekv4attention_pa_t_kernel(
             )
             gate_tiles[chunk] = gates
 
-        def weigh(chunk):
-            windows = windows_of(chunk)
-            n_win = len(windows)
-            w_a = windows[0]
+        def stabilise(chunk):
+            n_win = len(windows_of(chunk))
+            w_a = windows_of(chunk)[0]
             gates = gate_tiles[chunk]
             peak = m_pool.tile([P, CHUNK_WINDOWS + 1, FEAT], F32)
             nc.vector.tensor_tensor(
@@ -214,42 +240,61 @@ def tile_deepseekv4attention_pa_t_kernel(
             )
             peak_flat = peak[:].rearrange("p t f -> p (t f)")
             for i in range(n_win):
-                nc.gpsimd.tensor_tensor(
+                nc.vector.tensor_tensor(
                     out=gates[:, i], in0=gates[:, i],
                     in1=peak_flat[:, i * FEAT : i * FEAT + COLS].unsqueeze(1).to_broadcast([P, RATIO, COLS]),
                     op=ALU.subtract,
                 )
-            nc.scalar.activation(out=gates[:, 0:n_win], in_=gates[:, 0:n_win], func=ACT.Exp)
-            weighted = e_pool.tile([P, CHUNK_WINDOWS, RATIO, COLS], F32)
-            for i, window in enumerate(windows):
-                nc.vector.tensor_tensor(out=weighted[:, i], in0=kv_banks[window][:], in1=gates[:, i], op=ALU.mult)
-            two = e_pool.tile([P, CHUNK_WINDOWS, 2, COLS], F32)
-            nc.gpsimd.tensor_tensor(out=two[:, 0:n_win], in0=gates[:, 0:n_win, 0:2, :], in1=gates[:, 0:n_win, 2:4, :], op=ALU.add)
-            nc.gpsimd.tensor_tensor(
-                out=den_half[:, w_a + 2 : w_a + 2 + n_win, :], in0=two[:, 0:n_win, 0, :], in1=two[:, 0:n_win, 1, :], op=ALU.add
-            )
-            nc.vector.tensor_reduce(
-                out=num_half[:, w_a + 2 : w_a + 2 + n_win, :],
-                in_=weighted[:, 0:n_win].rearrange("p w r c -> p w c r"),
-                axis=AXIS.X, op=ALU.add,
-            )
 
-        def finish(w0):
+        def exponent(chunk):
+            gates = gate_tiles[chunk]
+            for i in range(len(windows_of(chunk))):
+                nc.scalar.activation(out=gates[:, i], in_=gates[:, i], func=ACT.Exp)
+
+        def weigh(chunk):
+            gates = gate_tiles[chunk]
+            weighted = e_pool.tile([P, CHUNK_WINDOWS, RATIO, COLS], F32)
+            for i, window in enumerate(windows_of(chunk)):
+                nc.vector.tensor_tensor(out=weighted[:, i], in0=kv_banks[window][:], in1=gates[:, i], op=ALU.mult)
+            weighted_tiles[chunk] = weighted
+
+        def sums(chunk):
+            n_win = len(windows_of(chunk))
+            first = windows_of(chunk)[0] + 2
+            for terms, total in ((gate_tiles[chunk], den_half), (weighted_tiles[chunk], num_half)):
+                two = e_pool.tile([P, CHUNK_WINDOWS, 2, COLS], F32)
+                nc.gpsimd.tensor_tensor(out=two[:, 0:n_win], in0=terms[:, 0:n_win, 0:2, :], in1=terms[:, 0:n_win, 2:4, :], op=ALU.add)
+                nc.gpsimd.tensor_tensor(
+                    out=total[:, first : first + n_win, :], in0=two[:, 0:n_win, 0, :], in1=two[:, 0:n_win, 1, :], op=ALU.add
+                )
+
+        def join_halves(w0):
             w1 = w0 + BATCH_TARGETS
             den = o_pool.tile([P, BATCH_TARGETS, FEAT], F32)
             num = o_pool.tile([P, BATCH_TARGETS, FEAT], F32)
             nc.gpsimd.tensor_tensor(
                 out=den[:], in0=den_half[:, w0 + 2 : w1 + 2, 0:FEAT], in1=den_half[:, w0 + 1 : w1 + 1, FEAT:COLS], op=ALU.add
             )
-            nc.vector.tensor_tensor(
+            nc.gpsimd.tensor_tensor(
                 out=num[:], in0=num_half[:, w0 + 2 : w1 + 2, 0:FEAT], in1=num_half[:, w0 + 1 : w1 + 1, FEAT:COLS], op=ALU.add
             )
+            batch_tiles[w0] = [den, num]
+
+        def invert(w0):
+            den = batch_tiles[w0][0]
             nc.scalar.activation(out=den[:], in_=den[:], func=ACT.Ln)
             nc.scalar.activation(out=den[:], in_=den[:], func=ACT.Exp, scale=-1.0)
+
+        def divide(w0):
+            den, num = batch_tiles[w0]
             pooled = o_pool.tile([P, BATCH_TARGETS, FEAT], F32)
             nc.vector.tensor_tensor(out=pooled[:], in0=num[:], in1=den[:], op=ALU.mult)
-            nc.sync.dma_start(out=pooled_runs[:, w0:w1, :], in_=pooled[:])
+            nc.sync.dma_start(out=pooled_runs[:, w0 : w0 + BATCH_TARGETS, :], in_=pooled[:])
+            batch_tiles[w0].append(pooled)
 
+        def rotate(w0):
+            w1 = w0 + BATCH_TARGETS
+            pooled = batch_tiles[w0][2]
             k_rot = o_pool.tile([P, BATCH_TARGETS, FEAT], F32)
             cross = o_pool.tile([P, BATCH_TARGETS, PAIRS, 2], F32)
             plain = FEAT - ROPE
@@ -263,11 +308,43 @@ def tile_deepseekv4attention_pa_t_kernel(
             nc.gpsimd.tensor_tensor(out=pairs_out, in0=pairs_out, in1=cross[:], op=ALU.add)
             nc.sync.dma_start(out=krot_runs[:, w0:w1, :], in_=k_rot[:])
 
-        for step in range(N_CHUNKS + 1):
-            if step < N_CHUNKS:
-                project(step)
-            if step >= 1:
-                weigh(step - 1)
-                last_window = windows_of(step - 1)[-1]
-                if (last_window + 1) % BATCH_TARGETS == 0 and last_window > 0:
-                    finish(last_window + 1 - BATCH_TARGETS)
+        def batch_done_by(chunk):
+            if not 0 <= chunk < N_CHUNKS:
+                return None
+            after = windows_of(chunk)[-1] + 1
+            return after - BATCH_TARGETS if after > 0 and after % BATCH_TARGETS == 0 else None
+
+        def live(chunk):
+            return 0 <= chunk < N_CHUNKS
+
+        for a in range(-3, N_CHUNKS + 6):
+            if live(a - 1):
+                multiply(a - 1, 1, psum_k, kv_banks)
+            if live(a):
+                offset_and_top(a)
+            if live(a + 1):
+                multiply(a + 1, 0, psum_g, gate_banks)
+            if live(a - 1):
+                stabilise(a - 1)
+            if live(a + 3):
+                flip(a + 3, 0)
+            if live(a - 1):
+                exponent(a - 1)
+            if live(a + 3):
+                flip(a + 3, 1)
+            if live(a + 2):
+                quantise(a + 2)
+            if batch_done_by(a - 4) is not None:
+                divide(batch_done_by(a - 4))
+            if live(a - 1):
+                weigh(a - 1)
+            if live(a - 2):
+                sums(a - 2)
+            if batch_done_by(a - 2) is not None:
+                join_halves(batch_done_by(a - 2))
+            if batch_done_by(a - 3) is not None:
+                invert(batch_done_by(a - 3))
+            if batch_done_by(a - 5) is not None:
+                rotate(batch_done_by(a - 5))
+            if live(a + 3 + LOADS_AHEAD):
+                load(a + 3 + LOADS_AHEAD)

@@ -52,8 +52,8 @@ def tile_deepseekv4attention_pa_t_kernel(
         x_pool = ctx.enter_context(tc.tile_pool(name="x", bufs=4))
         grouped_pool = ctx.enter_context(tc.tile_pool(name="grouped", bufs=3))
         code_pool = ctx.enter_context(tc.tile_pool(name="codes", bufs=5))
-        g_pool = ctx.enter_context(tc.tile_pool(name="gates", bufs=4))
-        e_pool = ctx.enter_context(tc.tile_pool(name="weighted", bufs=3))
+        term_pool = ctx.enter_context(tc.tile_pool(name="terms", bufs=6))
+        s_pool = ctx.enter_context(tc.tile_pool(name="sums", bufs=2))
         m_pool = ctx.enter_context(tc.tile_pool(name="maxima", bufs=2))
         o_pool = ctx.enter_context(tc.tile_pool(name="outs", bufs=2))
         psum_t = ctx.enter_context(tc.psum_pool(name="psum_t", bufs=4))
@@ -138,8 +138,7 @@ def tile_deepseekv4attention_pa_t_kernel(
         nc.scalar.activation(out=neg_sin[:], in_=turns[:, 0], func=ACT.Sin, scale=-2.0 * math.pi)
 
         top = const.tile([P, RUN_WINDOWS + 3, COLS], F32)
-        den_half = const.tile([P, RUN_WINDOWS + 3, COLS], F32)
-        num_half = const.tile([P, RUN_WINDOWS + 3, COLS], F32)
+        totals = const.tile([P, RUN_WINDOWS, 2, FEAT], F32)
         nc.vector.memset(top[:, 0, :], NO_SLOT)
         nc.vector.memset(top[:, RUN_WINDOWS + 2, :], NO_SLOT)
 
@@ -161,8 +160,8 @@ def tile_deepseekv4attention_pa_t_kernel(
         code_tiles = {}
         gate_banks = {}
         kv_banks = {}
-        gate_tiles = {}
-        weighted_tiles = {}
+        term_tiles = {}
+        flipped_sums = {}
         batch_tiles = {}
 
         def flip(chunk, part):
@@ -173,7 +172,7 @@ def tile_deepseekv4attention_pa_t_kernel(
             x_words = x_tiles[chunk][:].rearrange("p j k -> p (j k)").bitcast(F32)
             order = from_left if chunk == 0 else ident
             for pair in range(part * n_pairs // 2, (part + 1) * n_pairs // 2):
-                flipped = psum_t.tile([P, 2, 2, P], F32)
+                flipped = psum_t.tile([P, 2, 2, P], F32, tag="ring")
                 for t in range(2):
                     base = (2 * pair + t) * WORDS
                     for h in range(2):
@@ -213,24 +212,29 @@ def tile_deepseekv4attention_pa_t_kernel(
                     )
                 banks[window] = bank
 
+        def by_half(rows):
+            return rows.rearrange("p r (h f) -> p h r f", h=2)
+
         def offset_and_top(chunk):
             windows = windows_of(chunk)
             n_win = len(windows)
             offset = ape_before if chunk == 0 else ape_f
-            gates = g_pool.tile([P, CHUNK_WINDOWS, RATIO, COLS], F32)
+            terms = term_pool.tile([P, CHUNK_WINDOWS, 2, RATIO, 2, FEAT], F32)
             for i, window in enumerate(windows):
-                nc.vector.tensor_tensor(out=gates[:, i], in0=gate_banks[window][:], in1=offset[:], op=ALU.add)
+                nc.vector.tensor_tensor(
+                    out=terms[:, i, :, :, 0, :], in0=by_half(gate_banks[window][:]), in1=by_half(offset[:]), op=ALU.add
+                )
             nc.vector.tensor_reduce(
-                out=top[:, windows[0] + 2 : windows[0] + 2 + n_win, :],
-                in_=gates[:, 0:n_win].rearrange("p w r c -> p w c r"),
+                out=top[:, windows[0] + 2 : windows[0] + 2 + n_win, :].rearrange("p w (h f) -> p (w h) f", h=2),
+                in_=terms[:, 0:n_win, :, :, 0, :].rearrange("p w h r f -> p (w h) f r"),
                 axis=AXIS.X, op=ALU.max,
             )
-            gate_tiles[chunk] = gates
+            term_tiles[chunk] = terms
 
         def stabilise(chunk):
             n_win = len(windows_of(chunk))
             w_a = windows_of(chunk)[0]
-            gates = gate_tiles[chunk]
+            terms = term_tiles[chunk]
             peak = m_pool.tile([P, CHUNK_WINDOWS + 1, FEAT], F32)
             nc.vector.tensor_tensor(
                 out=peak[:, 0 : n_win + 1, :],
@@ -238,63 +242,70 @@ def tile_deepseekv4attention_pa_t_kernel(
                 in1=top[:, w_a + 1 : w_a + n_win + 2, FEAT:COLS],
                 op=ALU.max,
             )
-            peak_flat = peak[:].rearrange("p t f -> p (t f)")
             for i in range(n_win):
-                nc.vector.tensor_tensor(
-                    out=gates[:, i], in0=gates[:, i],
-                    in1=peak_flat[:, i * FEAT : i * FEAT + COLS].unsqueeze(1).to_broadcast([P, RATIO, COLS]),
+                nc.gpsimd.tensor_tensor(
+                    out=terms[:, i, :, :, 0, :], in0=terms[:, i, :, :, 0, :],
+                    in1=peak[:, i : i + 2, :].unsqueeze(2).to_broadcast([P, 2, RATIO, FEAT]),
                     op=ALU.subtract,
                 )
 
-        def exponent(chunk):
-            gates = gate_tiles[chunk]
-            for i in range(len(windows_of(chunk))):
-                nc.scalar.activation(out=gates[:, i], in_=gates[:, i], func=ACT.Exp)
+        def exponent(chunk, i):
+            if i < len(windows_of(chunk)):
+                gates = term_tiles[chunk][:, i, :, :, 0, :].rearrange("p h r f -> p (h r) f")
+                nc.scalar.activation(out=gates, in_=gates, func=ACT.Exp)
 
         def weigh(chunk):
-            gates = gate_tiles[chunk]
-            weighted = e_pool.tile([P, CHUNK_WINDOWS, RATIO, COLS], F32)
+            terms = term_tiles[chunk]
             for i, window in enumerate(windows_of(chunk)):
-                nc.vector.tensor_tensor(out=weighted[:, i], in0=kv_banks[window][:], in1=gates[:, i], op=ALU.mult)
-            weighted_tiles[chunk] = weighted
-
-        def sums(chunk):
-            n_win = len(windows_of(chunk))
-            first = windows_of(chunk)[0] + 2
-            for terms, total in ((gate_tiles[chunk], den_half), (weighted_tiles[chunk], num_half)):
-                two = e_pool.tile([P, CHUNK_WINDOWS, 2, COLS], F32)
-                nc.gpsimd.tensor_tensor(out=two[:, 0:n_win], in0=terms[:, 0:n_win, 0:2, :], in1=terms[:, 0:n_win, 2:4, :], op=ALU.add)
-                nc.gpsimd.tensor_tensor(
-                    out=total[:, first : first + n_win, :], in0=two[:, 0:n_win, 0, :], in1=two[:, 0:n_win, 1, :], op=ALU.add
+                nc.vector.tensor_tensor(
+                    out=terms[:, i, :, :, 1, :], in0=by_half(kv_banks[window][:]), in1=terms[:, i, :, :, 0, :], op=ALU.mult
                 )
 
-        def join_halves(w0):
-            w1 = w0 + BATCH_TARGETS
-            den = o_pool.tile([P, BATCH_TARGETS, FEAT], F32)
-            num = o_pool.tile([P, BATCH_TARGETS, FEAT], F32)
-            nc.gpsimd.tensor_tensor(
-                out=den[:], in0=den_half[:, w0 + 2 : w1 + 2, 0:FEAT], in1=den_half[:, w0 + 1 : w1 + 1, FEAT:COLS], op=ALU.add
+        def slot_sums(chunk):
+            acc = psum_t.tile([P, CHUNK_WINDOWS, P], F32, tag="ring")
+            for i in range(CHUNK_WINDOWS):
+                before = (term_tiles[chunk], i - 1) if i > 0 else (term_tiles[chunk - 1], len(windows_of(chunk - 1)) - 1)
+                pieces = [(term_tiles[chunk], i, 0, r) for r in range(RATIO)]
+                pieces += [(before[0], before[1], 1, r) for r in range(RATIO)]
+                for n, (terms, w, h, r) in enumerate(pieces):
+                    nc.tensor.matmul(
+                        out=acc[:, i, :],
+                        lhsT=terms[:, w, h, r].rearrange("p k f -> p (k f)"),
+                        rhs=ident[:],
+                        is_transpose=True,
+                        start=(n == 0),
+                        stop=(n == len(pieces) - 1),
+                    )
+            acc_sb = s_pool.tile([P, CHUNK_WINDOWS, P], F32)
+            nc.scalar.copy(out=acc_sb[:], in_=acc[:])
+            flipped_sums[chunk] = acc_sb
+
+        def sums_back(chunk):
+            back = psum_t.tile([P, CHUNK_WINDOWS, P], F32, tag="ring")
+            for i in range(CHUNK_WINDOWS):
+                nc.tensor.transpose(back[:, i, :], flipped_sums[chunk][:, i, :], ident[:])
+            w_a = windows_of(chunk)[0]
+            nc.scalar.copy(
+                out=totals[:, w_a : w_a + CHUNK_WINDOWS].rearrange("p w k f -> p w (k f)"), in_=back[:]
             )
-            nc.gpsimd.tensor_tensor(
-                out=num[:], in0=num_half[:, w0 + 2 : w1 + 2, 0:FEAT], in1=num_half[:, w0 + 1 : w1 + 1, FEAT:COLS], op=ALU.add
-            )
-            batch_tiles[w0] = [den, num]
 
         def invert(w0):
-            den = batch_tiles[w0][0]
-            nc.scalar.activation(out=den[:], in_=den[:], func=ACT.Ln)
-            nc.scalar.activation(out=den[:], in_=den[:], func=ACT.Exp, scale=-1.0)
+            inverse = o_pool.tile([P, BATCH_TARGETS, FEAT], F32)
+            nc.scalar.activation(out=inverse[:], in_=totals[:, w0 : w0 + BATCH_TARGETS, 0, :], func=ACT.Ln)
+            nc.scalar.activation(out=inverse[:], in_=inverse[:], func=ACT.Exp, scale=-1.0)
+            batch_tiles[w0] = [inverse]
 
         def divide(w0):
-            den, num = batch_tiles[w0]
             pooled = o_pool.tile([P, BATCH_TARGETS, FEAT], F32)
-            nc.vector.tensor_tensor(out=pooled[:], in0=num[:], in1=den[:], op=ALU.mult)
+            nc.vector.tensor_tensor(
+                out=pooled[:], in0=totals[:, w0 : w0 + BATCH_TARGETS, 1, :], in1=batch_tiles[w0][0][:], op=ALU.mult
+            )
             nc.sync.dma_start(out=pooled_runs[:, w0 : w0 + BATCH_TARGETS, :], in_=pooled[:])
             batch_tiles[w0].append(pooled)
 
         def rotate(w0):
             w1 = w0 + BATCH_TARGETS
-            pooled = batch_tiles[w0][2]
+            pooled = batch_tiles[w0][1]
             k_rot = o_pool.tile([P, BATCH_TARGETS, FEAT], F32)
             cross = o_pool.tile([P, BATCH_TARGETS, PAIRS, 2], F32)
             plain = FEAT - ROPE
@@ -314,37 +325,39 @@ def tile_deepseekv4attention_pa_t_kernel(
             after = windows_of(chunk)[-1] + 1
             return after - BATCH_TARGETS if after > 0 and after % BATCH_TARGETS == 0 else None
 
-        def live(chunk):
-            return 0 <= chunk < N_CHUNKS
+        def live(chunk, first=0):
+            return first <= chunk < N_CHUNKS
 
-        for a in range(-3, N_CHUNKS + 6):
-            if live(a - 1):
-                multiply(a - 1, 1, psum_k, kv_banks)
+        for a in range(-3, N_CHUNKS + 10):
+            if live(a - 3):
+                weigh(a - 3)
+            if live(a + 3):
+                flip(a + 3, 0)
+            if live(a - 2):
+                exponent(a - 2, 0)
+            if live(a + 3):
+                flip(a + 3, 1)
+            if live(a - 2):
+                exponent(a - 2, 1)
+            if live(a - 3, 1):
+                slot_sums(a - 3)
+            if live(a - 4, 1):
+                sums_back(a - 4)
+            if live(a - 2):
+                multiply(a - 2, 1, psum_k, kv_banks)
             if live(a):
                 offset_and_top(a)
             if live(a + 1):
                 multiply(a + 1, 0, psum_g, gate_banks)
-            if live(a - 1):
-                stabilise(a - 1)
-            if live(a + 3):
-                flip(a + 3, 0)
-            if live(a - 1):
-                exponent(a - 1)
-            if live(a + 3):
-                flip(a + 3, 1)
             if live(a + 2):
                 quantise(a + 2)
-            if batch_done_by(a - 4) is not None:
-                divide(batch_done_by(a - 4))
             if live(a - 1):
-                weigh(a - 1)
-            if live(a - 2):
-                sums(a - 2)
-            if batch_done_by(a - 2) is not None:
-                join_halves(batch_done_by(a - 2))
-            if batch_done_by(a - 3) is not None:
-                invert(batch_done_by(a - 3))
+                stabilise(a - 1)
+            if batch_done_by(a - 8) is not None:
+                divide(batch_done_by(a - 8))
             if batch_done_by(a - 5) is not None:
-                rotate(batch_done_by(a - 5))
+                invert(batch_done_by(a - 5))
+            if batch_done_by(a - 9) is not None:
+                rotate(batch_done_by(a - 9))
             if live(a + 3 + LOADS_AHEAD):
                 load(a + 3 + LOADS_AHEAD)

@@ -328,36 +328,34 @@ def tile_deepseekv4attention_pa_t_kernel(
         def live(chunk, first=0):
             return first <= chunk < N_CHUNKS
 
-        for a in range(-3, N_CHUNKS + 10):
+        for a in range(-3, N_CHUNKS + 12):
             if live(a - 3):
                 weigh(a - 3)
             if live(a + 3):
                 flip(a + 3, 0)
             if live(a - 2):
+                multiply(a - 2, 1, psum_k, kv_banks)
                 exponent(a - 2, 0)
+                exponent(a - 2, 1)
             if live(a + 3):
                 flip(a + 3, 1)
-            if live(a - 2):
-                exponent(a - 2, 1)
-            if live(a - 3, 1):
-                slot_sums(a - 3)
-            if live(a - 4, 1):
-                sums_back(a - 4)
-            if live(a - 2):
-                multiply(a - 2, 1, psum_k, kv_banks)
             if live(a):
                 offset_and_top(a)
             if live(a + 1):
                 multiply(a + 1, 0, psum_g, gate_banks)
+            if live(a - 3, 1):
+                slot_sums(a - 3)
+            if live(a - 4, 1):
+                sums_back(a - 4)
             if live(a + 2):
                 quantise(a + 2)
             if live(a - 1):
                 stabilise(a - 1)
-            if batch_done_by(a - 8) is not None:
-                divide(batch_done_by(a - 8))
-            if batch_done_by(a - 5) is not None:
-                invert(batch_done_by(a - 5))
-            if batch_done_by(a - 9) is not None:
-                rotate(batch_done_by(a - 9))
+            if batch_done_by(a - 10) is not None:
+                divide(batch_done_by(a - 10))
+            if batch_done_by(a - 6) is not None:
+                invert(batch_done_by(a - 6))
+            if batch_done_by(a - 11) is not None:
+                rotate(batch_done_by(a - 11))
             if live(a + 3 + LOADS_AHEAD):
                 load(a + 3 + LOADS_AHEAD)

@@ -13,7 +13,6 @@ FP8X4 = mybir.dt.float8_e4m3fn_x4
 FP4X4 = mybir.dt.float4_e2m1fn_x4
 ALU = mybir.AluOpType
 ACT = mybir.ActivationFunctionType
-AXIS = mybir.AxisListType
 
 P = 128
 BATCH, SEQ, HID = 4, 4096, 512
@@ -30,10 +29,11 @@ RUNS_PER_SEQ = SEQ // RUN_TOKENS
 WORDS = HID // 2
 CHUNK_WINDOWS = 2
 CHUNK_TOKENS = CHUNK_WINDOWS * RATIO
+WIDE = CHUNK_WINDOWS * P
 N_CHUNKS = 1 + RUN_WINDOWS // CHUNK_WINDOWS
 BATCH_TARGETS = 8
 LOADS_AHEAD = 3
-NO_SLOT = -1.0e30
+NO_SLOT = -(2.0**100)
 ROUND = 1.5 * 2.0**23
 
 FLOPS = 2 * BATCH * SEQ * HID * 2 * COLS
@@ -50,17 +50,16 @@ def tile_deepseekv4attention_pa_t_kernel(
     with ExitStack() as ctx:
         const = ctx.enter_context(tc.tile_pool(name="const", bufs=1))
         x_pool = ctx.enter_context(tc.tile_pool(name="x", bufs=4))
-        grouped_pool = ctx.enter_context(tc.tile_pool(name="grouped", bufs=3))
-        code_pool = ctx.enter_context(tc.tile_pool(name="codes", bufs=5))
-        term_pool = ctx.enter_context(tc.tile_pool(name="terms", bufs=6))
-        s_pool = ctx.enter_context(tc.tile_pool(name="sums", bufs=2))
-        m_pool = ctx.enter_context(tc.tile_pool(name="maxima", bufs=2))
+        grouped_pool = ctx.enter_context(tc.tile_pool(name="grouped", bufs=2))
+        code_pool = ctx.enter_context(tc.tile_pool(name="codes", bufs=8))
+        t_pool = ctx.enter_context(tc.tile_pool(name="gates", bufs=8))
+        y_pool = ctx.enter_context(tc.tile_pool(name="products", bufs=3))
+        m_pool = ctx.enter_context(tc.tile_pool(name="maxima", bufs=3))
         o_pool = ctx.enter_context(tc.tile_pool(name="outs", bufs=2))
         psum_t = ctx.enter_context(tc.psum_pool(name="psum_t", bufs=4))
         psum_g = ctx.enter_context(tc.psum_pool(name="psum_g", bufs=2))
         psum_k = ctx.enter_context(tc.psum_pool(name="psum_k", bufs=2))
         ctx.enter_context(tc.manual_schedule())
-
 
         def windows_of(chunk):
             if chunk == 0:
@@ -76,24 +75,19 @@ def tile_deepseekv4attention_pa_t_kernel(
             nc.sync.dma_start(out=x_sb[:, 0:n_tok, :], in_=x_runs[:, first_token : first_token + n_tok, :])
             x_tiles[chunk] = x_sb
 
-        raw_words = const.tile([P, 2, 2 * COLS], U8, align_bytes=64)
-        raw_plane = const.tile([P, 2, COLS], U8, align_bytes=64)
         w_words = const.tile([P, 2, 2 * COLS], U8, align_bytes=64)
         w_plane = const.tile([P, 2, COLS], U8, align_bytes=64)
-        ape_rows = const.tile([P, RATIO, COLS], BF16)
-        nc.vector.memset(raw_plane[:].rearrange("p w c -> p (w c)").bitcast(I32), 0)
+        ape_rows = const.tile([P, COLS], BF16)
+        nc.vector.memset(w_plane[:].rearrange("p w c -> p (w c)").bitcast(I32), 0)
         load(0)
         for i, (words, scales) in enumerate(((wgate_words, wgate_scales), (wkv_words, wkv_scales))):
-            nc.sync.dma_start(out=raw_words[:, i, :].bitcast(I32), in_=words[0].bitcast(I32))
+            nc.sync.dma_start(out=w_words[:, i, :].bitcast(I32), in_=words[0].bitcast(I32))
             for quad in range(4):
                 nc.sync.dma_start(
-                    out=raw_plane[32 * quad : 32 * quad + 4, i, :].bitcast(I32),
+                    out=w_plane[32 * quad : 32 * quad + 4, i, :].bitcast(I32),
                     in_=scales[0, 4 * quad : 4 * quad + 4, :].bitcast(I32),
                 )
-        nc.sync.dma_start(
-            out=ape_rows[:].rearrange("p r c -> p (r c)"),
-            in_=ape.rearrange("r c -> (r c)").partition_broadcast(P),
-        )
+        nc.sync.dma_start(out=ape_rows[0:RATIO, :], in_=ape)
         for chunk in range(1, LOADS_AHEAD):
             load(chunk)
 
@@ -102,6 +96,20 @@ def tile_deepseekv4attention_pa_t_kernel(
         from_left = const.tile([P, P], F32)
         nc.vector.tensor_copy(out=from_left[:, 1:P], in_=ident[:, 0 : P - 1])
         nc.vector.tensor_copy(out=from_left[:, 0:1], in_=ident[:, P - 1 : P])
+        upper_down = const.tile([P, P], BF16)
+        lower_up = const.tile([P, P], BF16)
+        nc.vector.memset(upper_down[:], 0.0)
+        nc.vector.memset(lower_up[:], 0.0)
+        nc.vector.tensor_copy(out=upper_down[:, 0:FEAT], in_=ident[:, FEAT:COLS])
+        nc.vector.tensor_copy(out=lower_up[:, FEAT:COLS], in_=ident[:, 0:FEAT])
+
+        ape_square = const.tile([P, P], F32)
+        nc.vector.memset(ape_square[:], 0.0)
+        nc.vector.tensor_copy(out=ape_square[0:RATIO, :], in_=ape_rows[0:RATIO, :])
+        ape_flipped = psum_t.tile([P, P], F32, tag="ring")
+        nc.tensor.transpose(ape_flipped[:], ape_square[:], ident[:])
+        ape_cols = const.tile([P, RATIO], F32)
+        nc.vector.tensor_copy(out=ape_cols[:], in_=ape_flipped[:, 0:RATIO])
 
         win_i = const.tile([P, RUN_WINDOWS], I32)
         nc.gpsimd.iota(win_i[:], pattern=[[1, RUN_WINDOWS]], base=0, channel_multiplier=0)
@@ -114,7 +122,7 @@ def tile_deepseekv4attention_pa_t_kernel(
         run_f = const.tile([P, 1], F32)
         nc.vector.tensor_copy(out=run_f[:], in_=run_i[:])
         run_turns = const.tile([P, PAIRS], F32)
-        turns = const.tile([P, 2, RUN_WINDOWS, PAIRS], F32)
+        turns = t_pool.tile([P, 2, RUN_WINDOWS, PAIRS], F32, name="gates")
         for j in range(PAIRS):
             per_window = RATIO * THETA ** (-j / PAIRS) / (2.0 * math.pi)
             per_run = RUN_WINDOWS * per_window
@@ -127,7 +135,7 @@ def tile_deepseekv4attention_pa_t_kernel(
                 op0=ALU.mult, op1=ALU.add,
             )
         nc.vector.tensor_scalar(out=turns[:, 1], in0=turns[:, 0], scalar1=0.25, scalar2=None, op0=ALU.add)
-        whole = const.tile([P, 2, RUN_WINDOWS, PAIRS], F32)
+        whole = t_pool.tile([P, 2, RUN_WINDOWS, PAIRS], F32, name="gates")
         nc.vector.tensor_scalar(
             out=whole[:], in0=turns[:], scalar1=ROUND, scalar2=ROUND, op0=ALU.add, op1=ALU.subtract
         )
@@ -137,38 +145,32 @@ def tile_deepseekv4attention_pa_t_kernel(
         neg_sin = const.tile([P, RUN_WINDOWS, PAIRS], F32)
         nc.scalar.activation(out=neg_sin[:], in_=turns[:, 0], func=ACT.Sin, scale=-2.0 * math.pi)
 
-        top = const.tile([P, RUN_WINDOWS + 3, COLS], F32)
-        totals = const.tile([P, RUN_WINDOWS, 2, FEAT], F32)
+        top = const.tile([P, RUN_WINDOWS + 3, P], BF16)
         nc.vector.memset(top[:, 0, :], NO_SLOT)
         nc.vector.memset(top[:, RUN_WINDOWS + 2, :], NO_SLOT)
-
-        nc.vector.tensor_copy(out=w_words[:, :, 0:COLS].bitcast(I32), in_=raw_words[:, :, COLS : 2 * COLS].bitcast(I32))
-        nc.vector.tensor_copy(out=w_words[:, :, COLS : 2 * COLS].bitcast(I32), in_=raw_words[:, :, 0:COLS].bitcast(I32))
-        nc.vector.tensor_copy(out=w_plane[:, :, 0:FEAT].bitcast(I32), in_=raw_plane[:, :, FEAT:COLS].bitcast(I32))
-        nc.vector.tensor_copy(out=w_plane[:, :, FEAT:COLS].bitcast(I32), in_=raw_plane[:, :, 0:FEAT].bitcast(I32))
-        ape_f = const.tile([P, RATIO, COLS], F32)
-        nc.vector.tensor_copy(out=ape_f[:, :, 0:FEAT], in_=ape_rows[:, :, FEAT:COLS])
-        nc.vector.tensor_copy(out=ape_f[:, :, FEAT:COLS], in_=ape_rows[:, :, 0:FEAT])
-        start_bias = const.tile([P, 1], F32)
-        nc.vector.memset(start_bias[:], 0.0)
-        for b in range(BATCH):
-            nc.vector.memset(start_bias[RUNS_PER_SEQ * b : RUNS_PER_SEQ * b + 1, :], NO_SLOT)
-        ape_before = const.tile([P, RATIO, COLS], F32)
-        nc.vector.tensor_scalar(out=ape_before[:], in0=ape_f[:], scalar1=start_bias[:, 0:1], scalar2=None, op0=ALU.add)
+        totals = const.tile([P, RUN_WINDOWS + 1, 2, COLS], F32)
 
         grouped_tiles = {}
         code_tiles = {}
         gate_banks = {}
         kv_banks = {}
-        term_tiles = {}
-        flipped_sums = {}
+        gate_tiles = {}
+        half_tops = {}
+        partner_tiles = {}
+        peak_tiles = {}
+        product_tiles = {}
+        sum_banks = {}
         batch_tiles = {}
 
+        def width_of(chunk):
+            return P * len(windows_of(chunk))
+
         def flip(chunk, part):
-            n_pairs = RATIO * len(windows_of(chunk)) // 2
+            n_win = len(windows_of(chunk))
+            n_pairs = RATIO * n_win // 2
             if part == 0:
                 grouped_tiles[chunk] = grouped_pool.tile([P, CHUNK_TOKENS * P * 4], BF16, align_bytes=64, name="grouped")
-            grouped_words = grouped_tiles[chunk][:].bitcast(F32)
+            blocks = grouped_tiles[chunk][:].bitcast(F32).rearrange("p (b n h) -> p b n h", n=P, h=2)
             x_words = x_tiles[chunk][:].rearrange("p j k -> p (j k)").bitcast(F32)
             order = from_left if chunk == 0 else ident
             for pair in range(part * n_pairs // 2, (part + 1) * n_pairs // 2):
@@ -177,10 +179,9 @@ def tile_deepseekv4attention_pa_t_kernel(
                     base = (2 * pair + t) * WORDS
                     for h in range(2):
                         nc.tensor.transpose(flipped[:, t, h, :], x_words[:, base + h : base + WORDS : 2], order[:])
+                first = ((2 * pair) % RATIO) * n_win + (2 * pair) // RATIO
                 nc.scalar.copy(
-                    out=grouped_words[:, pair * 4 * P : (pair + 1) * 4 * P].rearrange(
-                        "p (t n h) -> p t n h", t=2, h=2
-                    ),
+                    out=blocks[:, first : first + n_win + 1 : n_win],
                     in_=flipped[:].rearrange("p t h n -> p t n h"),
                 )
 
@@ -197,122 +198,148 @@ def tile_deepseekv4attention_pa_t_kernel(
 
         def multiply(chunk, which, pool, banks):
             codes, plane = code_tiles[chunk]
-            for i, window in enumerate(windows_of(chunk)):
-                bank = pool.tile([P, RATIO, COLS], F32, name="bank")
-                for r in range(RATIO):
-                    cols = slice((RATIO * i + r) * P, (RATIO * i + r + 1) * P)
+            width = width_of(chunk)
+            banks[chunk] = []
+            for half in range(2):
+                bank = pool.tile([P, 2, WIDE], F32, name="bank")
+                for s in range(2):
+                    r = 2 * half + s
+                    cols = slice(r * width, (r + 1) * width)
                     nc.tensor.matmul_mx(
-                        out=bank[:, r, :],
-                        lhsT=codes[:, cols].bitcast(FP8X4),
-                        lhsT_scale=plane[:, cols],
-                        rhs=w_words[:, which, :].bitcast(FP4X4),
-                        rhs_scale=w_plane[:, which, :],
+                        out=bank[:, s, 0:width],
+                        lhsT=w_words[:, which, :].bitcast(FP4X4),
+                        lhsT_scale=w_plane[:, which, :],
+                        rhs=codes[:, cols].bitcast(FP8X4),
+                        rhs_scale=plane[:, cols],
                         start=True,
                         stop=True,
                     )
-                banks[window] = bank
+                banks[chunk].append(bank)
 
-        def by_half(rows):
-            return rows.rearrange("p r (h f) -> p h r f", h=2)
-
-        def offset_and_top(chunk):
-            windows = windows_of(chunk)
-            n_win = len(windows)
-            offset = ape_before if chunk == 0 else ape_f
-            terms = term_pool.tile([P, CHUNK_WINDOWS, 2, RATIO, 2, FEAT], F32)
-            for i, window in enumerate(windows):
-                nc.vector.tensor_tensor(
-                    out=terms[:, i, :, :, 0, :], in0=by_half(gate_banks[window][:]), in1=by_half(offset[:]), op=ALU.add
+        def offset(chunk):
+            width = width_of(chunk)
+            gates = t_pool.tile([P, RATIO, WIDE], F32, name="gates")
+            for r in range(RATIO):
+                nc.scalar.activation(
+                    out=gates[:, r, 0:width], in_=gate_banks[chunk][r // 2][:, r % 2, 0:width],
+                    func=ACT.Identity, bias=ape_cols[:, r : r + 1], scale=1.0,
                 )
-            nc.vector.tensor_reduce(
-                out=top[:, windows[0] + 2 : windows[0] + 2 + n_win, :].rearrange("p w (h f) -> p (w h) f", h=2),
-                in_=terms[:, 0:n_win, :, :, 0, :].rearrange("p w h r f -> p (w h) f r"),
-                axis=AXIS.X, op=ALU.max,
+            if chunk == 0:
+                nc.vector.memset(gates[:, :, 0:P:RUNS_PER_SEQ], NO_SLOT)
+            gate_tiles[chunk] = gates
+
+        def top_first(chunk):
+            width = width_of(chunk)
+            gates = gate_tiles[chunk]
+            half_top = m_pool.tile([P, 2, WIDE], F32)
+            nc.vector.tensor_tensor(
+                out=half_top[:, :, 0:width], in0=gates[:, 0:2, 0:width], in1=gates[:, 2:4, 0:width], op=ALU.max
             )
-            term_tiles[chunk] = terms
+            half_tops[chunk] = half_top
+
+        def own_top(chunk, shift=0):
+            first = windows_of(chunk)[0] + 2 + shift
+            return top[:, first : first + len(windows_of(chunk)), :].rearrange("p w q -> p (w q)")
+
+        def top_second(chunk):
+            width = width_of(chunk)
+            nc.vector.tensor_tensor(
+                out=own_top(chunk), in0=half_tops[chunk][:, 0, 0:width], in1=half_tops[chunk][:, 1, 0:width], op=ALU.max
+            )
+
+        def exchange(chunk):
+            width = width_of(chunk)
+            partner = psum_t.tile([P, WIDE], F32, tag="ring")
+            nc.tensor.matmul(out=partner[:, 0:width], lhsT=upper_down[:], rhs=own_top(chunk, 1), start=True, stop=False)
+            nc.tensor.matmul(out=partner[:, 0:width], lhsT=lower_up[:], rhs=own_top(chunk, -1), start=False, stop=True)
+            partner_tiles[chunk] = partner
+
+        def peak_of(chunk):
+            width = width_of(chunk)
+            peak = m_pool.tile([P, WIDE], F32)
+            nc.vector.tensor_tensor(
+                out=peak[:, 0:width], in0=partner_tiles[chunk][:, 0:width], in1=own_top(chunk), op=ALU.max
+            )
+            peak_tiles[chunk] = peak
 
         def stabilise(chunk):
-            n_win = len(windows_of(chunk))
-            w_a = windows_of(chunk)[0]
-            terms = term_tiles[chunk]
-            peak = m_pool.tile([P, CHUNK_WINDOWS + 1, FEAT], F32)
+            width = width_of(chunk)
+            gates = gate_tiles[chunk]
             nc.vector.tensor_tensor(
-                out=peak[:, 0 : n_win + 1, :],
-                in0=top[:, w_a + 2 : w_a + n_win + 3, 0:FEAT],
-                in1=top[:, w_a + 1 : w_a + n_win + 2, FEAT:COLS],
-                op=ALU.max,
+                out=gates[:, :, 0:width], in0=gates[:, :, 0:width],
+                in1=peak_tiles[chunk][:, 0:width].unsqueeze(1).to_broadcast([P, RATIO, width]),
+                op=ALU.subtract,
             )
-            for i in range(n_win):
-                nc.gpsimd.tensor_tensor(
-                    out=terms[:, i, :, :, 0, :], in0=terms[:, i, :, :, 0, :],
-                    in1=peak[:, i : i + 2, :].unsqueeze(2).to_broadcast([P, 2, RATIO, FEAT]),
-                    op=ALU.subtract,
-                )
 
-        def exponent(chunk, i):
-            if i < len(windows_of(chunk)):
-                gates = term_tiles[chunk][:, i, :, :, 0, :].rearrange("p h r f -> p (h r) f")
-                nc.scalar.activation(out=gates, in_=gates, func=ACT.Exp)
+        def exponent(chunk):
+            width = width_of(chunk)
+            gates = gate_tiles[chunk]
+            nc.scalar.activation(out=gates[:, :, 0:width], in_=gates[:, :, 0:width], func=ACT.Exp)
 
-        def weigh(chunk):
-            terms = term_tiles[chunk]
-            for i, window in enumerate(windows_of(chunk)):
-                nc.vector.tensor_tensor(
-                    out=terms[:, i, :, :, 1, :], in0=by_half(kv_banks[window][:]), in1=terms[:, i, :, :, 0, :], op=ALU.mult
-                )
+        def weigh(chunk, half):
+            width = width_of(chunk)
+            if half == 0:
+                product_tiles[chunk] = y_pool.tile([P, RATIO, WIDE], F32, name="products")
+            rows = slice(2 * half, 2 * half + 2)
+            nc.vector.tensor_tensor(
+                out=product_tiles[chunk][:, rows, 0:width], in0=kv_banks[chunk][half][:, :, 0:width],
+                in1=gate_tiles[chunk][:, rows, 0:width], op=ALU.mult,
+            )
 
         def slot_sums(chunk):
-            acc = psum_t.tile([P, CHUNK_WINDOWS, P], F32, tag="ring")
-            for i in range(CHUNK_WINDOWS):
-                before = (term_tiles[chunk], i - 1) if i > 0 else (term_tiles[chunk - 1], len(windows_of(chunk - 1)) - 1)
-                pieces = [(term_tiles[chunk], i, 0, r) for r in range(RATIO)]
-                pieces += [(before[0], before[1], 1, r) for r in range(RATIO)]
-                for n, (terms, w, h, r) in enumerate(pieces):
-                    nc.tensor.matmul(
-                        out=acc[:, i, :],
-                        lhsT=terms[:, w, h, r].rearrange("p k f -> p (k f)"),
-                        rhs=ident[:],
-                        is_transpose=True,
-                        start=(n == 0),
-                        stop=(n == len(pieces) - 1),
-                    )
-            acc_sb = s_pool.tile([P, CHUNK_WINDOWS, P], F32)
-            nc.scalar.copy(out=acc_sb[:], in_=acc[:])
-            flipped_sums[chunk] = acc_sb
+            acc = psum_t.tile([P, CHUNK_WINDOWS, 2, COLS], F32, tag="ring")
+            for i in range(len(windows_of(chunk))):
+                for kind, terms in enumerate((gate_tiles[chunk], product_tiles[chunk])):
+                    for r in range(RATIO):
+                        nc.tensor.matmul(
+                            out=acc[:, i, kind, :],
+                            lhsT=terms[:, r, i * P : (i + 1) * P],
+                            rhs=ident[:],
+                            is_transpose=True,
+                            start=(r == 0),
+                            stop=(r == RATIO - 1),
+                        )
+            sum_banks[chunk] = acc
 
-        def sums_back(chunk):
-            back = psum_t.tile([P, CHUNK_WINDOWS, P], F32, tag="ring")
-            for i in range(CHUNK_WINDOWS):
-                nc.tensor.transpose(back[:, i, :], flipped_sums[chunk][:, i, :], ident[:])
-            w_a = windows_of(chunk)[0]
+        def sums_out(chunk):
+            n_win = len(windows_of(chunk))
+            first = windows_of(chunk)[0] + 1
             nc.scalar.copy(
-                out=totals[:, w_a : w_a + CHUNK_WINDOWS].rearrange("p w k f -> p w (k f)"), in_=back[:]
+                out=totals[:, first : first + n_win].rearrange("p w k c -> p (w k c)"),
+                in_=sum_banks[chunk][:, 0:n_win].rearrange("p w k c -> p (w k c)"),
             )
+
+        def fold(w0):
+            both = o_pool.tile([P, BATCH_TARGETS, 2, FEAT], F32)
+            nc.vector.tensor_tensor(
+                out=both[:], in0=totals[:, w0 : w0 + BATCH_TARGETS, :, 0:FEAT],
+                in1=totals[:, w0 + 1 : w0 + 1 + BATCH_TARGETS, :, FEAT:COLS], op=ALU.add,
+            )
+            batch_tiles[w0] = [both]
 
         def invert(w0):
             inverse = o_pool.tile([P, BATCH_TARGETS, FEAT], F32)
-            nc.scalar.activation(out=inverse[:], in_=totals[:, w0 : w0 + BATCH_TARGETS, 0, :], func=ACT.Ln)
-            nc.scalar.activation(out=inverse[:], in_=inverse[:], func=ACT.Exp, scale=-1.0)
-            batch_tiles[w0] = [inverse]
+            nc.vector.reciprocal(out=inverse[:], in_=batch_tiles[w0][0][:, :, 0, :])
+            batch_tiles[w0].append(inverse)
 
         def divide(w0):
             pooled = o_pool.tile([P, BATCH_TARGETS, FEAT], F32)
             nc.vector.tensor_tensor(
-                out=pooled[:], in0=totals[:, w0 : w0 + BATCH_TARGETS, 1, :], in1=batch_tiles[w0][0][:], op=ALU.mult
+                out=pooled[:], in0=batch_tiles[w0][0][:, :, 1, :], in1=batch_tiles[w0][1][:], op=ALU.mult
             )
             nc.sync.dma_start(out=pooled_runs[:, w0 : w0 + BATCH_TARGETS, :], in_=pooled[:])
             batch_tiles[w0].append(pooled)
 
         def rotate(w0):
             w1 = w0 + BATCH_TARGETS
-            pooled = batch_tiles[w0][1]
+            pooled = batch_tiles[w0][2]
             k_rot = o_pool.tile([P, BATCH_TARGETS, FEAT], F32)
             cross = o_pool.tile([P, BATCH_TARGETS, PAIRS, 2], F32)
             plain = FEAT - ROPE
             pairs_in = pooled[:, :, plain:FEAT].rearrange("p w (j e) -> p w j e", e=2)
             pairs_out = k_rot[:, :, plain:FEAT].rearrange("p w (j e) -> p w j e", e=2)
             cos = sin_cos[:, 1, w0:w1, :].unsqueeze(3).to_broadcast([P, BATCH_TARGETS, PAIRS, 2])
-            nc.scalar.copy(out=k_rot[:, :, 0:plain], in_=pooled[:, :, 0:plain])
+            nc.gpsimd.tensor_copy(out=k_rot[:, :, 0:plain], in_=pooled[:, :, 0:plain])
             nc.gpsimd.tensor_tensor(out=pairs_out, in0=pairs_in, in1=cos, op=ALU.mult)
             nc.gpsimd.tensor_tensor(out=cross[:, :, :, 0], in0=pairs_in[:, :, :, 1], in1=neg_sin[:, w0:w1, :], op=ALU.mult)
             nc.gpsimd.tensor_tensor(out=cross[:, :, :, 1], in0=pairs_in[:, :, :, 0], in1=sin_cos[:, 0, w0:w1, :], op=ALU.mult)
@@ -325,37 +352,48 @@ def tile_deepseekv4attention_pa_t_kernel(
             after = windows_of(chunk)[-1] + 1
             return after - BATCH_TARGETS if after > 0 and after % BATCH_TARGETS == 0 else None
 
-        def live(chunk, first=0):
-            return first <= chunk < N_CHUNKS
+        def live(chunk):
+            return 0 <= chunk < N_CHUNKS
 
-        for a in range(-3, N_CHUNKS + 12):
+        for a in range(-3, N_CHUNKS + 11):
+            if live(a - 6):
+                sums_out(a - 6)
             if live(a - 3):
-                weigh(a - 3)
-            if live(a + 3):
-                flip(a + 3, 0)
-            if live(a - 2):
-                multiply(a - 2, 1, psum_k, kv_banks)
-                exponent(a - 2, 0)
-                exponent(a - 2, 1)
-            if live(a + 3):
-                flip(a + 3, 1)
-            if live(a):
-                offset_and_top(a)
+                stabilise(a - 3)
             if live(a + 1):
                 multiply(a + 1, 0, psum_g, gate_banks)
-            if live(a - 3, 1):
-                slot_sums(a - 3)
-            if live(a - 4, 1):
-                sums_back(a - 4)
+            if live(a - 4):
+                multiply(a - 4, 1, psum_k, kv_banks)
+            if live(a + 1):
+                offset(a + 1)
+            if live(a):
+                top_first(a)
+            if live(a + 3):
+                flip(a + 3, 0)
+            if live(a - 4):
+                weigh(a - 4, 0)
+            if live(a - 3):
+                exponent(a - 3)
+            if live(a + 3):
+                flip(a + 3, 1)
             if live(a + 2):
                 quantise(a + 2)
-            if live(a - 1):
-                stabilise(a - 1)
+            if live(a - 4):
+                weigh(a - 4, 1)
+            if live(a - 2):
+                exchange(a - 2)
+                peak_of(a - 2)
+            if live(a - 5):
+                slot_sums(a - 5)
+            if live(a):
+                top_second(a)
+            if batch_done_by(a - 7) is not None:
+                fold(batch_done_by(a - 7))
+            if batch_done_by(a - 8) is not None:
+                invert(batch_done_by(a - 8))
+            if batch_done_by(a - 9) is not None:
+                divide(batch_done_by(a - 9))
             if batch_done_by(a - 10) is not None:
-                divide(batch_done_by(a - 10))
-            if batch_done_by(a - 6) is not None:
-                invert(batch_done_by(a - 6))
-            if batch_done_by(a - 11) is not None:
-                rotate(batch_done_by(a - 11))
+                rotate(batch_done_by(a - 10))
             if live(a + 3 + LOADS_AHEAD):
                 load(a + 3 + LOADS_AHEAD)

@@ -32,6 +32,7 @@ CHUNK_TOKENS = CHUNK_WINDOWS * RATIO
 WIDE = CHUNK_WINDOWS * P
 N_CHUNKS = 1 + RUN_WINDOWS // CHUNK_WINDOWS
 BATCH_TARGETS = 8
+LAST_BATCH = RUN_WINDOWS - BATCH_TARGETS
 LOADS_AHEAD = 3
 NO_SLOT = -(2.0**100)
 ROUND = 1.5 * 2.0**23
@@ -51,11 +52,11 @@ def tile_deepseekv4attention_pa_t_kernel(
         const = ctx.enter_context(tc.tile_pool(name="const", bufs=1))
         x_pool = ctx.enter_context(tc.tile_pool(name="x", bufs=4))
         grouped_pool = ctx.enter_context(tc.tile_pool(name="grouped", bufs=2))
-        code_pool = ctx.enter_context(tc.tile_pool(name="codes", bufs=8))
+        code_pool = ctx.enter_context(tc.tile_pool(name="codes", bufs=7))
         t_pool = ctx.enter_context(tc.tile_pool(name="gates", bufs=8))
         y_pool = ctx.enter_context(tc.tile_pool(name="products", bufs=3))
         m_pool = ctx.enter_context(tc.tile_pool(name="maxima", bufs=3))
-        o_pool = ctx.enter_context(tc.tile_pool(name="outs", bufs=2))
+        o_pool = ctx.enter_context(tc.tile_pool(name="outs", bufs=4))
         psum_t = ctx.enter_context(tc.psum_pool(name="psum_t", bufs=4))
         psum_g = ctx.enter_context(tc.psum_pool(name="psum_g", bufs=2))
         psum_k = ctx.enter_context(tc.psum_pool(name="psum_k", bufs=2))
@@ -149,6 +150,7 @@ def tile_deepseekv4attention_pa_t_kernel(
         nc.vector.memset(top[:, 0, :], NO_SLOT)
         nc.vector.memset(top[:, RUN_WINDOWS + 2, :], NO_SLOT)
         totals = const.tile([P, RUN_WINDOWS + 1, 2, COLS], F32)
+        inverse = const.tile([P, RUN_WINDOWS, FEAT], F32)
 
         grouped_tiles = {}
         code_tiles = {}
@@ -310,40 +312,39 @@ def tile_deepseekv4attention_pa_t_kernel(
             )
 
         def fold(w0):
-            both = o_pool.tile([P, BATCH_TARGETS, 2, FEAT], F32)
-            nc.vector.tensor_tensor(
-                out=both[:], in0=totals[:, w0 : w0 + BATCH_TARGETS, :, 0:FEAT],
-                in1=totals[:, w0 + 1 : w0 + 1 + BATCH_TARGETS, :, FEAT:COLS], op=ALU.add,
-            )
-            batch_tiles[w0] = [both]
+            here = totals[:, w0 + 1 : w0 + 1 + BATCH_TARGETS, :, FEAT:COLS]
+            nc.vector.tensor_tensor(out=here, in0=totals[:, w0 : w0 + BATCH_TARGETS, :, 0:FEAT], in1=here, op=ALU.add)
+
+        def logarithm(w0, w1):
+            nc.scalar.activation(out=inverse[:, w0:w1, :], in_=totals[:, w0 + 1 : w1 + 1, 0, FEAT:COLS], func=ACT.Ln)
 
         def invert(w0):
-            inverse = o_pool.tile([P, BATCH_TARGETS, FEAT], F32)
-            nc.vector.reciprocal(out=inverse[:], in_=batch_tiles[w0][0][:, :, 0, :])
-            batch_tiles[w0].append(inverse)
+            rows = inverse[:, w0 : w0 + BATCH_TARGETS, :]
+            nc.scalar.activation(out=rows, in_=rows, func=ACT.Exp, scale=-1.0)
 
         def divide(w0):
             pooled = o_pool.tile([P, BATCH_TARGETS, FEAT], F32)
             nc.vector.tensor_tensor(
-                out=pooled[:], in0=batch_tiles[w0][0][:, :, 1, :], in1=batch_tiles[w0][1][:], op=ALU.mult
+                out=pooled[:], in0=totals[:, w0 + 1 : w0 + 1 + BATCH_TARGETS, 1, FEAT:COLS],
+                in1=inverse[:, w0 : w0 + BATCH_TARGETS, :], op=ALU.mult,
             )
             nc.sync.dma_start(out=pooled_runs[:, w0 : w0 + BATCH_TARGETS, :], in_=pooled[:])
-            batch_tiles[w0].append(pooled)
+            batch_tiles[w0] = pooled
 
-        def rotate(w0):
+        def rotate(w0, engine):
             w1 = w0 + BATCH_TARGETS
-            pooled = batch_tiles[w0][2]
+            pooled = batch_tiles[w0]
             k_rot = o_pool.tile([P, BATCH_TARGETS, FEAT], F32)
             cross = o_pool.tile([P, BATCH_TARGETS, PAIRS, 2], F32)
             plain = FEAT - ROPE
             pairs_in = pooled[:, :, plain:FEAT].rearrange("p w (j e) -> p w j e", e=2)
             pairs_out = k_rot[:, :, plain:FEAT].rearrange("p w (j e) -> p w j e", e=2)
             cos = sin_cos[:, 1, w0:w1, :].unsqueeze(3).to_broadcast([P, BATCH_TARGETS, PAIRS, 2])
-            nc.gpsimd.tensor_copy(out=k_rot[:, :, 0:plain], in_=pooled[:, :, 0:plain])
-            nc.gpsimd.tensor_tensor(out=pairs_out, in0=pairs_in, in1=cos, op=ALU.mult)
-            nc.gpsimd.tensor_tensor(out=cross[:, :, :, 0], in0=pairs_in[:, :, :, 1], in1=neg_sin[:, w0:w1, :], op=ALU.mult)
-            nc.gpsimd.tensor_tensor(out=cross[:, :, :, 1], in0=pairs_in[:, :, :, 0], in1=sin_cos[:, 0, w0:w1, :], op=ALU.mult)
-            nc.gpsimd.tensor_tensor(out=pairs_out, in0=pairs_out, in1=cross[:], op=ALU.add)
+            nc.scalar.copy(out=k_rot[:, :, 0:plain], in_=pooled[:, :, 0:plain])
+            engine.tensor_tensor(out=pairs_out, in0=pairs_in, in1=cos, op=ALU.mult)
+            engine.tensor_tensor(out=cross[:, :, :, 0], in0=pairs_in[:, :, :, 1], in1=neg_sin[:, w0:w1, :], op=ALU.mult)
+            engine.tensor_tensor(out=cross[:, :, :, 1], in0=pairs_in[:, :, :, 0], in1=sin_cos[:, 0, w0:w1, :], op=ALU.mult)
+            engine.tensor_tensor(out=pairs_out, in0=pairs_out, in1=cross[:], op=ALU.add)
             nc.sync.dma_start(out=krot_runs[:, w0:w1, :], in_=k_rot[:])
 
         def batch_done_by(chunk):
@@ -355,9 +356,11 @@ def tile_deepseekv4attention_pa_t_kernel(
         def live(chunk):
             return 0 <= chunk < N_CHUNKS
 
-        for a in range(-3, N_CHUNKS + 11):
+        for a in range(-3, N_CHUNKS + 8):
             if live(a - 6):
                 sums_out(a - 6)
+            if a - 3 == N_CHUNKS:
+                logarithm(0, LAST_BATCH)
             if live(a - 3):
                 stabilise(a - 3)
             if live(a + 1):
@@ -389,11 +392,17 @@ def tile_deepseekv4attention_pa_t_kernel(
                 top_second(a)
             if batch_done_by(a - 7) is not None:
                 fold(batch_done_by(a - 7))
-            if batch_done_by(a - 8) is not None:
-                invert(batch_done_by(a - 8))
-            if batch_done_by(a - 9) is not None:
-                divide(batch_done_by(a - 9))
-            if batch_done_by(a - 10) is not None:
-                rotate(batch_done_by(a - 10))
             if live(a + 3 + LOADS_AHEAD):
                 load(a + 3 + LOADS_AHEAD)
+
+        logarithm(LAST_BATCH, RUN_WINDOWS)
+        invert(LAST_BATCH)
+        for w0 in range(0, LAST_BATCH, BATCH_TARGETS):
+            invert(w0)
+        divide(LAST_BATCH)
+        divide(0)
+        rotate(0, nc.gpsimd)
+        rotate(LAST_BATCH, nc.vector)
+        for w0 in range(BATCH_TARGETS, LAST_BATCH, BATCH_TARGETS):
+            divide(w0)
+            rotate(w0, nc.vector)

@@ -34,6 +34,8 @@ N_CHUNKS = 1 + RUN_WINDOWS // CHUNK_WINDOWS
 BATCH_TARGETS = 8
 LAST_BATCH = RUN_WINDOWS - BATCH_TARGETS
 LOADS_AHEAD = 3
+VECTOR_HELPS = 3
+TRIG_ROUND = 1
 NO_SLOT = -(2.0**100)
 ROUND = 1.5 * 2.0**23
 
@@ -52,14 +54,13 @@ def tile_deepseekv4attention_pa_t_kernel(
         const = ctx.enter_context(tc.tile_pool(name="const", bufs=1))
         x_pool = ctx.enter_context(tc.tile_pool(name="x", bufs=4))
         grouped_pool = ctx.enter_context(tc.tile_pool(name="grouped", bufs=2))
-        code_pool = ctx.enter_context(tc.tile_pool(name="codes", bufs=7))
-        t_pool = ctx.enter_context(tc.tile_pool(name="gates", bufs=8))
-        y_pool = ctx.enter_context(tc.tile_pool(name="products", bufs=3))
-        m_pool = ctx.enter_context(tc.tile_pool(name="maxima", bufs=3))
+        code_pool = ctx.enter_context(tc.tile_pool(name="codes", bufs=5))
+        t_pool = ctx.enter_context(tc.tile_pool(name="gates", bufs=5))
+        y_pool = ctx.enter_context(tc.tile_pool(name="products", bufs=2))
+        m_pool = ctx.enter_context(tc.tile_pool(name="maxima", bufs=2))
         o_pool = ctx.enter_context(tc.tile_pool(name="outs", bufs=4))
-        psum_t = ctx.enter_context(tc.psum_pool(name="psum_t", bufs=4))
-        psum_g = ctx.enter_context(tc.psum_pool(name="psum_g", bufs=2))
-        psum_k = ctx.enter_context(tc.psum_pool(name="psum_k", bufs=2))
+        psum_t = ctx.enter_context(tc.psum_pool(name="psum_t", bufs=6))
+        psum_m = ctx.enter_context(tc.psum_pool(name="psum_m", bufs=2))
         ctx.enter_context(tc.manual_schedule())
 
         def windows_of(chunk):
@@ -104,14 +105,6 @@ def tile_deepseekv4attention_pa_t_kernel(
         nc.vector.tensor_copy(out=upper_down[:, 0:FEAT], in_=ident[:, FEAT:COLS])
         nc.vector.tensor_copy(out=lower_up[:, FEAT:COLS], in_=ident[:, 0:FEAT])
 
-        ape_square = const.tile([P, P], F32)
-        nc.vector.memset(ape_square[:], 0.0)
-        nc.vector.tensor_copy(out=ape_square[0:RATIO, :], in_=ape_rows[0:RATIO, :])
-        ape_flipped = psum_t.tile([P, P], F32, tag="ring")
-        nc.tensor.transpose(ape_flipped[:], ape_square[:], ident[:])
-        ape_cols = const.tile([P, RATIO], F32)
-        nc.vector.tensor_copy(out=ape_cols[:], in_=ape_flipped[:, 0:RATIO])
-
         win_i = const.tile([P, RUN_WINDOWS], I32)
         nc.gpsimd.iota(win_i[:], pattern=[[1, RUN_WINDOWS]], base=0, channel_multiplier=0)
         part_i = const.tile([P, 1], I32)
@@ -123,7 +116,7 @@ def tile_deepseekv4attention_pa_t_kernel(
         run_f = const.tile([P, 1], F32)
         nc.vector.tensor_copy(out=run_f[:], in_=run_i[:])
         run_turns = const.tile([P, PAIRS], F32)
-        turns = t_pool.tile([P, 2, RUN_WINDOWS, PAIRS], F32, name="gates")
+        turns = y_pool.tile([P, 2, RUN_WINDOWS, PAIRS], F32, name="products")
         for j in range(PAIRS):
             per_window = RATIO * THETA ** (-j / PAIRS) / (2.0 * math.pi)
             per_run = RUN_WINDOWS * per_window
@@ -136,15 +129,28 @@ def tile_deepseekv4attention_pa_t_kernel(
                 op0=ALU.mult, op1=ALU.add,
             )
         nc.vector.tensor_scalar(out=turns[:, 1], in0=turns[:, 0], scalar1=0.25, scalar2=None, op0=ALU.add)
-        whole = t_pool.tile([P, 2, RUN_WINDOWS, PAIRS], F32, name="gates")
+        whole = y_pool.tile([P, 2, RUN_WINDOWS, PAIRS], F32, name="products")
         nc.vector.tensor_scalar(
             out=whole[:], in0=turns[:], scalar1=ROUND, scalar2=ROUND, op0=ALU.add, op1=ALU.subtract
         )
         nc.vector.tensor_tensor(out=turns[:], in0=turns[:], in1=whole[:], op=ALU.subtract)
-        sin_cos = const.tile([P, 2, RUN_WINDOWS, PAIRS], F32)
-        nc.scalar.activation(out=sin_cos[:], in_=turns[:], func=ACT.Sin, scale=2.0 * math.pi)
-        neg_sin = const.tile([P, RUN_WINDOWS, PAIRS], F32)
-        nc.scalar.activation(out=neg_sin[:], in_=turns[:, 0], func=ACT.Sin, scale=-2.0 * math.pi)
+        cos = const.tile([P, RUN_WINDOWS, PAIRS], F32)
+        sin_pairs = const.tile([P, RUN_WINDOWS, PAIRS, 2], F32)
+
+        def trigonometry():
+            nc.scalar.activation(out=cos[:], in_=turns[:, 1], func=ACT.Sin, scale=2.0 * math.pi)
+            nc.scalar.activation(out=sin_pairs[:, :, :, 0], in_=turns[:, 0], func=ACT.Sin, scale=-2.0 * math.pi)
+            nc.scalar.activation(out=sin_pairs[:, :, :, 1], in_=turns[:, 0], func=ACT.Sin, scale=2.0 * math.pi)
+
+        ape_square = const.tile([P, P], F32)
+        nc.vector.memset(ape_square[:], 0.0)
+        nc.vector.tensor_copy(out=ape_square[0:RATIO, :], in_=ape_rows[0:RATIO, :])
+        ape_cols = const.tile([P, RATIO], F32)
+
+        def flip_offset():
+            ape_flipped = psum_t.tile([P, P], F32, tag="ring")
+            nc.tensor.transpose(ape_flipped[:], ape_square[:], ident[:])
+            nc.vector.tensor_copy(out=ape_cols[:], in_=ape_flipped[:, 0:RATIO])
 
         top = const.tile([P, RUN_WINDOWS + 3, P], BF16)
         nc.vector.memset(top[:, 0, :], NO_SLOT)
@@ -167,25 +173,25 @@ def tile_deepseekv4attention_pa_t_kernel(
         def width_of(chunk):
             return P * len(windows_of(chunk))
 
-        def flip(chunk, part):
+        def flip(chunk):
             n_win = len(windows_of(chunk))
             n_pairs = RATIO * n_win // 2
-            if part == 0:
-                grouped_tiles[chunk] = grouped_pool.tile([P, CHUNK_TOKENS * P * 4], BF16, align_bytes=64, name="grouped")
+            grouped_tiles[chunk] = grouped_pool.tile([P, CHUNK_TOKENS * P * 4], BF16, align_bytes=64, name="grouped")
             blocks = grouped_tiles[chunk][:].bitcast(F32).rearrange("p (b n h) -> p b n h", n=P, h=2)
             x_words = x_tiles[chunk][:].rearrange("p j k -> p (j k)").bitcast(F32)
             order = from_left if chunk == 0 else ident
-            for pair in range(part * n_pairs // 2, (part + 1) * n_pairs // 2):
+            for pair in range(n_pairs):
                 flipped = psum_t.tile([P, 2, 2, P], F32, tag="ring")
                 for t in range(2):
                     base = (2 * pair + t) * WORDS
                     for h in range(2):
                         nc.tensor.transpose(flipped[:, t, h, :], x_words[:, base + h : base + WORDS : 2], order[:])
                 first = ((2 * pair) % RATIO) * n_win + (2 * pair) // RATIO
-                nc.scalar.copy(
-                    out=blocks[:, first : first + n_win + 1 : n_win],
-                    in_=flipped[:].rearrange("p t h n -> p t n h"),
-                )
+                out = blocks[:, first : first + n_win + 1 : n_win]
+                if chunk < VECTOR_HELPS and pair % 2 == 1:
+                    nc.vector.tensor_copy(out=out, in_=flipped[:].rearrange("p t h n -> p t n h"))
+                else:
+                    nc.scalar.copy(out=out, in_=flipped[:].rearrange("p t h n -> p t n h"))
 
         def quantise(chunk):
             n_tok = RATIO * len(windows_of(chunk))
@@ -198,32 +204,30 @@ def tile_deepseekv4attention_pa_t_kernel(
             )
             code_tiles[chunk] = (codes, plane)
 
-        def multiply(chunk, which, pool, banks):
+        def multiply(chunk, which, banks):
             codes, plane = code_tiles[chunk]
             width = width_of(chunk)
             banks[chunk] = []
             for half in range(2):
-                bank = pool.tile([P, 2, WIDE], F32, name="bank")
-                for s in range(2):
-                    r = 2 * half + s
-                    cols = slice(r * width, (r + 1) * width)
-                    nc.tensor.matmul_mx(
-                        out=bank[:, s, 0:width],
-                        lhsT=w_words[:, which, :].bitcast(FP4X4),
-                        lhsT_scale=w_plane[:, which, :],
-                        rhs=codes[:, cols].bitcast(FP8X4),
-                        rhs_scale=plane[:, cols],
-                        start=True,
-                        stop=True,
-                    )
-                banks[chunk].append(bank)
+                bank = psum_m.tile([P, 2 * WIDE], F32, name="bank")
+                cols = slice(2 * half * width, 2 * (half + 1) * width)
+                nc.tensor.matmul_mx(
+                    out=bank[:, 0 : 2 * width],
+                    lhsT=w_words[:, which, :].bitcast(FP4X4),
+                    lhsT_scale=w_plane[:, which, :],
+                    rhs=codes[:, cols].bitcast(FP8X4),
+                    rhs_scale=plane[:, cols],
+                    start=True,
+                    stop=True,
+                )
+                banks[chunk].append(bank[:, 0 : 2 * width].rearrange("p (s n) -> p s n", s=2))
 
         def offset(chunk):
             width = width_of(chunk)
             gates = t_pool.tile([P, RATIO, WIDE], F32, name="gates")
             for r in range(RATIO):
                 nc.scalar.activation(
-                    out=gates[:, r, 0:width], in_=gate_banks[chunk][r // 2][:, r % 2, 0:width],
+                    out=gates[:, r, 0:width], in_=gate_banks[chunk][r // 2][:, r % 2, :],
                     func=ACT.Identity, bias=ape_cols[:, r : r + 1], scale=1.0,
                 )
             if chunk == 0:
@@ -284,7 +288,7 @@ def tile_deepseekv4attention_pa_t_kernel(
                 product_tiles[chunk] = y_pool.tile([P, RATIO, WIDE], F32, name="products")
             rows = slice(2 * half, 2 * half + 2)
             nc.vector.tensor_tensor(
-                out=product_tiles[chunk][:, rows, 0:width], in0=kv_banks[chunk][half][:, :, 0:width],
+                out=product_tiles[chunk][:, rows, 0:width], in0=kv_banks[chunk][half],
                 in1=gate_tiles[chunk][:, rows, 0:width], op=ALU.mult,
             )
 
@@ -339,11 +343,12 @@ def tile_deepseekv4attention_pa_t_kernel(
             plain = FEAT - ROPE
             pairs_in = pooled[:, :, plain:FEAT].rearrange("p w (j e) -> p w j e", e=2)
             pairs_out = k_rot[:, :, plain:FEAT].rearrange("p w (j e) -> p w j e", e=2)
-            cos = sin_cos[:, 1, w0:w1, :].unsqueeze(3).to_broadcast([P, BATCH_TARGETS, PAIRS, 2])
-            nc.scalar.copy(out=k_rot[:, :, 0:plain], in_=pooled[:, :, 0:plain])
-            engine.tensor_tensor(out=pairs_out, in0=pairs_in, in1=cos, op=ALU.mult)
-            engine.tensor_tensor(out=cross[:, :, :, 0], in0=pairs_in[:, :, :, 1], in1=neg_sin[:, w0:w1, :], op=ALU.mult)
-            engine.tensor_tensor(out=cross[:, :, :, 1], in0=pairs_in[:, :, :, 0], in1=sin_cos[:, 0, w0:w1, :], op=ALU.mult)
+            nc.gpsimd.tensor_copy(out=k_rot[:, :, 0:plain], in_=pooled[:, :, 0:plain])
+            engine.tensor_tensor(
+                out=pairs_out, in0=pairs_in,
+                in1=cos[:, w0:w1, :].unsqueeze(3).to_broadcast([P, BATCH_TARGETS, PAIRS, 2]), op=ALU.mult,
+            )
+            engine.tensor_tensor(out=cross[:], in0=pairs_in[:, :, :, ::-1], in1=sin_pairs[:, w0:w1], op=ALU.mult)
             engine.tensor_tensor(out=pairs_out, in0=pairs_out, in1=cross[:], op=ALU.add)
             nc.sync.dma_start(out=krot_runs[:, w0:w1, :], in_=k_rot[:])
 
@@ -356,44 +361,43 @@ def tile_deepseekv4attention_pa_t_kernel(
         def live(chunk):
             return 0 <= chunk < N_CHUNKS
 
-        for a in range(-3, N_CHUNKS + 8):
-            if live(a - 6):
-                sums_out(a - 6)
-            if a - 3 == N_CHUNKS:
-                logarithm(0, LAST_BATCH)
-            if live(a - 3):
-                stabilise(a - 3)
-            if live(a + 1):
-                multiply(a + 1, 0, psum_g, gate_banks)
-            if live(a - 4):
-                multiply(a - 4, 1, psum_k, kv_banks)
-            if live(a + 1):
-                offset(a + 1)
-            if live(a):
-                top_first(a)
-            if live(a + 3):
-                flip(a + 3, 0)
-            if live(a - 4):
-                weigh(a - 4, 0)
-            if live(a - 3):
-                exponent(a - 3)
-            if live(a + 3):
-                flip(a + 3, 1)
-            if live(a + 2):
-                quantise(a + 2)
-            if live(a - 4):
-                weigh(a - 4, 1)
-            if live(a - 2):
-                exchange(a - 2)
-                peak_of(a - 2)
+        for a in range(0, N_CHUNKS + 8):
+            if live(a - 7):
+                sums_out(a - 7)
             if live(a - 5):
-                slot_sums(a - 5)
+                stabilise(a - 5)
+            if a == 2:
+                flip_offset()
+            if live(a - 2):
+                multiply(a - 2, 0, gate_banks)
+                offset(a - 2)
+            if live(a - 5):
+                exponent(a - 5)
+            if a - 5 == N_CHUNKS:
+                logarithm(0, LAST_BATCH)
+            if live(a - 1):
+                quantise(a - 1)
             if live(a):
-                top_second(a)
+                flip(a)
+            if a == TRIG_ROUND:
+                trigonometry()
+            if live(a - 2):
+                top_first(a - 2)
+            if live(a - 5):
+                multiply(a - 5, 1, kv_banks)
+                weigh(a - 5, 0)
+                weigh(a - 5, 1)
+            if live(a - 4):
+                exchange(a - 4)
+                peak_of(a - 4)
+            if live(a - 2):
+                top_second(a - 2)
+            if live(a - 6):
+                slot_sums(a - 6)
             if batch_done_by(a - 7) is not None:
                 fold(batch_done_by(a - 7))
-            if live(a + 3 + LOADS_AHEAD):
-                load(a + 3 + LOADS_AHEAD)
+            if live(a + LOADS_AHEAD):
+                load(a + LOADS_AHEAD)
 
         logarithm(LAST_BATCH, RUN_WINDOWS)
         invert(LAST_BATCH)

@@ -34,8 +34,8 @@ N_CHUNKS = 1 + RUN_WINDOWS // CHUNK_WINDOWS
 BATCH_TARGETS = 8
 LAST_BATCH = RUN_WINDOWS - BATCH_TARGETS
 LOADS_AHEAD = 3
-VECTOR_HELPS = 3
-TRIG_ROUND = 1
+VECTOR_HELPS = 6
+TRIG_ROUND = 3
 NO_SLOT = -(2.0**100)
 ROUND = 1.5 * 2.0**23
 
@@ -54,8 +54,8 @@ def tile_deepseekv4attention_pa_t_kernel(
         const = ctx.enter_context(tc.tile_pool(name="const", bufs=1))
         x_pool = ctx.enter_context(tc.tile_pool(name="x", bufs=4))
         grouped_pool = ctx.enter_context(tc.tile_pool(name="grouped", bufs=2))
-        code_pool = ctx.enter_context(tc.tile_pool(name="codes", bufs=5))
-        t_pool = ctx.enter_context(tc.tile_pool(name="gates", bufs=5))
+        code_pool = ctx.enter_context(tc.tile_pool(name="codes", bufs=6))
+        t_pool = ctx.enter_context(tc.tile_pool(name="gates", bufs=6))
         y_pool = ctx.enter_context(tc.tile_pool(name="products", bufs=2))
         m_pool = ctx.enter_context(tc.tile_pool(name="maxima", bufs=2))
         o_pool = ctx.enter_context(tc.tile_pool(name="outs", bufs=4))
@@ -121,19 +121,19 @@ def tile_deepseekv4attention_pa_t_kernel(
             per_window = RATIO * THETA ** (-j / PAIRS) / (2.0 * math.pi)
             per_run = RUN_WINDOWS * per_window
             per_run = per_run - round(per_run)
-            nc.vector.tensor_scalar(
+            nc.gpsimd.tensor_scalar(
                 out=run_turns[:, j : j + 1], in0=run_f[:], scalar1=per_run, scalar2=None, op0=ALU.mult
             )
-            nc.vector.tensor_scalar(
+            nc.gpsimd.tensor_scalar(
                 out=turns[:, 0, :, j], in0=win_f[:], scalar1=per_window, scalar2=run_turns[:, j : j + 1],
                 op0=ALU.mult, op1=ALU.add,
             )
-        nc.vector.tensor_scalar(out=turns[:, 1], in0=turns[:, 0], scalar1=0.25, scalar2=None, op0=ALU.add)
+        nc.gpsimd.tensor_scalar(out=turns[:, 1], in0=turns[:, 0], scalar1=0.25, scalar2=None, op0=ALU.add)
         whole = y_pool.tile([P, 2, RUN_WINDOWS, PAIRS], F32, name="products")
-        nc.vector.tensor_scalar(
+        nc.gpsimd.tensor_scalar(
             out=whole[:], in0=turns[:], scalar1=ROUND, scalar2=ROUND, op0=ALU.add, op1=ALU.subtract
         )
-        nc.vector.tensor_tensor(out=turns[:], in0=turns[:], in1=whole[:], op=ALU.subtract)
+        nc.gpsimd.tensor_tensor(out=turns[:], in0=turns[:], in1=whole[:], op=ALU.subtract)
         cos = const.tile([P, RUN_WINDOWS, PAIRS], F32)
         sin_pairs = const.tile([P, RUN_WINDOWS, PAIRS, 2], F32)
 
@@ -315,9 +315,9 @@ def tile_deepseekv4attention_pa_t_kernel(
                 in_=sum_banks[chunk][:, 0:n_win].rearrange("p w k c -> p (w k c)"),
             )
 
-        def fold(w0):
-            here = totals[:, w0 + 1 : w0 + 1 + BATCH_TARGETS, :, FEAT:COLS]
-            nc.vector.tensor_tensor(out=here, in0=totals[:, w0 : w0 + BATCH_TARGETS, :, 0:FEAT], in1=here, op=ALU.add)
+        def fold(w0, w1, engine):
+            here = totals[:, w0 + 1 : w1 + 1, :, FEAT:COLS]
+            engine.tensor_tensor(out=here, in0=totals[:, w0:w1, :, 0:FEAT], in1=here, op=ALU.add)
 
         def logarithm(w0, w1):
             nc.scalar.activation(out=inverse[:, w0:w1, :], in_=totals[:, w0 + 1 : w1 + 1, 0, FEAT:COLS], func=ACT.Ln)
@@ -343,7 +343,7 @@ def tile_deepseekv4attention_pa_t_kernel(
             plain = FEAT - ROPE
             pairs_in = pooled[:, :, plain:FEAT].rearrange("p w (j e) -> p w j e", e=2)
             pairs_out = k_rot[:, :, plain:FEAT].rearrange("p w (j e) -> p w j e", e=2)
-            nc.gpsimd.tensor_copy(out=k_rot[:, :, 0:plain], in_=pooled[:, :, 0:plain])
+            nc.scalar.copy(out=k_rot[:, :, 0:plain], in_=pooled[:, :, 0:plain])
             engine.tensor_tensor(
                 out=pairs_out, in0=pairs_in,
                 in1=cos[:, w0:w1, :].unsqueeze(3).to_broadcast([P, BATCH_TARGETS, PAIRS, 2]), op=ALU.mult,
@@ -361,9 +361,9 @@ def tile_deepseekv4attention_pa_t_kernel(
         def live(chunk):
             return 0 <= chunk < N_CHUNKS
 
-        for a in range(0, N_CHUNKS + 8):
-            if live(a - 7):
-                sums_out(a - 7)
+        for a in range(0, N_CHUNKS + 9):
+            if live(a - 8):
+                sums_out(a - 8)
             if live(a - 5):
                 stabilise(a - 5)
             if a == 2:
@@ -373,8 +373,9 @@ def tile_deepseekv4attention_pa_t_kernel(
                 offset(a - 2)
             if live(a - 5):
                 exponent(a - 5)
-            if a - 5 == N_CHUNKS:
-                logarithm(0, LAST_BATCH)
+            if N_CHUNKS <= a - 5 < N_CHUNKS + 3:
+                w0 = BATCH_TARGETS * (a - 5 - N_CHUNKS)
+                logarithm(w0, w0 + BATCH_TARGETS)
             if live(a - 1):
                 quantise(a - 1)
             if live(a):
@@ -383,19 +384,23 @@ def tile_deepseekv4attention_pa_t_kernel(
                 trigonometry()
             if live(a - 2):
                 top_first(a - 2)
-            if live(a - 5):
-                multiply(a - 5, 1, kv_banks)
-                weigh(a - 5, 0)
-                weigh(a - 5, 1)
+            if live(a - 6):
+                multiply(a - 6, 1, kv_banks)
+                weigh(a - 6, 0)
+                weigh(a - 6, 1)
             if live(a - 4):
                 exchange(a - 4)
                 peak_of(a - 4)
             if live(a - 2):
                 top_second(a - 2)
-            if live(a - 6):
-                slot_sums(a - 6)
-            if batch_done_by(a - 7) is not None:
-                fold(batch_done_by(a - 7))
+            if live(a - 7):
+                slot_sums(a - 7)
+            if batch_done_by(a - 8) is not None and batch_done_by(a - 8) < LAST_BATCH:
+                fold(batch_done_by(a - 8), batch_done_by(a - 8) + BATCH_TARGETS, nc.gpsimd)
+            if a - 8 == N_CHUNKS - 2:
+                fold(LAST_BATCH, RUN_WINDOWS - CHUNK_WINDOWS, nc.vector)
+            if a - 8 == N_CHUNKS - 1:
+                fold(RUN_WINDOWS - CHUNK_WINDOWS, RUN_WINDOWS, nc.vector)
             if live(a + LOADS_AHEAD):
                 load(a + LOADS_AHEAD)
 
@@ -406,7 +411,8 @@ def tile_deepseekv4attention_pa_t_kernel(
         divide(LAST_BATCH)
         divide(0)
         rotate(0, nc.gpsimd)
+        divide(BATCH_TARGETS)
+        rotate(BATCH_TARGETS, nc.gpsimd)
         rotate(LAST_BATCH, nc.vector)
-        for w0 in range(BATCH_TARGETS, LAST_BATCH, BATCH_TARGETS):
-            divide(w0)
-            rotate(w0, nc.vector)
+        divide(2 * BATCH_TARGETS)
+        rotate(2 * BATCH_TARGETS, nc.vector)

@@ -34,8 +34,8 @@ N_CHUNKS = 1 + RUN_WINDOWS // CHUNK_WINDOWS
 BATCH_TARGETS = 8
 LAST_BATCH = RUN_WINDOWS - BATCH_TARGETS
 LOADS_AHEAD = 3
-VECTOR_HELPS = 6
-TRIG_ROUND = 3
+VECTOR_HELPS = 4
+TRIG_ROUND = 0
 NO_SLOT = -(2.0**100)
 ROUND = 1.5 * 2.0**23
 
@@ -93,17 +93,15 @@ def tile_deepseekv4attention_pa_t_kernel(
         for chunk in range(1, LOADS_AHEAD):
             load(chunk)
 
+        warm = const.tile([P, 1], F32)
+        nc.vector.memset(warm[:], 0.0)
+        nc.scalar.activation(out=warm[:], in_=warm[:], func=ACT.Sin)
+
         ident = const.tile([P, P], F32)
         masks.make_identity(nc, ident[:])
         from_left = const.tile([P, P], F32)
         nc.vector.tensor_copy(out=from_left[:, 1:P], in_=ident[:, 0 : P - 1])
         nc.vector.tensor_copy(out=from_left[:, 0:1], in_=ident[:, P - 1 : P])
-        upper_down = const.tile([P, P], BF16)
-        lower_up = const.tile([P, P], BF16)
-        nc.vector.memset(upper_down[:], 0.0)
-        nc.vector.memset(lower_up[:], 0.0)
-        nc.vector.tensor_copy(out=upper_down[:, 0:FEAT], in_=ident[:, FEAT:COLS])
-        nc.vector.tensor_copy(out=lower_up[:, FEAT:COLS], in_=ident[:, 0:FEAT])
 
         win_i = const.tile([P, RUN_WINDOWS], I32)
         nc.gpsimd.iota(win_i[:], pattern=[[1, RUN_WINDOWS]], base=0, channel_multiplier=0)
@@ -121,26 +119,36 @@ def tile_deepseekv4attention_pa_t_kernel(
             per_window = RATIO * THETA ** (-j / PAIRS) / (2.0 * math.pi)
             per_run = RUN_WINDOWS * per_window
             per_run = per_run - round(per_run)
-            nc.gpsimd.tensor_scalar(
+            nc.vector.tensor_scalar(
                 out=run_turns[:, j : j + 1], in0=run_f[:], scalar1=per_run, scalar2=None, op0=ALU.mult
             )
-            nc.gpsimd.tensor_scalar(
+            nc.vector.tensor_scalar(
                 out=turns[:, 0, :, j], in0=win_f[:], scalar1=per_window, scalar2=run_turns[:, j : j + 1],
                 op0=ALU.mult, op1=ALU.add,
             )
-        nc.gpsimd.tensor_scalar(out=turns[:, 1], in0=turns[:, 0], scalar1=0.25, scalar2=None, op0=ALU.add)
+        nc.vector.tensor_scalar(out=turns[:, 1], in0=turns[:, 0], scalar1=0.25, scalar2=None, op0=ALU.add)
         whole = y_pool.tile([P, 2, RUN_WINDOWS, PAIRS], F32, name="products")
-        nc.gpsimd.tensor_scalar(
+        nc.vector.tensor_scalar(
             out=whole[:], in0=turns[:], scalar1=ROUND, scalar2=ROUND, op0=ALU.add, op1=ALU.subtract
         )
-        nc.gpsimd.tensor_tensor(out=turns[:], in0=turns[:], in1=whole[:], op=ALU.subtract)
-        cos = const.tile([P, RUN_WINDOWS, PAIRS], F32)
+        nc.vector.tensor_tensor(out=turns[:], in0=turns[:], in1=whole[:], op=ALU.subtract)
+        cos_pairs = const.tile([P, RUN_WINDOWS, PAIRS, 2], F32)
         sin_pairs = const.tile([P, RUN_WINDOWS, PAIRS, 2], F32)
 
         def trigonometry():
-            nc.scalar.activation(out=cos[:], in_=turns[:, 1], func=ACT.Sin, scale=2.0 * math.pi)
+            nc.scalar.activation(
+                out=cos_pairs[:], in_=turns[:, 1].unsqueeze(3).to_broadcast([P, RUN_WINDOWS, PAIRS, 2]),
+                func=ACT.Sin, scale=2.0 * math.pi,
+            )
             nc.scalar.activation(out=sin_pairs[:, :, :, 0], in_=turns[:, 0], func=ACT.Sin, scale=-2.0 * math.pi)
             nc.scalar.activation(out=sin_pairs[:, :, :, 1], in_=turns[:, 0], func=ACT.Sin, scale=2.0 * math.pi)
+
+        upper_down = const.tile([P, P], BF16)
+        lower_up = const.tile([P, P], BF16)
+        nc.vector.memset(upper_down[:], 0.0)
+        nc.vector.memset(lower_up[:], 0.0)
+        nc.vector.tensor_copy(out=upper_down[:, 0:FEAT], in_=ident[:, FEAT:COLS])
+        nc.vector.tensor_copy(out=lower_up[:, FEAT:COLS], in_=ident[:, 0:FEAT])
 
         ape_square = const.tile([P, P], F32)
         nc.vector.memset(ape_square[:], 0.0)
@@ -188,7 +196,7 @@ def tile_deepseekv4attention_pa_t_kernel(
                         nc.tensor.transpose(flipped[:, t, h, :], x_words[:, base + h : base + WORDS : 2], order[:])
                 first = ((2 * pair) % RATIO) * n_win + (2 * pair) // RATIO
                 out = blocks[:, first : first + n_win + 1 : n_win]
-                if chunk < VECTOR_HELPS and pair % 2 == 1:
+                if 0 < chunk < VECTOR_HELPS and pair % 2 == 1:
                     nc.vector.tensor_copy(out=out, in_=flipped[:].rearrange("p t h n -> p t n h"))
                 else:
                     nc.scalar.copy(out=out, in_=flipped[:].rearrange("p t h n -> p t n h"))
@@ -237,7 +245,7 @@ def tile_deepseekv4attention_pa_t_kernel(
         def top_first(chunk):
             width = width_of(chunk)
             gates = gate_tiles[chunk]
-            half_top = m_pool.tile([P, 2, WIDE], F32)
+            half_top = m_pool.tile([P, 2, WIDE], BF16)
             nc.vector.tensor_tensor(
                 out=half_top[:, :, 0:width], in0=gates[:, 0:2, 0:width], in1=gates[:, 2:4, 0:width], op=ALU.max
             )
@@ -335,21 +343,26 @@ def tile_deepseekv4attention_pa_t_kernel(
             nc.sync.dma_start(out=pooled_runs[:, w0 : w0 + BATCH_TARGETS, :], in_=pooled[:])
             batch_tiles[w0] = pooled
 
-        def rotate(w0, engine):
+        def rotate(w0):
             w1 = w0 + BATCH_TARGETS
             pooled = batch_tiles[w0]
             k_rot = o_pool.tile([P, BATCH_TARGETS, FEAT], F32)
-            cross = o_pool.tile([P, BATCH_TARGETS, PAIRS, 2], F32)
+            swapped = o_pool.tile([P, BATCH_TARGETS, PAIRS, 2], F32)
             plain = FEAT - ROPE
-            pairs_in = pooled[:, :, plain:FEAT].rearrange("p w (j e) -> p w j e", e=2)
-            pairs_out = k_rot[:, :, plain:FEAT].rearrange("p w (j e) -> p w j e", e=2)
+            nc.scalar.copy(out=swapped[:], in_=pooled[:, :, plain:FEAT].rearrange("p w (j e) -> p w j e", e=2)[:, :, :, ::-1])
             nc.scalar.copy(out=k_rot[:, :, 0:plain], in_=pooled[:, :, 0:plain])
-            engine.tensor_tensor(
-                out=pairs_out, in0=pairs_in,
-                in1=cos[:, w0:w1, :].unsqueeze(3).to_broadcast([P, BATCH_TARGETS, PAIRS, 2]), op=ALU.mult,
+            by_row = "p w j e -> p w (j e)"
+            nc.vector.tensor_tensor(
+                out=k_rot[:, :, plain:FEAT], in0=pooled[:, :, plain:FEAT],
+                in1=cos_pairs[:, w0:w1].rearrange(by_row), op=ALU.mult,
             )
-            engine.tensor_tensor(out=cross[:], in0=pairs_in[:, :, :, ::-1], in1=sin_pairs[:, w0:w1], op=ALU.mult)
-            engine.tensor_tensor(out=pairs_out, in0=pairs_out, in1=cross[:], op=ALU.add)
+            nc.vector.tensor_tensor(
+                out=swapped[:].rearrange(by_row), in0=swapped[:].rearrange(by_row),
+                in1=sin_pairs[:, w0:w1].rearrange(by_row), op=ALU.mult,
+            )
+            nc.vector.tensor_tensor(
+                out=k_rot[:, :, plain:FEAT], in0=k_rot[:, :, plain:FEAT], in1=swapped[:].rearrange(by_row), op=ALU.add
+            )
             nc.sync.dma_start(out=krot_runs[:, w0:w1, :], in_=k_rot[:])
 
         def batch_done_by(chunk):
@@ -396,7 +409,7 @@ def tile_deepseekv4attention_pa_t_kernel(
             if live(a - 7):
                 slot_sums(a - 7)
             if batch_done_by(a - 8) is not None and batch_done_by(a - 8) < LAST_BATCH:
-                fold(batch_done_by(a - 8), batch_done_by(a - 8) + BATCH_TARGETS, nc.gpsimd)
+                fold(batch_done_by(a - 8), batch_done_by(a - 8) + BATCH_TARGETS, nc.vector)
             if a - 8 == N_CHUNKS - 2:
                 fold(LAST_BATCH, RUN_WINDOWS - CHUNK_WINDOWS, nc.vector)
             if a - 8 == N_CHUNKS - 1:
@@ -408,11 +421,6 @@ def tile_deepseekv4attention_pa_t_kernel(
         invert(LAST_BATCH)
         for w0 in range(0, LAST_BATCH, BATCH_TARGETS):
             invert(w0)
-        divide(LAST_BATCH)
-        divide(0)
-        rotate(0, nc.gpsimd)
-        divide(BATCH_TARGETS)
-        rotate(BATCH_TARGETS, nc.gpsimd)
-        rotate(LAST_BATCH, nc.vector)
-        divide(2 * BATCH_TARGETS)
-        rotate(2 * BATCH_TARGETS, nc.vector)
+        for w0 in (LAST_BATCH, 0, BATCH_TARGETS, 2 * BATCH_TARGETS):
+            divide(w0)
+            rotate(w0)

@@ -177,6 +177,7 @@ def tile_deepseekv4attention_pa_t_kernel(
         product_tiles = {}
         sum_banks = {}
         batch_tiles = {}
+        rot_tiles = {}
 
         def width_of(chunk):
             return P * len(windows_of(chunk))
@@ -263,14 +264,14 @@ def tile_deepseekv4attention_pa_t_kernel(
 
         def exchange(chunk):
             width = width_of(chunk)
-            partner = psum_t.tile([P, WIDE], F32, tag="ring")
+            partner = psum_t.tile([P, WIDE], BF16, tag="ring")
             nc.tensor.matmul(out=partner[:, 0:width], lhsT=upper_down[:], rhs=own_top(chunk, 1), start=True, stop=False)
             nc.tensor.matmul(out=partner[:, 0:width], lhsT=lower_up[:], rhs=own_top(chunk, -1), start=False, stop=True)
             partner_tiles[chunk] = partner
 
         def peak_of(chunk):
             width = width_of(chunk)
-            peak = m_pool.tile([P, WIDE], F32)
+            peak = m_pool.tile([P, WIDE], BF16)
             nc.vector.tensor_tensor(
                 out=peak[:, 0:width], in0=partner_tiles[chunk][:, 0:width], in1=own_top(chunk), op=ALU.max
             )
@@ -343,27 +344,34 @@ def tile_deepseekv4attention_pa_t_kernel(
             nc.sync.dma_start(out=pooled_runs[:, w0 : w0 + BATCH_TARGETS, :], in_=pooled[:])
             batch_tiles[w0] = pooled
 
-        def rotate(w0):
+        def rotate(w0, step):
             w1 = w0 + BATCH_TARGETS
-            pooled = batch_tiles[w0]
-            k_rot = o_pool.tile([P, BATCH_TARGETS, FEAT], F32)
-            swapped = o_pool.tile([P, BATCH_TARGETS, PAIRS, 2], F32)
             plain = FEAT - ROPE
-            nc.scalar.copy(out=swapped[:], in_=pooled[:, :, plain:FEAT].rearrange("p w (j e) -> p w j e", e=2)[:, :, :, ::-1])
-            nc.scalar.copy(out=k_rot[:, :, 0:plain], in_=pooled[:, :, 0:plain])
             by_row = "p w j e -> p w (j e)"
-            nc.vector.tensor_tensor(
-                out=k_rot[:, :, plain:FEAT], in0=pooled[:, :, plain:FEAT],
-                in1=cos_pairs[:, w0:w1].rearrange(by_row), op=ALU.mult,
-            )
-            nc.vector.tensor_tensor(
-                out=swapped[:].rearrange(by_row), in0=swapped[:].rearrange(by_row),
-                in1=sin_pairs[:, w0:w1].rearrange(by_row), op=ALU.mult,
-            )
-            nc.vector.tensor_tensor(
-                out=k_rot[:, :, plain:FEAT], in0=k_rot[:, :, plain:FEAT], in1=swapped[:].rearrange(by_row), op=ALU.add
-            )
-            nc.sync.dma_start(out=krot_runs[:, w0:w1, :], in_=k_rot[:])
+            if step == 0:
+                pooled = batch_tiles[w0]
+                k_rot = o_pool.tile([P, BATCH_TARGETS, FEAT], F32)
+                swapped = o_pool.tile([P, BATCH_TARGETS, PAIRS, 2], F32)
+                nc.scalar.copy(
+                    out=swapped[:], in_=pooled[:, :, plain:FEAT].rearrange("p w (j e) -> p w j e", e=2)[:, :, :, ::-1]
+                )
+                nc.scalar.copy(out=k_rot[:, :, 0:plain], in_=pooled[:, :, 0:plain])
+                nc.vector.tensor_tensor(
+                    out=k_rot[:, :, plain:FEAT], in0=pooled[:, :, plain:FEAT],
+                    in1=cos_pairs[:, w0:w1].rearrange(by_row), op=ALU.mult,
+                )
+                rot_tiles[w0] = (k_rot, swapped)
+            k_rot, swapped = rot_tiles[w0]
+            if step == 1:
+                nc.vector.tensor_tensor(
+                    out=swapped[:].rearrange(by_row), in0=swapped[:].rearrange(by_row),
+                    in1=sin_pairs[:, w0:w1].rearrange(by_row), op=ALU.mult,
+                )
+            if step == 2:
+                nc.vector.tensor_tensor(
+                    out=k_rot[:, :, plain:FEAT], in0=k_rot[:, :, plain:FEAT], in1=swapped[:].rearrange(by_row), op=ALU.add
+                )
+                nc.sync.dma_start(out=krot_runs[:, w0:w1, :], in_=k_rot[:])
 
         def batch_done_by(chunk):
             if not 0 <= chunk < N_CHUNKS:
@@ -421,6 +429,9 @@ def tile_deepseekv4attention_pa_t_kernel(
         invert(LAST_BATCH)
         for w0 in range(0, LAST_BATCH, BATCH_TARGETS):
             invert(w0)
-        for w0 in (LAST_BATCH, 0, BATCH_TARGETS, 2 * BATCH_TARGETS):
-            divide(w0)
-            rotate(w0)
+        for pair in ((LAST_BATCH, 0), (BATCH_TARGETS, 2 * BATCH_TARGETS)):
+            for w0 in pair:
+                divide(w0)
+            for step in range(3):
+                for w0 in pair:
+                    rotate(w0, step)

@@ -163,7 +163,8 @@ def tile_deepseekv4attention_pa_t_kernel(
         top = const.tile([P, RUN_WINDOWS + 3, P], BF16)
         nc.vector.memset(top[:, 0, :], NO_SLOT)
         nc.vector.memset(top[:, RUN_WINDOWS + 2, :], NO_SLOT)
-        totals = const.tile([P, RUN_WINDOWS + 1, 2, COLS], F32)
+        first_half = const.tile([P, RUN_WINDOWS + 1, 2, FEAT], F32)
+        totals = const.tile([P, RUN_WINDOWS, 2, FEAT], F32)
         inverse = const.tile([P, RUN_WINDOWS, FEAT], F32)
 
         grouped_tiles = {}
@@ -318,18 +319,20 @@ def tile_deepseekv4attention_pa_t_kernel(
 
         def sums_out(chunk):
             n_win = len(windows_of(chunk))
-            first = windows_of(chunk)[0] + 1
-            nc.scalar.copy(
-                out=totals[:, first : first + n_win].rearrange("p w k c -> p (w k c)"),
-                in_=sum_banks[chunk][:, 0:n_win].rearrange("p w k c -> p (w k c)"),
-            )
+            first = windows_of(chunk)[0]
+            nc.scalar.copy(out=first_half[:, first + 1 : first + 1 + n_win], in_=sum_banks[chunk][:, 0:n_win, :, 0:FEAT])
 
-        def fold(w0, w1, engine):
-            here = totals[:, w0 + 1 : w1 + 1, :, FEAT:COLS]
-            engine.tensor_tensor(out=here, in0=totals[:, w0:w1, :, 0:FEAT], in1=here, op=ALU.add)
+        def fold(chunk):
+            n_win = len(windows_of(chunk))
+            first = windows_of(chunk)[0]
+            if chunk > 0:
+                nc.vector.tensor_tensor(
+                    out=totals[:, first : first + n_win], in0=sum_banks[chunk][:, 0:n_win, :, FEAT:COLS],
+                    in1=first_half[:, first : first + n_win], op=ALU.add,
+                )
 
         def logarithm(w0, w1):
-            nc.scalar.activation(out=inverse[:, w0:w1, :], in_=totals[:, w0 + 1 : w1 + 1, 0, FEAT:COLS], func=ACT.Ln)
+            nc.scalar.activation(out=inverse[:, w0:w1, :], in_=totals[:, w0:w1, 0, :], func=ACT.Ln)
 
         def invert(w0):
             rows = inverse[:, w0 : w0 + BATCH_TARGETS, :]
@@ -338,7 +341,7 @@ def tile_deepseekv4attention_pa_t_kernel(
         def divide(w0):
             pooled = o_pool.tile([P, BATCH_TARGETS, FEAT], F32)
             nc.vector.tensor_tensor(
-                out=pooled[:], in0=totals[:, w0 + 1 : w0 + 1 + BATCH_TARGETS, 1, FEAT:COLS],
+                out=pooled[:], in0=totals[:, w0 : w0 + BATCH_TARGETS, 1, :],
                 in1=inverse[:, w0 : w0 + BATCH_TARGETS, :], op=ALU.mult,
             )
             nc.sync.dma_start(out=pooled_runs[:, w0 : w0 + BATCH_TARGETS, :], in_=pooled[:])
@@ -399,6 +402,8 @@ def tile_deepseekv4attention_pa_t_kernel(
                 logarithm(w0, w0 + BATCH_TARGETS)
             if live(a - 1):
                 quantise(a - 1)
+            if live(a - 8):
+                fold(a - 8)
             if live(a):
                 flip(a)
             if a == TRIG_ROUND:
@@ -416,12 +421,6 @@ def tile_deepseekv4attention_pa_t_kernel(
                 top_second(a - 2)
             if live(a - 7):
                 slot_sums(a - 7)
-            if batch_done_by(a - 8) is not None and batch_done_by(a - 8) < LAST_BATCH:
-                fold(batch_done_by(a - 8), batch_done_by(a - 8) + BATCH_TARGETS, nc.vector)
-            if a - 8 == N_CHUNKS - 2:
-                fold(LAST_BATCH, RUN_WINDOWS - CHUNK_WINDOWS, nc.vector)
-            if a - 8 == N_CHUNKS - 1:
-                fold(RUN_WINDOWS - CHUNK_WINDOWS, RUN_WINDOWS, nc.vector)
             if live(a + LOADS_AHEAD):
                 load(a + LOADS_AHEAD)
 

@@ -34,8 +34,9 @@ N_CHUNKS = 1 + RUN_WINDOWS // CHUNK_WINDOWS
 BATCH_TARGETS = 8
 LAST_BATCH = RUN_WINDOWS - BATCH_TARGETS
 LOADS_AHEAD = 3
+SPLIT_LOADS = 2
 VECTOR_HELPS = 4
-TRIG_ROUND = 0
+TRIG_ROUND = 1
 NO_SLOT = -(2.0**100)
 ROUND = 1.5 * 2.0**23
 
@@ -74,7 +75,12 @@ def tile_deepseekv4attention_pa_t_kernel(
             n_tok = RATIO * len(windows_of(chunk))
             first_token = RUN_TOKENS - RATIO if chunk == 0 else RATIO * windows_of(chunk)[0]
             x_sb = x_pool.tile([P, CHUNK_TOKENS, HID], BF16)
-            nc.sync.dma_start(out=x_sb[:, 0:n_tok, :], in_=x_runs[:, first_token : first_token + n_tok, :])
+            pieces = 2 if chunk < SPLIT_LOADS else 1
+            step = n_tok // pieces
+            for t0 in range(0, n_tok, step):
+                nc.sync.dma_start(
+                    out=x_sb[:, t0 : t0 + step, :], in_=x_runs[:, first_token + t0 : first_token + t0 + step, :]
+                )
             x_tiles[chunk] = x_sb
 
         w_words = const.tile([P, 2, 2 * COLS], U8, align_bytes=64)
@@ -95,6 +101,8 @@ def tile_deepseekv4attention_pa_t_kernel(
 
         warm = const.tile([P, 1], F32)
         nc.vector.memset(warm[:], 0.0)
+        no_slot = const.tile([P, 1], F32)
+        nc.vector.memset(no_slot[:], NO_SLOT)
         nc.scalar.activation(out=warm[:], in_=warm[:], func=ACT.Sin)
 
         ident = const.tile([P, P], F32)
@@ -142,6 +150,7 @@ def tile_deepseekv4attention_pa_t_kernel(
             )
             nc.scalar.activation(out=sin_pairs[:, :, :, 0], in_=turns[:, 0], func=ACT.Sin, scale=-2.0 * math.pi)
             nc.scalar.activation(out=sin_pairs[:, :, :, 1], in_=turns[:, 0], func=ACT.Sin, scale=2.0 * math.pi)
+            nc.scalar.activation(out=warm[:], in_=warm[:], func=ACT.Exp)
 
         upper_down = const.tile([P, P], BF16)
         lower_up = const.tile([P, P], BF16)
@@ -241,7 +250,8 @@ def tile_deepseekv4attention_pa_t_kernel(
                     func=ACT.Identity, bias=ape_cols[:, r : r + 1], scale=1.0,
                 )
             if chunk == 0:
-                nc.vector.memset(gates[:, :, 0:P:RUNS_PER_SEQ], NO_SLOT)
+                starts = gates[:, :, 0:P:RUNS_PER_SEQ]
+                nc.scalar.activation(out=starts, in_=starts, func=ACT.Identity, scale=0.0, bias=no_slot[:, 0:1])
             gate_tiles[chunk] = gates
 
         def top_first(chunk):

@@ -37,6 +37,7 @@ LOADS_AHEAD = 3
 SPLIT_LOADS = 2
 VECTOR_HELPS = 4
 TRIG_ROUND = 1
+LATE_CHUNKS = 3
 NO_SLOT = -(2.0**100)
 ROUND = 1.5 * 2.0**23
 
@@ -330,7 +331,10 @@ def tile_deepseekv4attention_pa_t_kernel(
         def sums_out(chunk):
             n_win = len(windows_of(chunk))
             first = windows_of(chunk)[0]
-            nc.scalar.copy(out=first_half[:, first + 1 : first + 1 + n_win], in_=sum_banks[chunk][:, 0:n_win, :, 0:FEAT])
+            if chunk < N_CHUNKS - LATE_CHUNKS:
+                nc.scalar.copy(out=first_half[:, first + 1 : first + 1 + n_win], in_=sum_banks[chunk][:, 0:n_win, :, 0:FEAT])
+            else:
+                nc.vector.tensor_copy(out=first_half[:, first + 1 : first + 1 + n_win], in_=sum_banks[chunk][:, 0:n_win, :, 0:FEAT])
 
         def fold(chunk):
             n_win = len(windows_of(chunk))
@@ -344,9 +348,12 @@ def tile_deepseekv4attention_pa_t_kernel(
         def logarithm(w0, w1):
             nc.scalar.activation(out=inverse[:, w0:w1, :], in_=totals[:, w0:w1, 0, :], func=ACT.Ln)
 
-        def invert(w0):
-            rows = inverse[:, w0 : w0 + BATCH_TARGETS, :]
+        def invert(w0, n=BATCH_TARGETS):
+            rows = inverse[:, w0 : w0 + n, :]
             nc.scalar.activation(out=rows, in_=rows, func=ACT.Exp, scale=-1.0)
+
+        def invert_exactly(w0, w1):
+            nc.vector.reciprocal(out=inverse[:, w0:w1, :], in_=totals[:, w0:w1, 0, :])
 
         def divide(w0):
             pooled = o_pool.tile([P, BATCH_TARGETS, FEAT], F32)
@@ -407,13 +414,14 @@ def tile_deepseekv4attention_pa_t_kernel(
                 offset(a - 2)
             if live(a - 5):
                 exponent(a - 5)
-            if N_CHUNKS <= a - 5 < N_CHUNKS + 3:
-                w0 = BATCH_TARGETS * (a - 5 - N_CHUNKS)
-                logarithm(w0, w0 + BATCH_TARGETS)
+            if a - 5 == N_CHUNKS:
+                logarithm(0, LAST_BATCH)
             if live(a - 1):
                 quantise(a - 1)
             if live(a - 8):
                 fold(a - 8)
+            if a - 8 == N_CHUNKS - 2:
+                logarithm(LAST_BATCH, RUN_WINDOWS - CHUNK_WINDOWS)
             if live(a):
                 flip(a)
             if a == TRIG_ROUND:
@@ -434,11 +442,11 @@ def tile_deepseekv4attention_pa_t_kernel(
             if live(a + LOADS_AHEAD):
                 load(a + LOADS_AHEAD)
 
-        logarithm(LAST_BATCH, RUN_WINDOWS)
-        invert(LAST_BATCH)
         for w0 in range(0, LAST_BATCH, BATCH_TARGETS):
             invert(w0)
-        for pair in ((LAST_BATCH, 0), (BATCH_TARGETS, 2 * BATCH_TARGETS)):
+        invert(LAST_BATCH, BATCH_TARGETS - CHUNK_WINDOWS)
+        invert_exactly(RUN_WINDOWS - CHUNK_WINDOWS, RUN_WINDOWS)
+        for pair in ((0, BATCH_TARGETS), (2 * BATCH_TARGETS, LAST_BATCH)):
             for w0 in pair:
                 divide(w0)
             for step in range(3):

@@ -89,6 +89,7 @@ def tile_deepseekv4attention_pa_t_kernel(
         ape_rows = const.tile([P, COLS], BF16)
         nc.vector.memset(w_plane[:].rearrange("p w c -> p (w c)").bitcast(I32), 0)
         load(0)
+        load(1)
         for i, (words, scales) in enumerate(((wgate_words, wgate_scales), (wkv_words, wkv_scales))):
             nc.sync.dma_start(out=w_words[:, i, :].bitcast(I32), in_=words[0].bitcast(I32))
             for quad in range(4):
@@ -97,7 +98,7 @@ def tile_deepseekv4attention_pa_t_kernel(
                     in_=scales[0, 4 * quad : 4 * quad + 4, :].bitcast(I32),
                 )
         nc.sync.dma_start(out=ape_rows[0:RATIO, :], in_=ape)
-        for chunk in range(1, LOADS_AHEAD):
+        for chunk in range(2, LOADS_AHEAD):
             load(chunk)
 
         warm = const.tile([P, 1], F32)
@@ -112,28 +113,18 @@ def tile_deepseekv4attention_pa_t_kernel(
         nc.vector.tensor_copy(out=from_left[:, 1:P], in_=ident[:, 0 : P - 1])
         nc.vector.tensor_copy(out=from_left[:, 0:1], in_=ident[:, P - 1 : P])
 
-        win_i = const.tile([P, RUN_WINDOWS], I32)
-        nc.gpsimd.iota(win_i[:], pattern=[[1, RUN_WINDOWS]], base=0, channel_multiplier=0)
-        part_i = const.tile([P, 1], I32)
-        nc.gpsimd.iota(part_i[:], pattern=[[0, 1]], base=0, channel_multiplier=1)
-        run_i = const.tile([P, 1], I32)
-        nc.vector.tensor_single_scalar(out=run_i[:], in_=part_i[:], scalar=RUNS_PER_SEQ - 1, op=ALU.bitwise_and)
-        win_f = const.tile([P, RUN_WINDOWS], F32)
-        nc.vector.tensor_copy(out=win_f[:], in_=win_i[:])
-        run_f = const.tile([P, 1], F32)
-        nc.vector.tensor_copy(out=run_f[:], in_=run_i[:])
-        run_turns = const.tile([P, PAIRS], F32)
+        window = const.tile([P, RUN_WINDOWS], F32)
+        for s in range(BATCH):
+            nc.gpsimd.iota(
+                window[s * RUNS_PER_SEQ : (s + 1) * RUNS_PER_SEQ, :], pattern=[[1, RUN_WINDOWS]], base=0,
+                channel_multiplier=RUN_WINDOWS, allow_small_or_imprecise_dtypes=True,
+            )
         turns = y_pool.tile([P, 2, RUN_WINDOWS, PAIRS], F32, name="products")
         for j in range(PAIRS):
             per_window = RATIO * THETA ** (-j / PAIRS) / (2.0 * math.pi)
-            per_run = RUN_WINDOWS * per_window
-            per_run = per_run - round(per_run)
+            per_window = per_window - round(per_window)
             nc.vector.tensor_scalar(
-                out=run_turns[:, j : j + 1], in0=run_f[:], scalar1=per_run, scalar2=None, op0=ALU.mult
-            )
-            nc.vector.tensor_scalar(
-                out=turns[:, 0, :, j], in0=win_f[:], scalar1=per_window, scalar2=run_turns[:, j : j + 1],
-                op0=ALU.mult, op1=ALU.add,
+                out=turns[:, 0, :, j], in0=window[:], scalar1=per_window, scalar2=None, op0=ALU.mult
             )
         nc.vector.tensor_scalar(out=turns[:, 1], in0=turns[:, 0], scalar1=0.25, scalar2=None, op0=ALU.add)
         whole = y_pool.tile([P, 2, RUN_WINDOWS, PAIRS], F32, name="products")
@@ -161,11 +152,11 @@ def tile_deepseekv4attention_pa_t_kernel(
         nc.vector.tensor_copy(out=lower_up[:, FEAT:COLS], in_=ident[:, 0:FEAT])
 
         ape_square = const.tile([P, P], F32)
-        nc.vector.memset(ape_square[:], 0.0)
-        nc.vector.tensor_copy(out=ape_square[0:RATIO, :], in_=ape_rows[0:RATIO, :])
+        nc.gpsimd.memset(ape_square[:], 0.0)
         ape_cols = const.tile([P, RATIO], F32)
 
         def flip_offset():
+            nc.vector.tensor_copy(out=ape_square[0:RATIO, :], in_=ape_rows[0:RATIO, :])
             ape_flipped = psum_t.tile([P, P], F32, tag="ring")
             nc.tensor.transpose(ape_flipped[:], ape_square[:], ident[:])
             nc.vector.tensor_copy(out=ape_cols[:], in_=ape_flipped[:, 0:RATIO])

@@ -31,10 +31,10 @@ CHUNK_WINDOWS = 2
 CHUNK_TOKENS = CHUNK_WINDOWS * RATIO
 WIDE = CHUNK_WINDOWS * P
 N_CHUNKS = 1 + RUN_WINDOWS // CHUNK_WINDOWS
+LAST = RUN_WINDOWS - 1
 BATCH_TARGETS = 8
 LAST_BATCH = RUN_WINDOWS - BATCH_TARGETS
 LOADS_AHEAD = 3
-SPLIT_LOADS = 2
 VECTOR_HELPS = 4
 TRIG_ROUND = 1
 LATE_CHUNKS = 3
@@ -67,21 +67,27 @@ def tile_deepseekv4attention_pa_t_kernel(
 
         def windows_of(chunk):
             if chunk == 0:
-                return [-1]
-            return [CHUNK_WINDOWS * (chunk - 1) + i for i in range(CHUNK_WINDOWS)]
+                return [LAST - 1]
+            if chunk == 1:
+                return [0, LAST]
+            return [CHUNK_WINDOWS * chunk - 3, CHUNK_WINDOWS * chunk - 2] if chunk < N_CHUNKS - 1 else [LAST - 2]
+
+        def unit_of(chunk):
+            return [LAST - 2, LAST - 1] if chunk == N_CHUNKS - 1 else windows_of(chunk)
 
         x_tiles = {}
 
         def load(chunk):
-            n_tok = RATIO * len(windows_of(chunk))
-            first_token = RUN_TOKENS - RATIO if chunk == 0 else RATIO * windows_of(chunk)[0]
+            windows = windows_of(chunk)
             x_sb = x_pool.tile([P, CHUNK_TOKENS, HID], BF16)
-            pieces = 2 if chunk < SPLIT_LOADS else 1
-            step = n_tok // pieces
-            for t0 in range(0, n_tok, step):
-                nc.sync.dma_start(
-                    out=x_sb[:, t0 : t0 + step, :], in_=x_runs[:, first_token + t0 : first_token + t0 + step, :]
-                )
+            if chunk == 0:
+                pieces = [(t, RATIO * windows[0] + t, RATIO // 2) for t in (0, RATIO // 2)]
+            elif chunk == 1:
+                pieces = [(RATIO * i, RATIO * w, RATIO) for i, w in enumerate(windows)]
+            else:
+                pieces = [(0, RATIO * windows[0], RATIO * len(windows))]
+            for place, token, count in pieces:
+                nc.sync.dma_start(out=x_sb[:, place : place + count, :], in_=x_runs[:, token : token + count, :])
             x_tiles[chunk] = x_sb
 
         w_words = const.tile([P, 2, 2 * COLS], U8, align_bytes=64)
@@ -103,15 +109,10 @@ def tile_deepseekv4attention_pa_t_kernel(
 
         warm = const.tile([P, 1], F32)
         nc.vector.memset(warm[:], 0.0)
-        no_slot = const.tile([P, 1], F32)
-        nc.vector.memset(no_slot[:], NO_SLOT)
         nc.scalar.activation(out=warm[:], in_=warm[:], func=ACT.Sin)
 
         ident = const.tile([P, P], F32)
         masks.make_identity(nc, ident[:])
-        from_left = const.tile([P, P], F32)
-        nc.vector.tensor_copy(out=from_left[:, 1:P], in_=ident[:, 0 : P - 1])
-        nc.vector.tensor_copy(out=from_left[:, 0:1], in_=ident[:, P - 1 : P])
 
         window = const.tile([P, RUN_WINDOWS], F32)
         for s in range(BATCH):
@@ -161,9 +162,17 @@ def tile_deepseekv4attention_pa_t_kernel(
             nc.tensor.transpose(ape_flipped[:], ape_square[:], ident[:])
             nc.vector.tensor_copy(out=ape_cols[:], in_=ape_flipped[:, 0:RATIO])
 
-        top = const.tile([P, RUN_WINDOWS + 3, P], BF16)
-        nc.vector.memset(top[:, 0, :], NO_SLOT)
-        nc.vector.memset(top[:, RUN_WINDOWS + 2, :], NO_SLOT)
+        top = const.tile([P, LAST, P], BF16)
+        top_flat = top[:].rearrange("p w q -> p (w q)")
+        top_last = const.tile([P, BATCH, RUNS_PER_SEQ + 1], BF16)
+        nc.vector.memset(top_last[:], NO_SLOT)
+        own_last = top_last[:, :, 1:]
+        left_last = top_last[:, :, 0:RUNS_PER_SEQ]
+        inner = const.tile([P, 1], F32)
+        nc.vector.tensor_single_scalar(out=inner[:], in_=window[:, 0:1], scalar=0.0, op=ALU.is_gt)
+        gates_last = const.tile([P, RATIO, WIDE], F32)
+        codes_first = const.tile([P, RATIO * P], U32, align_bytes=64)
+        plane_first = const.tile([P, RATIO * P], U8, align_bytes=64)
         first_half = const.tile([P, RUN_WINDOWS + 1, 2, FEAT], F32)
         totals = const.tile([P, RUN_WINDOWS, 2, FEAT], F32)
         inverse = const.tile([P, RUN_WINDOWS, FEAT], F32)
@@ -179,6 +188,7 @@ def tile_deepseekv4attention_pa_t_kernel(
         product_tiles = {}
         sum_banks = {}
         batch_tiles = {}
+        shifted_sums = []
         rot_tiles = {}
 
         def width_of(chunk):
@@ -190,13 +200,12 @@ def tile_deepseekv4attention_pa_t_kernel(
             grouped_tiles[chunk] = grouped_pool.tile([P, CHUNK_TOKENS * P * 4], BF16, align_bytes=64, name="grouped")
             blocks = grouped_tiles[chunk][:].bitcast(F32).rearrange("p (b n h) -> p b n h", n=P, h=2)
             x_words = x_tiles[chunk][:].rearrange("p j k -> p (j k)").bitcast(F32)
-            order = from_left if chunk == 0 else ident
             for pair in range(n_pairs):
                 flipped = psum_t.tile([P, 2, 2, P], F32, tag="ring")
                 for t in range(2):
                     base = (2 * pair + t) * WORDS
                     for h in range(2):
-                        nc.tensor.transpose(flipped[:, t, h, :], x_words[:, base + h : base + WORDS : 2], order[:])
+                        nc.tensor.transpose(flipped[:, t, h, :], x_words[:, base + h : base + WORDS : 2], ident[:])
                 first = ((2 * pair) % RATIO) * n_win + (2 * pair) // RATIO
                 out = blocks[:, first : first + n_win + 1 : n_win]
                 if 0 < chunk < VECTOR_HELPS and pair % 2 == 1:
@@ -206,8 +215,11 @@ def tile_deepseekv4attention_pa_t_kernel(
 
         def quantise(chunk):
             n_tok = RATIO * len(windows_of(chunk))
-            codes = code_pool.tile([P, CHUNK_TOKENS * P], U32, align_bytes=64)
-            plane = code_pool.tile([P, CHUNK_TOKENS * P], U8, align_bytes=64)
+            if chunk == 0:
+                codes, plane = codes_first, plane_first
+            else:
+                codes = code_pool.tile([P, CHUNK_TOKENS * P], U32, align_bytes=64)
+                plane = code_pool.tile([P, CHUNK_TOKENS * P], U8, align_bytes=64)
             nc.vector.quantize_mx(
                 out=codes[:, 0 : n_tok * P].bitcast(FP8X4),
                 scales=plane[:, 0 : n_tok * P],
@@ -215,126 +227,183 @@ def tile_deepseekv4attention_pa_t_kernel(
             )
             code_tiles[chunk] = (codes, plane)
 
-        def multiply(chunk, which, banks):
-            codes, plane = code_tiles[chunk]
+        def one_pass(out, which, source, cols):
+            codes, plane = code_tiles[source]
+            nc.tensor.matmul_mx(
+                out=out,
+                lhsT=w_words[:, which, :].bitcast(FP4X4),
+                lhsT_scale=w_plane[:, which, :],
+                rhs=codes[:, cols].bitcast(FP8X4),
+                rhs_scale=plane[:, cols],
+                start=True,
+                stop=True,
+            )
+
+        def gate_product(chunk):
             width = width_of(chunk)
-            banks[chunk] = []
+            gate_banks[chunk] = []
             for half in range(2):
                 bank = psum_m.tile([P, 2 * WIDE], F32, name="bank")
-                cols = slice(2 * half * width, 2 * (half + 1) * width)
-                nc.tensor.matmul_mx(
-                    out=bank[:, 0 : 2 * width],
-                    lhsT=w_words[:, which, :].bitcast(FP4X4),
-                    lhsT_scale=w_plane[:, which, :],
-                    rhs=codes[:, cols].bitcast(FP8X4),
-                    rhs_scale=plane[:, cols],
-                    start=True,
-                    stop=True,
-                )
-                banks[chunk].append(bank[:, 0 : 2 * width].rearrange("p (s n) -> p s n", s=2))
+                one_pass(bank[:, 0 : 2 * width], 0, chunk, slice(2 * half * width, 2 * (half + 1) * width))
+                gate_banks[chunk].append(bank[:, 0 : 2 * width].rearrange("p (s n) -> p s n", s=2))
+
+        def kv_product(chunk):
+            kv_banks[chunk] = []
+            for half in range(2):
+                bank = psum_m.tile([P, 2 * WIDE], F32, name="bank")
+                if chunk < N_CHUNKS - 1:
+                    one_pass(bank[:], 1, chunk, slice(2 * half * WIDE, 2 * (half + 1) * WIDE))
+                    view = bank[:].rearrange("p (s i n) -> p s i n", s=2, n=P)
+                else:
+                    for i, source in enumerate((chunk, 0)):
+                        one_pass(bank[:, i * WIDE : (i + 1) * WIDE], 1, source, slice(half * WIDE, (half + 1) * WIDE))
+                    view = bank[:].rearrange("p (i s n) -> p s i n", i=2, n=P)
+                kv_banks[chunk].append(view)
+
+        def early_gates(chunk):
+            if chunk == 0:
+                return gates_last[:, :, P:WIDE]
+            if chunk == N_CHUNKS - 1:
+                return gates_last[:, :, 0:P]
+            return gate_tiles[chunk][:]
 
         def offset(chunk):
-            width = width_of(chunk)
-            gates = t_pool.tile([P, RATIO, WIDE], F32, name="gates")
+            if 0 < chunk < N_CHUNKS - 1:
+                gate_tiles[chunk] = t_pool.tile([P, RATIO, WIDE], F32, name="gates")
+            elif chunk == N_CHUNKS - 1:
+                gate_tiles[chunk] = gates_last
+            gates = early_gates(chunk)
             for r in range(RATIO):
                 nc.scalar.activation(
-                    out=gates[:, r, 0:width], in_=gate_banks[chunk][r // 2][:, r % 2, :],
+                    out=gates[:, r, :], in_=gate_banks[chunk][r // 2][:, r % 2, :],
                     func=ACT.Identity, bias=ape_cols[:, r : r + 1], scale=1.0,
                 )
-            if chunk == 0:
-                starts = gates[:, :, 0:P:RUNS_PER_SEQ]
-                nc.scalar.activation(out=starts, in_=starts, func=ACT.Identity, scale=0.0, bias=no_slot[:, 0:1])
-            gate_tiles[chunk] = gates
 
         def top_first(chunk):
             width = width_of(chunk)
-            gates = gate_tiles[chunk]
+            gates = early_gates(chunk)
             half_top = m_pool.tile([P, 2, WIDE], BF16)
-            nc.vector.tensor_tensor(
-                out=half_top[:, :, 0:width], in0=gates[:, 0:2, 0:width], in1=gates[:, 2:4, 0:width], op=ALU.max
-            )
+            nc.vector.tensor_tensor(out=half_top[:, :, 0:width], in0=gates[:, 0:2, :], in1=gates[:, 2:4, :], op=ALU.max)
             half_tops[chunk] = half_top
 
-        def own_top(chunk, shift=0):
-            first = windows_of(chunk)[0] + 2 + shift
-            return top[:, first : first + len(windows_of(chunk)), :].rearrange("p w q -> p (w q)")
+        by_seq = "p (b q) -> p b q"
 
         def top_second(chunk):
-            width = width_of(chunk)
-            nc.vector.tensor_tensor(
-                out=own_top(chunk), in0=half_tops[chunk][:, 0, 0:width], in1=half_tops[chunk][:, 1, 0:width], op=ALU.max
-            )
+            a, b = half_tops[chunk][:, 0, :], half_tops[chunk][:, 1, :]
+            w = windows_of(chunk)
+            if chunk == 1:
+                nc.vector.tensor_tensor(out=top[:, 0, :], in0=a[:, 0:P], in1=b[:, 0:P], op=ALU.max)
+                nc.vector.tensor_tensor(
+                    out=own_last, in0=a[:, P:WIDE].rearrange(by_seq, b=BATCH), in1=b[:, P:WIDE].rearrange(by_seq, b=BATCH), op=ALU.max
+                )
+            else:
+                width = width_of(chunk)
+                nc.vector.tensor_tensor(
+                    out=top_flat[:, w[0] * P : w[0] * P + width], in0=a[:, 0:width], in1=b[:, 0:width], op=ALU.max
+                )
 
         def exchange(chunk):
-            width = width_of(chunk)
             partner = psum_t.tile([P, WIDE], BF16, tag="ring")
-            nc.tensor.matmul(out=partner[:, 0:width], lhsT=upper_down[:], rhs=own_top(chunk, 1), start=True, stop=False)
-            nc.tensor.matmul(out=partner[:, 0:width], lhsT=lower_up[:], rhs=own_top(chunk, -1), start=False, stop=True)
+            if chunk == 1:
+                parts = [
+                    (0, P, top[:, 1, :], left_last),
+                    (P, WIDE, top_flat[:, 1 : P + 1], top[:, LAST - 1, :]),
+                ]
+            elif chunk == N_CHUNKS - 1:
+                parts = [
+                    (0, P, top[:, LAST - 1, :], top[:, LAST - 3, :]),
+                    (P, WIDE, own_last, top[:, LAST - 2, :]),
+                ]
+            else:
+                first = unit_of(chunk)[0] * P
+                parts = [(0, WIDE, top_flat[:, first + P : first + P + WIDE], top_flat[:, first - P : first - P + WIDE])]
+            for n0, n1, after, before in parts:
+                nc.tensor.matmul(out=partner[:, n0:n1], lhsT=upper_down[:], rhs=after, start=True, stop=False)
+                nc.tensor.matmul(out=partner[:, n0:n1], lhsT=lower_up[:], rhs=before, start=False, stop=True)
             partner_tiles[chunk] = partner
 
         def peak_of(chunk):
-            width = width_of(chunk)
             peak = m_pool.tile([P, WIDE], BF16)
-            nc.vector.tensor_tensor(
-                out=peak[:, 0:width], in0=partner_tiles[chunk][:, 0:width], in1=own_top(chunk), op=ALU.max
-            )
+            partner = partner_tiles[chunk]
+            if chunk == 1:
+                nc.vector.tensor_tensor(out=peak[:, 0:P], in0=partner[:, 0:P], in1=top[:, 0, :], op=ALU.max)
+                nc.vector.tensor_tensor(
+                    out=peak[:, P:WIDE].rearrange(by_seq, b=BATCH), in0=partner[:, P:WIDE].rearrange(by_seq, b=BATCH), in1=own_last, op=ALU.max
+                )
+            else:
+                first = unit_of(chunk)[0] * P
+                nc.vector.tensor_tensor(out=peak[:], in0=partner[:], in1=top_flat[:, first : first + WIDE], op=ALU.max)
             peak_tiles[chunk] = peak
 
         def stabilise(chunk):
-            width = width_of(chunk)
             gates = gate_tiles[chunk]
             nc.vector.tensor_tensor(
-                out=gates[:, :, 0:width], in0=gates[:, :, 0:width],
-                in1=peak_tiles[chunk][:, 0:width].unsqueeze(1).to_broadcast([P, RATIO, width]),
-                op=ALU.subtract,
+                out=gates[:], in0=gates[:], in1=peak_tiles[chunk][:].unsqueeze(1).to_broadcast([P, RATIO, WIDE]), op=ALU.subtract
             )
 
         def exponent(chunk):
-            width = width_of(chunk)
             gates = gate_tiles[chunk]
-            nc.scalar.activation(out=gates[:, :, 0:width], in_=gates[:, :, 0:width], func=ACT.Exp)
+            nc.scalar.activation(out=gates[:], in_=gates[:], func=ACT.Exp)
 
         def weigh(chunk, half):
-            width = width_of(chunk)
             if half == 0:
                 product_tiles[chunk] = y_pool.tile([P, RATIO, WIDE], F32, name="products")
             rows = slice(2 * half, 2 * half + 2)
+            by_window = "p s (i n) -> p s i n"
             nc.vector.tensor_tensor(
-                out=product_tiles[chunk][:, rows, 0:width], in0=kv_banks[chunk][half],
-                in1=gate_tiles[chunk][:, rows, 0:width], op=ALU.mult,
+                out=product_tiles[chunk][:, rows, :].rearrange(by_window, n=P), in0=kv_banks[chunk][half],
+                in1=gate_tiles[chunk][:, rows, :].rearrange(by_window, n=P), op=ALU.mult,
             )
 
         def slot_sums(chunk):
             acc = psum_t.tile([P, CHUNK_WINDOWS, 2, COLS], F32, tag="ring")
-            for i in range(len(windows_of(chunk))):
-                for kind, terms in enumerate((gate_tiles[chunk], product_tiles[chunk])):
-                    for r in range(RATIO):
-                        nc.tensor.matmul(
-                            out=acc[:, i, kind, :],
-                            lhsT=terms[:, r, i * P : (i + 1) * P],
-                            rhs=ident[:],
-                            is_transpose=True,
-                            start=(r == 0),
-                            stop=(r == RATIO - 1),
-                        )
+
+            def one_sum(out, kind, first):
+                terms = (gate_tiles[chunk], product_tiles[chunk])[kind]
+                for r in range(RATIO):
+                    nc.tensor.matmul(
+                        out=out, lhsT=terms[:, r, first : first + P], rhs=ident[:], is_transpose=True,
+                        start=(r == 0), stop=(r == RATIO - 1),
+                    )
+
+            for i in range(CHUNK_WINDOWS):
+                for kind in range(2):
+                    one_sum(acc[:, i, kind, :], kind, i * P)
             sum_banks[chunk] = acc
+            if chunk == 1:
+                shifted = psum_m.tile([P, 2 * WIDE], F32, name="bank")
+                for kind in range(2):
+                    one_sum(shifted[:, kind * COLS : (kind + 1) * COLS], kind, P - 1)
+                shifted_sums.append(shifted[:, 0 : 2 * COLS].rearrange("p (k c) -> p k c", k=2))
 
         def sums_out(chunk):
-            n_win = len(windows_of(chunk))
-            first = windows_of(chunk)[0]
-            if chunk < N_CHUNKS - LATE_CHUNKS:
-                nc.scalar.copy(out=first_half[:, first + 1 : first + 1 + n_win], in_=sum_banks[chunk][:, 0:n_win, :, 0:FEAT])
+            acc = sum_banks[chunk]
+            if chunk == 1:
+                nc.scalar.activation(
+                    out=first_half[:, 0], in_=shifted_sums[0][:, :, 0:FEAT], func=ACT.Copy, scale=inner[:, 0:1]
+                )
+                nc.scalar.copy(out=first_half[:, 1], in_=acc[:, 0, :, 0:FEAT])
+                nc.scalar.copy(out=totals[:, LAST], in_=acc[:, 1, :, FEAT:COLS])
+            elif chunk == N_CHUNKS - 1:
+                nc.vector.tensor_copy(out=first_half[:, LAST - 1], in_=acc[:, 0, :, 0:FEAT])
             else:
-                nc.vector.tensor_copy(out=first_half[:, first + 1 : first + 1 + n_win], in_=sum_banks[chunk][:, 0:n_win, :, 0:FEAT])
+                first = unit_of(chunk)[0]
+                out, source = first_half[:, first + 1 : first + 3], acc[:, :, :, 0:FEAT]
+                if chunk < N_CHUNKS - LATE_CHUNKS:
+                    nc.scalar.copy(out=out, in_=source)
+                else:
+                    nc.vector.tensor_copy(out=out, in_=source)
 
         def fold(chunk):
-            n_win = len(windows_of(chunk))
-            first = windows_of(chunk)[0]
-            if chunk > 0:
-                nc.vector.tensor_tensor(
-                    out=totals[:, first : first + n_win], in0=sum_banks[chunk][:, 0:n_win, :, FEAT:COLS],
-                    in1=first_half[:, first : first + n_win], op=ALU.add,
-                )
+            acc = sum_banks[chunk]
+            first = unit_of(chunk)[0]
+            count = 1 if chunk == 1 else 2
+            nc.vector.tensor_tensor(
+                out=totals[:, first : first + count], in0=acc[:, 0:count, :, FEAT:COLS],
+                in1=first_half[:, first : first + count], op=ALU.add,
+            )
+            if chunk == N_CHUNKS - 1:
+                nc.vector.tensor_tensor(out=totals[:, LAST], in0=acc[:, 1, :, 0:FEAT], in1=totals[:, LAST], op=ALU.add)
 
         def logarithm(w0, w1):
             nc.scalar.activation(out=inverse[:, w0:w1, :], in_=totals[:, w0:w1, 0, :], func=ACT.Ln)
@@ -384,59 +453,56 @@ def tile_deepseekv4attention_pa_t_kernel(
                 )
                 nc.sync.dma_start(out=krot_runs[:, w0:w1, :], in_=k_rot[:])
 
-        def batch_done_by(chunk):
-            if not 0 <= chunk < N_CHUNKS:
-                return None
-            after = windows_of(chunk)[-1] + 1
-            return after - BATCH_TARGETS if after > 0 and after % BATCH_TARGETS == 0 else None
-
         def live(chunk):
             return 0 <= chunk < N_CHUNKS
 
+        def unit(chunk):
+            return 1 <= chunk < N_CHUNKS
+
         for a in range(0, N_CHUNKS + 9):
-            if live(a - 8):
+            if unit(a - 8):
                 sums_out(a - 8)
-            if live(a - 5):
+            if unit(a - 5):
                 stabilise(a - 5)
             if a == 2:
                 flip_offset()
             if live(a - 2):
-                multiply(a - 2, 0, gate_banks)
+                gate_product(a - 2)
                 offset(a - 2)
-            if live(a - 5):
+            if unit(a - 5):
                 exponent(a - 5)
             if a - 5 == N_CHUNKS:
                 logarithm(0, LAST_BATCH)
             if live(a - 1):
                 quantise(a - 1)
-            if live(a - 8):
+            if unit(a - 8):
                 fold(a - 8)
             if a - 8 == N_CHUNKS - 2:
-                logarithm(LAST_BATCH, RUN_WINDOWS - CHUNK_WINDOWS)
+                logarithm(LAST_BATCH, LAST - 2)
             if live(a):
                 flip(a)
             if a == TRIG_ROUND:
                 trigonometry()
             if live(a - 2):
                 top_first(a - 2)
-            if live(a - 6):
-                multiply(a - 6, 1, kv_banks)
+            if unit(a - 6):
+                kv_product(a - 6)
                 weigh(a - 6, 0)
                 weigh(a - 6, 1)
-            if live(a - 4):
+            if unit(a - 4):
                 exchange(a - 4)
                 peak_of(a - 4)
             if live(a - 2):
                 top_second(a - 2)
-            if live(a - 7):
+            if unit(a - 7):
                 slot_sums(a - 7)
             if live(a + LOADS_AHEAD):
                 load(a + LOADS_AHEAD)
 
         for w0 in range(0, LAST_BATCH, BATCH_TARGETS):
             invert(w0)
-        invert(LAST_BATCH, BATCH_TARGETS - CHUNK_WINDOWS)
-        invert_exactly(RUN_WINDOWS - CHUNK_WINDOWS, RUN_WINDOWS)
+        invert(LAST_BATCH, LAST - 2 - LAST_BATCH)
+        invert_exactly(LAST - 2, RUN_WINDOWS)
         for pair in ((0, BATCH_TARGETS), (2 * BATCH_TARGETS, LAST_BATCH)):
             for w0 in pair:
                 divide(w0)

@@ -56,13 +56,14 @@ def tile_deepseekv4attention_pa_t_kernel(
         const = ctx.enter_context(tc.tile_pool(name="const", bufs=1))
         x_pool = ctx.enter_context(tc.tile_pool(name="x", bufs=4))
         grouped_pool = ctx.enter_context(tc.tile_pool(name="grouped", bufs=2))
-        code_pool = ctx.enter_context(tc.tile_pool(name="codes", bufs=6))
-        t_pool = ctx.enter_context(tc.tile_pool(name="gates", bufs=6))
+        code_pool = ctx.enter_context(tc.tile_pool(name="codes", bufs=7))
+        t_pool = ctx.enter_context(tc.tile_pool(name="gates", bufs=7))
         y_pool = ctx.enter_context(tc.tile_pool(name="products", bufs=2))
         m_pool = ctx.enter_context(tc.tile_pool(name="maxima", bufs=2))
+        p_pool = ctx.enter_context(tc.tile_pool(name="partners", bufs=3))
         o_pool = ctx.enter_context(tc.tile_pool(name="outs", bufs=4))
-        psum_t = ctx.enter_context(tc.psum_pool(name="psum_t", bufs=6))
-        psum_m = ctx.enter_context(tc.psum_pool(name="psum_m", bufs=2))
+        psum_t = ctx.enter_context(tc.psum_pool(name="psum_t", bufs=5))
+        psum_m = ctx.enter_context(tc.psum_pool(name="psum_m", bufs=3))
         ctx.enter_context(tc.manual_schedule())
 
         def windows_of(chunk):
@@ -145,13 +146,6 @@ def tile_deepseekv4attention_pa_t_kernel(
             nc.scalar.activation(out=sin_pairs[:, :, :, 1], in_=turns[:, 0], func=ACT.Sin, scale=2.0 * math.pi)
             nc.scalar.activation(out=warm[:], in_=warm[:], func=ACT.Exp)
 
-        upper_down = const.tile([P, P], BF16)
-        lower_up = const.tile([P, P], BF16)
-        nc.vector.memset(upper_down[:], 0.0)
-        nc.vector.memset(lower_up[:], 0.0)
-        nc.vector.tensor_copy(out=upper_down[:, 0:FEAT], in_=ident[:, FEAT:COLS])
-        nc.vector.tensor_copy(out=lower_up[:, FEAT:COLS], in_=ident[:, 0:FEAT])
-
         ape_square = const.tile([P, P], F32)
         nc.gpsimd.memset(ape_square[:], 0.0)
         ape_cols = const.tile([P, RATIO], F32)
@@ -164,10 +158,11 @@ def tile_deepseekv4attention_pa_t_kernel(
 
         top = const.tile([P, LAST, P], BF16)
         top_flat = top[:].rearrange("p w q -> p (w q)")
-        top_last = const.tile([P, BATCH, RUNS_PER_SEQ + 1], BF16)
-        nc.vector.memset(top_last[:], NO_SLOT)
-        own_last = top_last[:, :, 1:]
-        left_last = top_last[:, :, 0:RUNS_PER_SEQ]
+        own_last = const.tile([P, P], BF16)
+        left_last = const.tile([P, P], BF16)
+        right_first = const.tile([P, P], BF16)
+        nc.vector.memset(left_last[:], NO_SLOT)
+        nc.vector.memset(right_first[:], NO_SLOT)
         inner = const.tile([P, 1], F32)
         nc.vector.tensor_single_scalar(out=inner[:], in_=window[:, 0:1], scalar=0.0, op=ALU.is_gt)
         gates_last = const.tile([P, RATIO, WIDE], F32)
@@ -286,16 +281,18 @@ def tile_deepseekv4attention_pa_t_kernel(
             nc.vector.tensor_tensor(out=half_top[:, :, 0:width], in0=gates[:, 0:2, :], in1=gates[:, 2:4, :], op=ALU.max)
             half_tops[chunk] = half_top
 
-        by_seq = "p (b q) -> p b q"
-
         def top_second(chunk):
             a, b = half_tops[chunk][:, 0, :], half_tops[chunk][:, 1, :]
             w = windows_of(chunk)
             if chunk == 1:
                 nc.vector.tensor_tensor(out=top[:, 0, :], in0=a[:, 0:P], in1=b[:, 0:P], op=ALU.max)
-                nc.vector.tensor_tensor(
-                    out=own_last, in0=a[:, P:WIDE].rearrange(by_seq, b=BATCH), in1=b[:, P:WIDE].rearrange(by_seq, b=BATCH), op=ALU.max
+                nc.vector.tensor_tensor(out=own_last[:], in0=a[:, P:WIDE], in1=b[:, P:WIDE], op=ALU.max)
+                by_seq = "p (b q) -> p b q"
+                nc.vector.tensor_copy(
+                    out=left_last[:].rearrange(by_seq, b=BATCH)[:, :, 1:],
+                    in_=own_last[:].rearrange(by_seq, b=BATCH)[:, :, 0 : RUNS_PER_SEQ - 1],
                 )
+                nc.vector.tensor_copy(out=right_first[:, 0 : P - 1], in_=top[:, 0, 1:P])
             else:
                 width = width_of(chunk)
                 nc.vector.tensor_tensor(
@@ -303,23 +300,17 @@ def tile_deepseekv4attention_pa_t_kernel(
                 )
 
         def exchange(chunk):
-            partner = psum_t.tile([P, WIDE], BF16, tag="ring")
+            partner = p_pool.tile([P, WIDE], BF16)
             if chunk == 1:
-                parts = [
-                    (0, P, top[:, 1, :], left_last),
-                    (P, WIDE, top_flat[:, 1 : P + 1], top[:, LAST - 1, :]),
-                ]
+                parts = [(0, P, top[:, 1, :], left_last[:]), (P, WIDE, right_first[:], top[:, LAST - 1, :])]
             elif chunk == N_CHUNKS - 1:
-                parts = [
-                    (0, P, top[:, LAST - 1, :], top[:, LAST - 3, :]),
-                    (P, WIDE, own_last, top[:, LAST - 2, :]),
-                ]
+                parts = [(0, P, top[:, LAST - 1, :], top[:, LAST - 3, :]), (P, WIDE, own_last[:], top[:, LAST - 2, :])]
             else:
                 first = unit_of(chunk)[0] * P
                 parts = [(0, WIDE, top_flat[:, first + P : first + P + WIDE], top_flat[:, first - P : first - P + WIDE])]
             for n0, n1, after, before in parts:
-                nc.tensor.matmul(out=partner[:, n0:n1], lhsT=upper_down[:], rhs=after, start=True, stop=False)
-                nc.tensor.matmul(out=partner[:, n0:n1], lhsT=lower_up[:], rhs=before, start=False, stop=True)
+                nc.sync.dma_start(out=partner[0:FEAT, n0:n1], in_=after[FEAT:COLS])
+                nc.sync.dma_start(out=partner[FEAT:COLS, n0:n1], in_=before[0:FEAT])
             partner_tiles[chunk] = partner
 
         def peak_of(chunk):
@@ -327,9 +318,7 @@ def tile_deepseekv4attention_pa_t_kernel(
             partner = partner_tiles[chunk]
             if chunk == 1:
                 nc.vector.tensor_tensor(out=peak[:, 0:P], in0=partner[:, 0:P], in1=top[:, 0, :], op=ALU.max)
-                nc.vector.tensor_tensor(
-                    out=peak[:, P:WIDE].rearrange(by_seq, b=BATCH), in0=partner[:, P:WIDE].rearrange(by_seq, b=BATCH), in1=own_last, op=ALU.max
-                )
+                nc.vector.tensor_tensor(out=peak[:, P:WIDE], in0=partner[:, P:WIDE], in1=own_last[:], op=ALU.max)
             else:
                 first = unit_of(chunk)[0] * P
                 nc.vector.tensor_tensor(out=peak[:], in0=partner[:], in1=top_flat[:, first : first + WIDE], op=ALU.max)
@@ -459,43 +448,44 @@ def tile_deepseekv4attention_pa_t_kernel(
         def unit(chunk):
             return 1 <= chunk < N_CHUNKS
 
-        for a in range(0, N_CHUNKS + 9):
-            if unit(a - 8):
-                sums_out(a - 8)
-            if unit(a - 5):
-                stabilise(a - 5)
+        for a in range(0, N_CHUNKS + 10):
+            if unit(a - 9):
+                sums_out(a - 9)
+            if unit(a - 6):
+                stabilise(a - 6)
             if a == 2:
                 flip_offset()
             if live(a - 2):
                 gate_product(a - 2)
                 offset(a - 2)
-            if unit(a - 5):
-                exponent(a - 5)
-            if a - 5 == N_CHUNKS:
+            if unit(a - 6):
+                exponent(a - 6)
+            if a - 6 == N_CHUNKS:
                 logarithm(0, LAST_BATCH)
+            if unit(a - 5):
+                peak_of(a - 5)
             if live(a - 1):
                 quantise(a - 1)
-            if unit(a - 8):
-                fold(a - 8)
-            if a - 8 == N_CHUNKS - 2:
+            if unit(a - 9):
+                fold(a - 9)
+            if a - 9 == N_CHUNKS - 2:
                 logarithm(LAST_BATCH, LAST - 2)
+            if unit(a - 4):
+                exchange(a - 4)
             if live(a):
                 flip(a)
             if a == TRIG_ROUND:
                 trigonometry()
             if live(a - 2):
                 top_first(a - 2)
-            if unit(a - 6):
-                kv_product(a - 6)
-                weigh(a - 6, 0)
-                weigh(a - 6, 1)
-            if unit(a - 4):
-                exchange(a - 4)
-                peak_of(a - 4)
+            if unit(a - 7):
+                kv_product(a - 7)
+                weigh(a - 7, 0)
+                weigh(a - 7, 1)
             if live(a - 2):
                 top_second(a - 2)
-            if unit(a - 7):
-                slot_sums(a - 7)
+            if unit(a - 8):
+                slot_sums(a - 8)
             if live(a + LOADS_AHEAD):
                 load(a + LOADS_AHEAD)
 

@@ -59,7 +59,7 @@ def tile_deepseekv4attention_pa_t_kernel(
         code_pool = ctx.enter_context(tc.tile_pool(name="codes", bufs=7))
         t_pool = ctx.enter_context(tc.tile_pool(name="gates", bufs=7))
         y_pool = ctx.enter_context(tc.tile_pool(name="products", bufs=2))
-        m_pool = ctx.enter_context(tc.tile_pool(name="maxima", bufs=2))
+        m_pool = ctx.enter_context(tc.tile_pool(name="maxima", bufs=3))
         p_pool = ctx.enter_context(tc.tile_pool(name="partners", bufs=3))
         o_pool = ctx.enter_context(tc.tile_pool(name="outs", bufs=4))
         psum_t = ctx.enter_context(tc.psum_pool(name="psum_t", bufs=5))
@@ -324,10 +324,11 @@ def tile_deepseekv4attention_pa_t_kernel(
                 nc.vector.tensor_tensor(out=peak[:], in0=partner[:], in1=top_flat[:, first : first + WIDE], op=ALU.max)
             peak_tiles[chunk] = peak
 
-        def stabilise(chunk):
+        def stabilise(chunk, engine, r0, r1):
             gates = gate_tiles[chunk]
-            nc.vector.tensor_tensor(
-                out=gates[:], in0=gates[:], in1=peak_tiles[chunk][:].unsqueeze(1).to_broadcast([P, RATIO, WIDE]), op=ALU.subtract
+            engine.tensor_tensor(
+                out=gates[:, r0:r1], in0=gates[:, r0:r1],
+                in1=peak_tiles[chunk][:].unsqueeze(1).to_broadcast([P, r1 - r0, WIDE]), op=ALU.subtract,
             )
 
         def exponent(chunk):
@@ -452,7 +453,7 @@ def tile_deepseekv4attention_pa_t_kernel(
             if unit(a - 9):
                 sums_out(a - 9)
             if unit(a - 6):
-                stabilise(a - 6)
+                stabilise(a - 6, nc.vector, 0, RATIO - 2)
             if a == 2:
                 flip_offset()
             if live(a - 2):
@@ -462,8 +463,6 @@ def tile_deepseekv4attention_pa_t_kernel(
                 exponent(a - 6)
             if a - 6 == N_CHUNKS:
                 logarithm(0, LAST_BATCH)
-            if unit(a - 5):
-                peak_of(a - 5)
             if live(a - 1):
                 quantise(a - 1)
             if unit(a - 9):
@@ -478,6 +477,9 @@ def tile_deepseekv4attention_pa_t_kernel(
                 trigonometry()
             if live(a - 2):
                 top_first(a - 2)
+            if unit(a - 5):
+                peak_of(a - 5)
+                stabilise(a - 5, nc.gpsimd, RATIO - 2, RATIO)
             if unit(a - 7):
                 kv_product(a - 7)
                 weigh(a - 7, 0)

@@ -35,8 +35,8 @@ LAST = RUN_WINDOWS - 1
 BATCH_TARGETS = 8
 LAST_BATCH = RUN_WINDOWS - BATCH_TARGETS
 LOADS_AHEAD = 3
-VECTOR_HELPS = 4
-TRIG_ROUND = 1
+VECTOR_HELPS = 8
+TABLE_ROUND = 1
 LATE_CHUNKS = 3
 NO_SLOT = -(2.0**100)
 ROUND = 1.5 * 2.0**23
@@ -58,7 +58,7 @@ def tile_deepseekv4attention_pa_t_kernel(
         grouped_pool = ctx.enter_context(tc.tile_pool(name="grouped", bufs=2))
         code_pool = ctx.enter_context(tc.tile_pool(name="codes", bufs=7))
         t_pool = ctx.enter_context(tc.tile_pool(name="gates", bufs=7))
-        y_pool = ctx.enter_context(tc.tile_pool(name="products", bufs=2))
+        y_pool = ctx.enter_context(tc.tile_pool(name="products", bufs=3))
         m_pool = ctx.enter_context(tc.tile_pool(name="maxima", bufs=3))
         p_pool = ctx.enter_context(tc.tile_pool(name="partners", bufs=3))
         o_pool = ctx.enter_context(tc.tile_pool(name="outs", bufs=4))
@@ -95,25 +95,26 @@ def tile_deepseekv4attention_pa_t_kernel(
         w_plane = const.tile([P, 2, COLS], U8, align_bytes=64)
         ape_rows = const.tile([P, COLS], BF16)
         nc.vector.memset(w_plane[:].rearrange("p w c -> p (w c)").bitcast(I32), 0)
-        load(0)
-        load(1)
-        for i, (words, scales) in enumerate(((wgate_words, wgate_scales), (wkv_words, wkv_scales))):
+
+        def load_weights(i, words, scales):
             nc.sync.dma_start(out=w_words[:, i, :].bitcast(I32), in_=words[0].bitcast(I32))
             for quad in range(4):
                 nc.sync.dma_start(
                     out=w_plane[32 * quad : 32 * quad + 4, i, :].bitcast(I32),
                     in_=scales[0, 4 * quad : 4 * quad + 4, :].bitcast(I32),
                 )
-        nc.sync.dma_start(out=ape_rows[0:RATIO, :], in_=ape)
+
+        nc.scalar.dma_start(out=ape_rows[0:RATIO, :], in_=ape)
+        load(0)
+        load(1)
+        load_weights(0, wgate_words, wgate_scales)
         for chunk in range(2, LOADS_AHEAD):
             load(chunk)
+        load_weights(1, wkv_words, wkv_scales)
 
         warm = const.tile([P, 1], F32)
         nc.vector.memset(warm[:], 0.0)
         nc.scalar.activation(out=warm[:], in_=warm[:], func=ACT.Sin)
-
-        ident = const.tile([P, P], F32)
-        masks.make_identity(nc, ident[:])
 
         window = const.tile([P, RUN_WINDOWS], F32)
         for s in range(BATCH):
@@ -121,12 +122,17 @@ def tile_deepseekv4attention_pa_t_kernel(
                 window[s * RUNS_PER_SEQ : (s + 1) * RUNS_PER_SEQ, :], pattern=[[1, RUN_WINDOWS]], base=0,
                 channel_multiplier=RUN_WINDOWS, allow_small_or_imprecise_dtypes=True,
             )
+        ident = const.tile([P, P], F32)
+        masks.make_identity(nc, ident[:])
         turns = y_pool.tile([P, 2, RUN_WINDOWS, PAIRS], F32, name="products")
-        for j in range(PAIRS):
+        for j in range(PAIRS // 4 + 1):
             per_window = RATIO * THETA ** (-j / PAIRS) / (2.0 * math.pi)
-            per_window = per_window - round(per_window)
             nc.vector.tensor_scalar(
-                out=turns[:, 0, :, j], in0=window[:], scalar1=per_window, scalar2=None, op0=ALU.mult
+                out=turns[:, 0, :, j], in0=window[:], scalar1=per_window - round(per_window), scalar2=None, op0=ALU.mult
+            )
+        for j0, j1 in ((PAIRS // 4 + 1, PAIRS // 2), (PAIRS // 2, 3 * PAIRS // 4), (3 * PAIRS // 4, PAIRS)):
+            nc.vector.tensor_scalar(
+                out=turns[:, 0, :, j0:j1], in0=turns[:, 0, :, j0 - PAIRS // 4 : j1 - PAIRS // 4], scalar1=THETA**-0.25, scalar2=None, op0=ALU.mult
             )
         nc.vector.tensor_scalar(out=turns[:, 1], in0=turns[:, 0], scalar1=0.25, scalar2=None, op0=ALU.add)
         whole = y_pool.tile([P, 2, RUN_WINDOWS, PAIRS], F32, name="products")
@@ -134,16 +140,22 @@ def tile_deepseekv4attention_pa_t_kernel(
             out=whole[:], in0=turns[:], scalar1=ROUND, scalar2=ROUND, op0=ALU.add, op1=ALU.subtract
         )
         nc.vector.tensor_tensor(out=turns[:], in0=turns[:], in1=whole[:], op=ALU.subtract)
+        waves = y_pool.tile([P, 2, RUN_WINDOWS, PAIRS], F32, name="products")
         cos_pairs = const.tile([P, RUN_WINDOWS, PAIRS, 2], F32)
         sin_pairs = const.tile([P, RUN_WINDOWS, PAIRS, 2], F32)
 
         def trigonometry():
-            nc.scalar.activation(
-                out=cos_pairs[:], in_=turns[:, 1].unsqueeze(3).to_broadcast([P, RUN_WINDOWS, PAIRS, 2]),
-                func=ACT.Sin, scale=2.0 * math.pi,
+            nc.scalar.activation(out=waves[:], in_=turns[:], func=ACT.Sin, scale=2.0 * math.pi)
+            for e, sign in enumerate((-1.0, 1.0)):
+                nc.gpsimd.tensor_scalar(
+                    out=sin_pairs[:, :, :, e], in0=waves[:, 0], scalar1=sign, scalar2=0.0, op0=ALU.mult, op1=ALU.add
+                )
+            nc.gpsimd.tensor_scalar(
+                out=cos_pairs[:], in0=waves[:, 1].unsqueeze(3).to_broadcast([P, RUN_WINDOWS, PAIRS, 2]),
+                scalar1=1.0, scalar2=0.0, op0=ALU.mult, op1=ALU.add,
             )
-            nc.scalar.activation(out=sin_pairs[:, :, :, 0], in_=turns[:, 0], func=ACT.Sin, scale=-2.0 * math.pi)
-            nc.scalar.activation(out=sin_pairs[:, :, :, 1], in_=turns[:, 0], func=ACT.Sin, scale=2.0 * math.pi)
+
+        def exponent_table():
             nc.scalar.activation(out=warm[:], in_=warm[:], func=ACT.Exp)
 
         ape_square = const.tile([P, P], F32)
@@ -203,7 +215,7 @@ def tile_deepseekv4attention_pa_t_kernel(
                         nc.tensor.transpose(flipped[:, t, h, :], x_words[:, base + h : base + WORDS : 2], ident[:])
                 first = ((2 * pair) % RATIO) * n_win + (2 * pair) // RATIO
                 out = blocks[:, first : first + n_win + 1 : n_win]
-                if 0 < chunk < VECTOR_HELPS and pair % 2 == 1:
+                if pair == 1 and chunk < VECTOR_HELPS or pair == 3 and chunk < VECTOR_HELPS // 2:
                     nc.vector.tensor_copy(out=out, in_=flipped[:].rearrange("p t h n -> p t n h"))
                 else:
                     nc.scalar.copy(out=out, in_=flipped[:].rearrange("p t h n -> p t n h"))
@@ -453,8 +465,8 @@ def tile_deepseekv4attention_pa_t_kernel(
             if unit(a - 9):
                 sums_out(a - 9)
             if unit(a - 6):
-                stabilise(a - 6, nc.vector, 0, RATIO - 2)
-            if a == 2:
+                stabilise(a - 6, nc.vector, 0, RATIO - 1)
+            if a == 1:
                 flip_offset()
             if live(a - 2):
                 gate_product(a - 2)
@@ -473,15 +485,19 @@ def tile_deepseekv4attention_pa_t_kernel(
                 exchange(a - 4)
             if live(a):
                 flip(a)
-            if a == TRIG_ROUND:
+            if a == 0:
                 trigonometry()
+            if a == TABLE_ROUND:
+                exponent_table()
             if live(a - 2):
                 top_first(a - 2)
             if unit(a - 5):
                 peak_of(a - 5)
-                stabilise(a - 5, nc.gpsimd, RATIO - 2, RATIO)
+            if unit(a - 5):
+                stabilise(a - 5, nc.gpsimd, RATIO - 1, RATIO)
             if unit(a - 7):
                 kv_product(a - 7)
+            if unit(a - 7):
                 weigh(a - 7, 0)
                 weigh(a - 7, 1)
             if live(a - 2):

@@ -465,16 +465,12 @@ def tile_deepseekv4attention_pa_t_kernel(
             if unit(a - 9):
                 sums_out(a - 9)
             if unit(a - 6):
-                stabilise(a - 6, nc.vector, 0, RATIO - 1)
+                stabilise(a - 6, nc.vector, 0, RATIO - 2)
             if a == 1:
                 flip_offset()
             if live(a - 2):
                 gate_product(a - 2)
                 offset(a - 2)
-            if unit(a - 6):
-                exponent(a - 6)
-            if a - 6 == N_CHUNKS:
-                logarithm(0, LAST_BATCH)
             if live(a - 1):
                 quantise(a - 1)
             if unit(a - 9):
@@ -489,12 +485,16 @@ def tile_deepseekv4attention_pa_t_kernel(
                 trigonometry()
             if a == TABLE_ROUND:
                 exponent_table()
+            if unit(a - 6):
+                exponent(a - 6)
+            if a - 6 == N_CHUNKS:
+                logarithm(0, LAST_BATCH)
             if live(a - 2):
                 top_first(a - 2)
             if unit(a - 5):
                 peak_of(a - 5)
             if unit(a - 5):
-                stabilise(a - 5, nc.gpsimd, RATIO - 1, RATIO)
+                stabilise(a - 5, nc.gpsimd, RATIO - 2, RATIO)
             if unit(a - 7):
                 kv_product(a - 7)
             if unit(a - 7):

import math
from contextlib import ExitStack

import concourse.masks as masks
import concourse.mybir as mybir

F32 = mybir.dt.float32
BF16 = mybir.dt.bfloat16
I32 = mybir.dt.int32
U32 = mybir.dt.uint32
U8 = mybir.dt.uint8
FP8X4 = mybir.dt.float8_e4m3fn_x4
FP4X4 = mybir.dt.float4_e2m1fn_x4
ALU = mybir.AluOpType
ACT = mybir.ActivationFunctionType

P = 128
BATCH, SEQ, HID = 4, 4096, 512
RATIO = 4
FEAT = 64
COLS = 2 * FEAT
ROPE = 32
PAIRS = ROPE // 2
THETA = 10000.0

RUN_TOKENS = BATCH * SEQ // P
RUN_WINDOWS = RUN_TOKENS // RATIO
RUNS_PER_SEQ = SEQ // RUN_TOKENS
WORDS = HID // 2
CHUNK_WINDOWS = 2
CHUNK_TOKENS = CHUNK_WINDOWS * RATIO
WIDE = CHUNK_WINDOWS * P
N_CHUNKS = 1 + RUN_WINDOWS // CHUNK_WINDOWS
LAST = RUN_WINDOWS - 1
BATCH_TARGETS = 8
LAST_BATCH = RUN_WINDOWS - BATCH_TARGETS
LOADS_AHEAD = 3
VECTOR_HELPS = 8
TABLE_ROUND = 1
LATE_CHUNKS = 3
NO_SLOT = -(2.0**100)
ROUND = 1.5 * 2.0**23

FLOPS = 2 * BATCH * SEQ * HID * 2 * COLS


def tile_deepseekv4attention_pa_t_kernel(
    tc, hidden, wkv_words, wkv_scales, wgate_words, wgate_scales, ape, out_0, out_1
):
    nc = tc.nc
    x_runs = hidden.rearrange("b (q j) k -> (b q) j k", j=RUN_TOKENS)
    krot_runs = out_0.rearrange("b (q u) f -> (b q) u f", u=RUN_WINDOWS)
    pooled_runs = out_1.rearrange("b (q u) f -> (b q) u f", u=RUN_WINDOWS)

    with ExitStack() as ctx:
        const = ctx.enter_context(tc.tile_pool(name="const", bufs=1))
        x_pool = ctx.enter_context(tc.tile_pool(name="x", bufs=4))
        grouped_pool = ctx.enter_context(tc.tile_pool(name="grouped", bufs=2))
        code_pool = ctx.enter_context(tc.tile_pool(name="codes", bufs=7))
        t_pool = ctx.enter_context(tc.tile_pool(name="gates", bufs=7))
        y_pool = ctx.enter_context(tc.tile_pool(name="products", bufs=3))
        m_pool = ctx.enter_context(tc.tile_pool(name="maxima", bufs=3))
        p_pool = ctx.enter_context(tc.tile_pool(name="partners", bufs=3))
        o_pool = ctx.enter_context(tc.tile_pool(name="outs", bufs=4))
        psum_t = ctx.enter_context(tc.psum_pool(name="psum_t", bufs=5))
        psum_m = ctx.enter_context(tc.psum_pool(name="psum_m", bufs=3))
        ctx.enter_context(tc.manual_schedule())

        def windows_of(chunk):
            if chunk == 0:
                return [LAST - 1]
            if chunk == 1:
                return [0, LAST]
            return [CHUNK_WINDOWS * chunk - 3, CHUNK_WINDOWS * chunk - 2] if chunk < N_CHUNKS - 1 else [LAST - 2]

        def unit_of(chunk):
            return [LAST - 2, LAST - 1] if chunk == N_CHUNKS - 1 else windows_of(chunk)

        x_tiles = {}

        def load(chunk):
            windows = windows_of(chunk)
            x_sb = x_pool.tile([P, CHUNK_TOKENS, HID], BF16)
            if chunk == 0:
                pieces = [(t, RATIO * windows[0] + t, RATIO // 2) for t in (0, RATIO // 2)]
            elif chunk == 1:
                pieces = [(RATIO * i, RATIO * w, RATIO) for i, w in enumerate(windows)]
            else:
                pieces = [(0, RATIO * windows[0], RATIO * len(windows))]
            for place, token, count in pieces:
                nc.sync.dma_start(out=x_sb[:, place : place + count, :], in_=x_runs[:, token : token + count, :])
            x_tiles[chunk] = x_sb

        w_words = const.tile([P, 2, 2 * COLS], U8, align_bytes=64)
        w_plane = const.tile([P, 2, COLS], U8, align_bytes=64)
        ape_rows = const.tile([P, COLS], BF16)
        nc.vector.memset(w_plane[:].rearrange("p w c -> p (w c)").bitcast(I32), 0)

        def load_weights(i, words, scales):
            nc.sync.dma_start(out=w_words[:, i, :].bitcast(I32), in_=words[0].bitcast(I32))
            for quad in range(4):
                nc.sync.dma_start(
                    out=w_plane[32 * quad : 32 * quad + 4, i, :].bitcast(I32),
                    in_=scales[0, 4 * quad : 4 * quad + 4, :].bitcast(I32),
                )

        nc.scalar.dma_start(out=ape_rows[0:RATIO, :], in_=ape)
        load(0)
        load(1)
        load_weights(0, wgate_words, wgate_scales)
        for chunk in range(2, LOADS_AHEAD):
            load(chunk)
        load_weights(1, wkv_words, wkv_scales)

        warm = const.tile([P, 1], F32)
        nc.vector.memset(warm[:], 0.0)
        nc.scalar.activation(out=warm[:], in_=warm[:], func=ACT.Sin)

        window = const.tile([P, RUN_WINDOWS], F32)
        for s in range(BATCH):
            nc.gpsimd.iota(
                window[s * RUNS_PER_SEQ : (s + 1) * RUNS_PER_SEQ, :], pattern=[[1, RUN_WINDOWS]], base=0,
                channel_multiplier=RUN_WINDOWS, allow_small_or_imprecise_dtypes=True,
            )
        ident = const.tile([P, P], F32)
        masks.make_identity(nc, ident[:])
        turns = y_pool.tile([P, 2, RUN_WINDOWS, PAIRS], F32, name="products")
        for j in range(PAIRS // 4 + 1):
            per_window = RATIO * THETA ** (-j / PAIRS) / (2.0 * math.pi)
            nc.vector.tensor_scalar(
                out=turns[:, 0, :, j], in0=window[:], scalar1=per_window - round(per_window), scalar2=None, op0=ALU.mult
            )
        for j0, j1 in ((PAIRS // 4 + 1, PAIRS // 2), (PAIRS // 2, 3 * PAIRS // 4), (3 * PAIRS // 4, PAIRS)):
            nc.vector.tensor_scalar(
                out=turns[:, 0, :, j0:j1], in0=turns[:, 0, :, j0 - PAIRS // 4 : j1 - PAIRS // 4], scalar1=THETA**-0.25, scalar2=None, op0=ALU.mult
            )
        nc.vector.tensor_scalar(out=turns[:, 1], in0=turns[:, 0], scalar1=0.25, scalar2=None, op0=ALU.add)
        whole = y_pool.tile([P, 2, RUN_WINDOWS, PAIRS], F32, name="products")
        nc.vector.tensor_scalar(
            out=whole[:], in0=turns[:], scalar1=ROUND, scalar2=ROUND, op0=ALU.add, op1=ALU.subtract
        )
        nc.vector.tensor_tensor(out=turns[:], in0=turns[:], in1=whole[:], op=ALU.subtract)
        waves = y_pool.tile([P, 2, RUN_WINDOWS, PAIRS], F32, name="products")
        cos_pairs = const.tile([P, RUN_WINDOWS, PAIRS, 2], F32)
        sin_pairs = const.tile([P, RUN_WINDOWS, PAIRS, 2], F32)

        def trigonometry():
            nc.scalar.activation(out=waves[:], in_=turns[:], func=ACT.Sin, scale=2.0 * math.pi)
            for e, sign in enumerate((-1.0, 1.0)):
                nc.gpsimd.tensor_scalar(
                    out=sin_pairs[:, :, :, e], in0=waves[:, 0], scalar1=sign, scalar2=0.0, op0=ALU.mult, op1=ALU.add
                )
            nc.gpsimd.tensor_scalar(
                out=cos_pairs[:], in0=waves[:, 1].unsqueeze(3).to_broadcast([P, RUN_WINDOWS, PAIRS, 2]),
                scalar1=1.0, scalar2=0.0, op0=ALU.mult, op1=ALU.add,
            )

        def exponent_table():
            nc.scalar.activation(out=warm[:], in_=warm[:], func=ACT.Exp)

        ape_square = const.tile([P, P], F32)
        nc.gpsimd.memset(ape_square[:], 0.0)
        ape_cols = const.tile([P, RATIO], F32)

        def flip_offset():
            nc.vector.tensor_copy(out=ape_square[0:RATIO, :], in_=ape_rows[0:RATIO, :])
            ape_flipped = psum_t.tile([P, P], F32, tag="ring")
            nc.tensor.transpose(ape_flipped[:], ape_square[:], ident[:])
            nc.vector.tensor_copy(out=ape_cols[:], in_=ape_flipped[:, 0:RATIO])

        top = const.tile([P, LAST, P], BF16)
        top_flat = top[:].rearrange("p w q -> p (w q)")
        own_last = const.tile([P, P], BF16)
        left_last = const.tile([P, P], BF16)
        right_first = const.tile([P, P], BF16)
        nc.vector.memset(left_last[:], NO_SLOT)
        nc.vector.memset(right_first[:], NO_SLOT)
        inner = const.tile([P, 1], F32)
        nc.vector.tensor_single_scalar(out=inner[:], in_=window[:, 0:1], scalar=0.0, op=ALU.is_gt)
        gates_last = const.tile([P, RATIO, WIDE], F32)
        codes_first = const.tile([P, RATIO * P], U32, align_bytes=64)
        plane_first = const.tile([P, RATIO * P], U8, align_bytes=64)
        first_half = const.tile([P, RUN_WINDOWS + 1, 2, FEAT], F32)
        totals = const.tile([P, RUN_WINDOWS, 2, FEAT], F32)
        inverse = const.tile([P, RUN_WINDOWS, FEAT], F32)

        grouped_tiles = {}
        code_tiles = {}
        gate_banks = {}
        kv_banks = {}
        gate_tiles = {}
        half_tops = {}
        partner_tiles = {}
        peak_tiles = {}
        product_tiles = {}
        sum_banks = {}
        batch_tiles = {}
        shifted_sums = []
        rot_tiles = {}

        def width_of(chunk):
            return P * len(windows_of(chunk))

        def flip(chunk):
            n_win = len(windows_of(chunk))
            n_pairs = RATIO * n_win // 2
            grouped_tiles[chunk] = grouped_pool.tile([P, CHUNK_TOKENS * P * 4], BF16, align_bytes=64, name="grouped")
            blocks = grouped_tiles[chunk][:].bitcast(F32).rearrange("p (b n h) -> p b n h", n=P, h=2)
            x_words = x_tiles[chunk][:].rearrange("p j k -> p (j k)").bitcast(F32)
            for pair in range(n_pairs):
                flipped = psum_t.tile([P, 2, 2, P], F32, tag="ring")
                for t in range(2):
                    base = (2 * pair + t) * WORDS
                    for h in range(2):
                        nc.tensor.transpose(flipped[:, t, h, :], x_words[:, base + h : base + WORDS : 2], ident[:])
                first = ((2 * pair) % RATIO) * n_win + (2 * pair) // RATIO
                out = blocks[:, first : first + n_win + 1 : n_win]
                if pair == 1 and chunk < VECTOR_HELPS or pair == 3 and chunk < VECTOR_HELPS // 2:
                    nc.vector.tensor_copy(out=out, in_=flipped[:].rearrange("p t h n -> p t n h"))
                else:
                    nc.scalar.copy(out=out, in_=flipped[:].rearrange("p t h n -> p t n h"))

        def quantise(chunk):
            n_tok = RATIO * len(windows_of(chunk))
            if chunk == 0:
                codes, plane = codes_first, plane_first
            else:
                codes = code_pool.tile([P, CHUNK_TOKENS * P], U32, align_bytes=64)
                plane = code_pool.tile([P, CHUNK_TOKENS * P], U8, align_bytes=64)
            nc.vector.quantize_mx(
                out=codes[:, 0 : n_tok * P].bitcast(FP8X4),
                scales=plane[:, 0 : n_tok * P],
                in_=grouped_tiles[chunk][:, 0 : n_tok * P * 4],
            )
            code_tiles[chunk] = (codes, plane)

        def one_pass(out, which, source, cols):
            codes, plane = code_tiles[source]
            nc.tensor.matmul_mx(
                out=out,
                lhsT=w_words[:, which, :].bitcast(FP4X4),
                lhsT_scale=w_plane[:, which, :],
                rhs=codes[:, cols].bitcast(FP8X4),
                rhs_scale=plane[:, cols],
                start=True,
                stop=True,
            )

        def gate_product(chunk):
            width = width_of(chunk)
            gate_banks[chunk] = []
            for half in range(2):
                bank = psum_m.tile([P, 2 * WIDE], F32, name="bank")
                one_pass(bank[:, 0 : 2 * width], 0, chunk, slice(2 * half * width, 2 * (half + 1) * width))
                gate_banks[chunk].append(bank[:, 0 : 2 * width].rearrange("p (s n) -> p s n", s=2))

        def kv_product(chunk):
            kv_banks[chunk] = []
            for half in range(2):
                bank = psum_m.tile([P, 2 * WIDE], F32, name="bank")
                if chunk < N_CHUNKS - 1:
                    one_pass(bank[:], 1, chunk, slice(2 * half * WIDE, 2 * (half + 1) * WIDE))
                    view = bank[:].rearrange("p (s i n) -> p s i n", s=2, n=P)
                else:
                    for i, source in enumerate((chunk, 0)):
                        one_pass(bank[:, i * WIDE : (i + 1) * WIDE], 1, source, slice(half * WIDE, (half + 1) * WIDE))
                    view = bank[:].rearrange("p (i s n) -> p s i n", i=2, n=P)
                kv_banks[chunk].append(view)

        def early_gates(chunk):
            if chunk == 0:
                return gates_last[:, :, P:WIDE]
            if chunk == N_CHUNKS - 1:
                return gates_last[:, :, 0:P]
            return gate_tiles[chunk][:]

        def offset(chunk):
            if 0 < chunk < N_CHUNKS - 1:
                gate_tiles[chunk] = t_pool.tile([P, RATIO, WIDE], F32, name="gates")
            elif chunk == N_CHUNKS - 1:
                gate_tiles[chunk] = gates_last
            gates = early_gates(chunk)
            for r in range(RATIO):
                nc.scalar.activation(
                    out=gates[:, r, :], in_=gate_banks[chunk][r // 2][:, r % 2, :],
                    func=ACT.Identity, bias=ape_cols[:, r : r + 1], scale=1.0,
                )

        def top_first(chunk):
            width = width_of(chunk)
            gates = early_gates(chunk)
            half_top = m_pool.tile([P, 2, WIDE], BF16)
            nc.vector.tensor_tensor(out=half_top[:, :, 0:width], in0=gates[:, 0:2, :], in1=gates[:, 2:4, :], op=ALU.max)
            half_tops[chunk] = half_top

        def top_second(chunk):
            a, b = half_tops[chunk][:, 0, :], half_tops[chunk][:, 1, :]
            w = windows_of(chunk)
            if chunk == 1:
                nc.vector.tensor_tensor(out=top[:, 0, :], in0=a[:, 0:P], in1=b[:, 0:P], op=ALU.max)
                nc.vector.tensor_tensor(out=own_last[:], in0=a[:, P:WIDE], in1=b[:, P:WIDE], op=ALU.max)
                by_seq = "p (b q) -> p b q"
                nc.vector.tensor_copy(
                    out=left_last[:].rearrange(by_seq, b=BATCH)[:, :, 1:],
                    in_=own_last[:].rearrange(by_seq, b=BATCH)[:, :, 0 : RUNS_PER_SEQ - 1],
                )
                nc.vector.tensor_copy(out=right_first[:, 0 : P - 1], in_=top[:, 0, 1:P])
            else:
                width = width_of(chunk)
                nc.vector.tensor_tensor(
                    out=top_flat[:, w[0] * P : w[0] * P + width], in0=a[:, 0:width], in1=b[:, 0:width], op=ALU.max
                )

        def exchange(chunk):
            partner = p_pool.tile([P, WIDE], BF16)
            if chunk == 1:
                parts = [(0, P, top[:, 1, :], left_last[:]), (P, WIDE, right_first[:], top[:, LAST - 1, :])]
            elif chunk == N_CHUNKS - 1:
                parts = [(0, P, top[:, LAST - 1, :], top[:, LAST - 3, :]), (P, WIDE, own_last[:], top[:, LAST - 2, :])]
            else:
                first = unit_of(chunk)[0] * P
                parts = [(0, WIDE, top_flat[:, first + P : first + P + WIDE], top_flat[:, first - P : first - P + WIDE])]
            for n0, n1, after, before in parts:
                nc.sync.dma_start(out=partner[0:FEAT, n0:n1], in_=after[FEAT:COLS])
                nc.sync.dma_start(out=partner[FEAT:COLS, n0:n1], in_=before[0:FEAT])
            partner_tiles[chunk] = partner

        def peak_of(chunk):
            peak = m_pool.tile([P, WIDE], BF16)
            partner = partner_tiles[chunk]
            if chunk == 1:
                nc.vector.tensor_tensor(out=peak[:, 0:P], in0=partner[:, 0:P], in1=top[:, 0, :], op=ALU.max)
                nc.vector.tensor_tensor(out=peak[:, P:WIDE], in0=partner[:, P:WIDE], in1=own_last[:], op=ALU.max)
            else:
                first = unit_of(chunk)[0] * P
                nc.vector.tensor_tensor(out=peak[:], in0=partner[:], in1=top_flat[:, first : first + WIDE], op=ALU.max)
            peak_tiles[chunk] = peak

        def stabilise(chunk, engine, r0, r1):
            gates = gate_tiles[chunk]
            engine.tensor_tensor(
                out=gates[:, r0:r1], in0=gates[:, r0:r1],
                in1=peak_tiles[chunk][:].unsqueeze(1).to_broadcast([P, r1 - r0, WIDE]), op=ALU.subtract,
            )

        def exponent(chunk):
            gates = gate_tiles[chunk]
            nc.scalar.activation(out=gates[:], in_=gates[:], func=ACT.Exp)

        def weigh(chunk, half):
            if half == 0:
                product_tiles[chunk] = y_pool.tile([P, RATIO, WIDE], F32, name="products")
            rows = slice(2 * half, 2 * half + 2)
            by_window = "p s (i n) -> p s i n"
            nc.vector.tensor_tensor(
                out=product_tiles[chunk][:, rows, :].rearrange(by_window, n=P), in0=kv_banks[chunk][half],
                in1=gate_tiles[chunk][:, rows, :].rearrange(by_window, n=P), op=ALU.mult,
            )

        def slot_sums(chunk):
            acc = psum_t.tile([P, CHUNK_WINDOWS, 2, COLS], F32, tag="ring")

            def one_sum(out, kind, first):
                terms = (gate_tiles[chunk], product_tiles[chunk])[kind]
                for r in range(RATIO):
                    nc.tensor.matmul(
                        out=out, lhsT=terms[:, r, first : first + P], rhs=ident[:], is_transpose=True,
                        start=(r == 0), stop=(r == RATIO - 1),
                    )

            for i in range(CHUNK_WINDOWS):
                for kind in range(2):
                    one_sum(acc[:, i, kind, :], kind, i * P)
            sum_banks[chunk] = acc
            if chunk == 1:
                shifted = psum_m.tile([P, 2 * WIDE], F32, name="bank")
                for kind in range(2):
                    one_sum(shifted[:, kind * COLS : (kind + 1) * COLS], kind, P - 1)
                shifted_sums.append(shifted[:, 0 : 2 * COLS].rearrange("p (k c) -> p k c", k=2))

        def sums_out(chunk):
            acc = sum_banks[chunk]
            if chunk == 1:
                nc.scalar.activation(
                    out=first_half[:, 0], in_=shifted_sums[0][:, :, 0:FEAT], func=ACT.Copy, scale=inner[:, 0:1]
                )
                nc.scalar.copy(out=first_half[:, 1], in_=acc[:, 0, :, 0:FEAT])
                nc.scalar.copy(out=totals[:, LAST], in_=acc[:, 1, :, FEAT:COLS])
            elif chunk == N_CHUNKS - 1:
                nc.vector.tensor_copy(out=first_half[:, LAST - 1], in_=acc[:, 0, :, 0:FEAT])
            else:
                first = unit_of(chunk)[0]
                out, source = first_half[:, first + 1 : first + 3], acc[:, :, :, 0:FEAT]
                if chunk < N_CHUNKS - LATE_CHUNKS:
                    nc.scalar.copy(out=out, in_=source)
                else:
                    nc.vector.tensor_copy(out=out, in_=source)

        def fold(chunk):
            acc = sum_banks[chunk]
            first = unit_of(chunk)[0]
            count = 1 if chunk == 1 else 2
            nc.vector.tensor_tensor(
                out=totals[:, first : first + count], in0=acc[:, 0:count, :, FEAT:COLS],
                in1=first_half[:, first : first + count], op=ALU.add,
            )
            if chunk == N_CHUNKS - 1:
                nc.vector.tensor_tensor(out=totals[:, LAST], in0=acc[:, 1, :, 0:FEAT], in1=totals[:, LAST], op=ALU.add)

        def logarithm(w0, w1):
            nc.scalar.activation(out=inverse[:, w0:w1, :], in_=totals[:, w0:w1, 0, :], func=ACT.Ln)

        def invert(w0, n=BATCH_TARGETS):
            rows = inverse[:, w0 : w0 + n, :]
            nc.scalar.activation(out=rows, in_=rows, func=ACT.Exp, scale=-1.0)

        def invert_exactly(w0, w1):
            nc.vector.reciprocal(out=inverse[:, w0:w1, :], in_=totals[:, w0:w1, 0, :])

        def divide(w0):
            pooled = o_pool.tile([P, BATCH_TARGETS, FEAT], F32)
            nc.vector.tensor_tensor(
                out=pooled[:], in0=totals[:, w0 : w0 + BATCH_TARGETS, 1, :],
                in1=inverse[:, w0 : w0 + BATCH_TARGETS, :], op=ALU.mult,
            )
            nc.sync.dma_start(out=pooled_runs[:, w0 : w0 + BATCH_TARGETS, :], in_=pooled[:])
            batch_tiles[w0] = pooled

        def rotate(w0, step):
            w1 = w0 + BATCH_TARGETS
            plain = FEAT - ROPE
            by_row = "p w j e -> p w (j e)"
            if step == 0:
                pooled = batch_tiles[w0]
                k_rot = o_pool.tile([P, BATCH_TARGETS, FEAT], F32)
                swapped = o_pool.tile([P, BATCH_TARGETS, PAIRS, 2], F32)
                nc.scalar.copy(
                    out=swapped[:], in_=pooled[:, :, plain:FEAT].rearrange("p w (j e) -> p w j e", e=2)[:, :, :, ::-1]
                )
                nc.scalar.copy(out=k_rot[:, :, 0:plain], in_=pooled[:, :, 0:plain])
                nc.vector.tensor_tensor(
                    out=k_rot[:, :, plain:FEAT], in0=pooled[:, :, plain:FEAT],
                    in1=cos_pairs[:, w0:w1].rearrange(by_row), op=ALU.mult,
                )
                rot_tiles[w0] = (k_rot, swapped)
            k_rot, swapped = rot_tiles[w0]
            if step == 1:
                nc.vector.tensor_tensor(
                    out=swapped[:].rearrange(by_row), in0=swapped[:].rearrange(by_row),
                    in1=sin_pairs[:, w0:w1].rearrange(by_row), op=ALU.mult,
                )
            if step == 2:
                nc.vector.tensor_tensor(
                    out=k_rot[:, :, plain:FEAT], in0=k_rot[:, :, plain:FEAT], in1=swapped[:].rearrange(by_row), op=ALU.add
                )
                nc.sync.dma_start(out=krot_runs[:, w0:w1, :], in_=k_rot[:])

        def live(chunk):
            return 0 <= chunk < N_CHUNKS

        def unit(chunk):
            return 1 <= chunk < N_CHUNKS

        for a in range(0, N_CHUNKS + 10):
            if unit(a - 9):
                sums_out(a - 9)
            if unit(a - 6):
                stabilise(a - 6, nc.vector, 0, RATIO - 2)
            if a == 1:
                flip_offset()
            if live(a - 2):
                gate_product(a - 2)
                offset(a - 2)
            if live(a - 1):
                quantise(a - 1)
            if unit(a - 9):
                fold(a - 9)
            if a - 9 == N_CHUNKS - 2:
                logarithm(LAST_BATCH, LAST - 2)
            if unit(a - 4):
                exchange(a - 4)
            if live(a):
                flip(a)
            if a == 0:
                trigonometry()
            if a == TABLE_ROUND:
                exponent_table()
            if unit(a - 6):
                exponent(a - 6)
            if a - 6 == N_CHUNKS:
                logarithm(0, LAST_BATCH)
            if live(a - 2):
                top_first(a - 2)
            if unit(a - 5):
                peak_of(a - 5)
            if unit(a - 5):
                stabilise(a - 5, nc.gpsimd, RATIO - 2, RATIO)
            if unit(a - 7):
                kv_product(a - 7)
            if unit(a - 7):
                weigh(a - 7, 0)
                weigh(a - 7, 1)
            if live(a - 2):
                top_second(a - 2)
            if unit(a - 8):
                slot_sums(a - 8)
            if live(a + LOADS_AHEAD):
                load(a + LOADS_AHEAD)

        for w0 in range(0, LAST_BATCH, BATCH_TARGETS):
            invert(w0)
        invert(LAST_BATCH, LAST - 2 - LAST_BATCH)
        invert_exactly(LAST - 2, RUN_WINDOWS)
        for pair in ((0, BATCH_TARGETS), (2 * BATCH_TARGETS, LAST_BATCH)):
            for w0 in pair:
                divide(w0)
            for step in range(3):
                for w0 in pair:
                    rotate(w0, step)
